import numpy as np
import ml_dtypes


def mxq(x, axis, fmt="e4m3"):
    dtype, down = {"e4m3": (ml_dtypes.float8_e4m3fn, 7), "e5m2": (ml_dtypes.float8_e5m2, 14)}[fmt]
    v = np.moveaxis(np.asarray(x, np.float32).astype(ml_dtypes.bfloat16).astype(np.float64), axis, -1)
    blocks = v.reshape(v.shape[:-1] + (-1, 32))
    amax = np.abs(blocks).max(-1, keepdims=True)
    byte = np.maximum(np.where(amax > 0, np.frexp(amax)[1] - 1 + 127, 0) - down, 1)
    scale = np.exp2(byte - 127.0)
    codes = (blocks / scale).astype(np.float32).astype(dtype).astype(np.float64)
    return np.moveaxis((codes * scale).reshape(v.shape), -1, axis)


WIDE = False


def mx_kscale(k):
    if not WIDE:
        return np.ones(k)
    levels = np.array([10, -10, 5, -5, 0])
    if k % 512:
        return np.exp2(np.random.permutation(np.resize(levels, k // 32))).repeat(32)
    a = np.empty((k // 512, 16))
    for p in range(k // 512):
        a[p, :8] = np.random.permutation(np.resize(levels, 8))
        for g in range(8):
            far = levels[np.abs(levels - a[p, g]) >= 10]
            a[p, g + 8] = far[np.random.randint(len(far))]
    return np.exp2(a.ravel()).repeat(32)


BF16 = ml_dtypes.bfloat16


def bf(x):
    return np.asarray(x, np.float32).astype(BF16)


def f64(x):
    return np.asarray(x).astype(np.float64)


E2M1 = np.array([0.0, 0.5, 1.0, 1.5, 2.0, 3.0, 4.0, 6.0, -0.0, -0.5, -1.0, -1.5, -2.0, -3.0, -4.0, -6.0])


def pack_weight(w, fmt):
    k, n = w.shape
    w = f64(bf(w)).reshape(k // 32, 32, n)
    amax = np.abs(w).max(1)
    if fmt == "e4m3":
        byte = np.frexp(amax)[1] - 1 + 127 - 7
    else:
        mant, ex = np.frexp(amax / 6.0)
        byte = np.where(mant > 0.5, ex, ex - 1) + 127
    byte = np.clip(np.where(amax > 0, byte, 1), 1, 254)
    scaled = (w * np.exp2(127.0 - byte)[:, None, :]).reshape(k, n).astype(np.float32)
    by_word = np.ascontiguousarray(scaled.reshape(k // 512, 128, 4, n).transpose(0, 1, 3, 2))
    if fmt == "e4m3":
        words = by_word.astype(ml_dtypes.float8_e4m3fn).view(np.uint8)
    else:
        c = by_word.astype(ml_dtypes.float4_e2m1fn).view(np.uint8) & 0xF
        words = c[..., 0::2] | (c[..., 1::2] << 4)
    return np.ascontiguousarray(words), np.ascontiguousarray(byte.astype(np.uint8).reshape(k // 512, 16, n))


def unpack_weight(words, scales, fmt):
    g, p, n, _ = words.shape
    if fmt == "e4m3":
        vals = np.ascontiguousarray(words).view(ml_dtypes.float8_e4m3fn).astype(np.float64)
    else:
        nib = np.empty((g, p, n, 4), np.uint8)
        nib[..., 0::2] = words & 0xF
        nib[..., 1::2] = words >> 4
        vals = E2M1[nib]
    vals = vals * np.repeat(np.exp2(scales.astype(np.float64) - 127.0), 8, axis=1)[..., None]
    return vals.transpose(0, 1, 3, 2).reshape(g * 512, n)


B, C, T, P, N, D = 8, 16, 2048, 128, 8, 512
L = T // P
G = L // N


def draw0():
    s = mx_kscale(D)
    u = mx_kscale(P * N)
    un = u.reshape(P, N).T
    ut = np.tile(u, G)
    h_enc = bf(np.random.standard_normal((N, B, C, G, D)) * 0.7 * s)
    dec_W = bf(np.random.standard_normal((N, D, P)) / np.sqrt(D) / s[None, :, None] * un[:, None, :])
    dec_b = bf(np.random.standard_normal((N, P)) * 0.2 * un)
    map_W_words, map_W_scales = pack_weight(np.random.standard_normal((T, T)) / np.sqrt(T) / ut[:, None], 'e4m3')
    map_b = bf(np.random.standard_normal(T) * 0.2)
    return {'h_enc': h_enc,
            'dec_W': dec_W,
            'dec_b': dec_b,
            'map_W_words': map_W_words,
            'map_W_scales': map_W_scales,
            'map_b': map_b}


def core(h_enc, dec_W, dec_b, map_W_words, map_W_scales, map_b):
    h = f64(h_enc).reshape(N, B * C * G, D)
    r = (mxq(h, 2, 'e4m3') @ mxq(f64(dec_W), 1, 'e4m3')) + f64(dec_b)[:, None, :]
    r = r.reshape(N, B, C, G * P)
    x_rec = np.moveaxis(r, 0, -1).reshape(B * C, T)
    y_hat = (mxq(x_rec, 1, 'e4m3') @ unpack_weight(map_W_words, map_W_scales, 'e4m3')) + f64(map_b)
    return y_hat.reshape(B, C, T)


def e4m3fn_bytes(y):
    return np.clip(np.asarray(y, np.float64), -448.0, 448.0).astype(np.float32).astype(ml_dtypes.float8_e4m3fn).view(np.uint8)


def e4m3fn_values(b):
    return np.asarray(b, np.uint8).view(ml_dtypes.float8_e4m3fn).astype(np.float64)


def setup_inputs():
    d = draw0()
    x0 = np.asarray(d['h_enc']).astype(np.float64)
    s = (np.max(np.abs(x0), axis=(0, 1, 2, 3), keepdims=True) / 448.0).astype(np.float32)
    out = {}
    for k, v in d.items():
        if k == 'h_enc':
            out['h_enc_bytes'] = e4m3fn_bytes(x0 / s.astype(np.float64))
            out['h_enc_scale'] = s
        else:
            out[k] = v
    return out


def reference(h_enc_bytes, h_enc_scale, dec_W, dec_b, map_W_words, map_W_scales, map_b):
    return core(e4m3fn_values(h_enc_bytes) * h_enc_scale.astype(np.float64), dec_W, dec_b, map_W_words, map_W_scales, map_b)

@@ -1,0 +1,255 @@
+from contextlib import ExitStack
+
+import concourse.mybir as mybir
+from concourse.masks import make_identity
+
+F32 = mybir.dt.float32
+BF16 = mybir.dt.bfloat16
+I32 = mybir.dt.int32
+U32 = mybir.dt.uint32
+U8 = mybir.dt.uint8
+FP8 = mybir.dt.float8_e4m3fn
+FP8X4 = mybir.dt.float8_e4m3fn_x4
+MULT = mybir.AluOpType.mult
+ADD = mybir.AluOpType.add
+
+P = 128
+MODELS = 8
+D = 512
+T = 2048
+BC = 128
+PATCHES = 2
+GROUPS = T // 512
+HALF = 64
+
+FLOPS = 2 * MODELS * BC * PATCHES * D * P + 2 * BC * T * T
+
+
+ORDER = """
+    D.0 sct W.0 M.0.0 M.1.1 M.1.0 T.0.0 T.1.1 M.2.1 D.1 D.2 bt.0 M.3.0 M.0.1 M.3.1 T.1.0 D.3 T.2.1 T.3.0 M.4.0 
+    T.0.1 M.2.0 W.2 B.0 bt.1 E.1 T.3.1 M.4.1 K E.0 Q.0 T.2.0 W.1 E.3 Q.1 E.2 T.4.0 Q.2 bt.2 B.1 M.5.0 T.4.1 
+    C.0.1 Q.3 C.0.0 C.2.0 W.3 C.1.0 C.2.1 C.3.0 E.4 B.2 C.1.1 M.5.1 C.3.1 X.0 M.6.0 T.5.1 M.6.1 xT.0 T.5.0 
+    xE.0 T.6.0 T.6.1 X.1 E.5 xT.1 xQ.0 G.0.0 M.7.0 G.0.2 xE.1 G.0.1 M.7.1 T.7.0 E.6 Q.5 T.7.1 E.7.0 Q.6 G.0.3 
+    C.5.1 Q.4 E.7.1 C.6.0 C.5.0 Q.7 C.4.0 xQ.1 C.7.0 C.7.1 C.4.1 X.2 C.6.1 G.1.1 G.1.2 xT.2 xE.2 X.3 xT.3 
+    G.1.0 xQ.2 xE.3 xQ.3 G.1.3 G.2.0 G.2.2 G.3.0 F.0 G.2.1 G.3.2 F.2 G.3.1 G.2.3 F.1 G.3.3 F.3 
+"""
+
+
+def tile_model_pb_w8_kernel(tc, h_bytes, h_scale, dec_W, dec_b, map_W_words, map_W_scales, map_b, out):
+    nc = tc.nc
+
+    with ExitStack() as ctx:
+        keep = ctx.enter_context(tc.tile_pool(name="keep", bufs=1))
+        psum = ctx.enter_context(tc.psum_pool(name="psum", bufs=1))
+        ctx.enter_context(tc.manual_schedule())
+
+        def sb(shape, dtype, name):
+            return keep.tile(shape, dtype, name=name, align_bytes=64)
+
+        def bank(i, shape, name, dtype=F32):
+            return psum.tile(shape, dtype, name=name, tag="bank%d" % i)
+
+        scale_col = sb([P, 4], F32, "scale_col")
+        nc.sync.dma_start(out=scale_col[:], in_=h_scale.rearrange("a b c d (p j) -> p (a b c d j)", p=P))
+
+        h_view = h_bytes.rearrange("n b c l d -> (b c) l n d")
+        hb = {}
+        w_raw = {}
+
+        def load_h(u0, u1):
+            l, n0 = u0 // 4, 2 * (u0 % 4)
+            t = sb([P, 2 * (u1 - u0), D], U8, "hb%d" % u0)
+            nc.sync.dma_start(out=t[:], in_=h_view[:, l, n0 : n0 + 2 * (u1 - u0)])
+            for u in range(u0, u1):
+                hb[u] = t[:, 2 * (u - u0) : 2 * (u - u0) + 2]
+
+        def load_w(n0):
+            t = sb([P, 2, 4, P], BF16, "w_raw%d" % n0)
+            nc.sync.dma_start(out=t[:], in_=dec_W[n0 : n0 + 2].rearrange("n (p j) w -> p n j w", j=4))
+            w_raw[n0 // 2] = t
+
+        load_w(0)
+        load_h(0, 1)
+        load_w(2)
+        load_h(1, 2)
+        load_h(2, 4)
+        load_w(4)
+        load_w(6)
+
+        ident = sb([P, P], F32, "ident")
+        make_identity(nc, ident[:])
+        rows = sb([P, T + MODELS * P], BF16, "rows")
+        nc.gpsimd.memset(rows[:].bitcast(I32), 0)
+        wsc = sb([P, T], U8, "wsc")
+        nc.gpsimd.memset(wsc[:].bitcast(I32), 0)
+        ones = sb([P, P], BF16, "ones")
+        nc.gpsimd.memset(ones[:], 1.0)
+        nc.sync.dma_start(out=rows[0:1, 0 : MODELS * P], in_=dec_b.rearrange("(o n) p -> o (n p)", o=1))
+        nc.sync.dma_start(out=rows[0:1, MODELS * P :], in_=map_b.rearrange("(o s) -> o s", o=1))
+        load_h(4, 8)
+        for q in range(4):
+            nc.sync.dma_start(
+                out=wsc[32 * q : 32 * q + 16, :].bitcast(I32),
+                in_=map_W_scales[:, 4 * q : 4 * q + 4, :].bitcast(I32),
+            )
+        ww = []
+        for g in range(GROUPS):
+            t = sb([P, T], I32, "ww%d" % g)
+            nc.sync.dma_start(out=t[:], in_=map_W_words[g].rearrange("p n t -> p (n t)").bitcast(I32))
+            ww.append(t)
+        scale = sb([P, D], F32, "scale")
+        bias = sb([P, T + MODELS * P], BF16, "bias")
+        dec_bias = bias[:, 0 : MODELS * P].rearrange("b (n p) -> b n p", n=MODELS)
+        map_bias = bias[:, MODELS * P :]
+
+        hx, ht, hg, hc, hs = {}, {}, {}, {}, {}
+        wg, wc, ws = {}, {}, {}
+        x_ps, xb, xt, xg, xc, xs = {}, {}, {}, {}, {}, {}
+        acc = {}
+
+        bias_ps = {}
+
+        def spread_scale():
+            ps = bank(0, [P, D], "scale_ps")
+            for m in range(4):
+                nc.tensor.transpose(ps[:, m * P : (m + 1) * P], scale_col[:, m : m + 1].to_broadcast([P, P]), ident[:])
+            nc.scalar.copy(out=scale[:].rearrange("b (p j) -> b p j", j=4), in_=ps[:].rearrange("b (j p) -> b p j", j=4))
+
+        def spread_bias(b):
+            bias_ps[b] = bank((2, 3, 1)[b], [P, 1024], "bias_ps%d" % b, BF16)
+            for c in range(2):
+                nc.tensor.matmul(
+                    bias_ps[b][:, 512 * c : 512 * (c + 1)],
+                    ones[:],
+                    rows[:, 1024 * b + 512 * c : 1024 * b + 512 * (c + 1)],
+                    start=True,
+                    stop=True,
+                )
+
+        def keep_warm():
+            nc.tensor.matmul(bank(0, [P, 512], "warm")[:], ones[:], rows[:, 0:512], start=True, stop=True)
+
+        def bias_out(b):
+            nc.scalar.copy(out=bias[:, 1024 * b : 1024 * (b + 1)], in_=bias_ps[b][:])
+
+        def widen(u, i):
+            if u not in hx:
+                hx[u] = sb([P, 2, D], BF16, "hx%d" % u)
+            nc.vector.tensor_tensor(out=hx[u][:, i], in0=hb[u][:, i].bitcast(FP8), in1=scale[:], op=MULT)
+
+        def turn(u, i):
+            if u < 7:
+                if u not in ht:
+                    ht[u] = bank(4 + u if u < 4 else u % 2, [P, 2, 2, P], "ht%d" % u)
+                dst = ht[u][:, i]
+            else:
+                ht[u, i] = bank(1 - i, [P, 2, P], "ht%d_%d" % (u, i))
+                dst = ht[u, i][:]
+            words = hx[u][:, i].bitcast(F32)
+            for e in range(2):
+                nc.tensor.transpose(dst[:, e], words[:, e::2], ident[:])
+
+        def h_out(u, i=None):
+            if u not in hg:
+                hg[u] = sb([P, 2, P, 4], BF16, "hg%d" % u)
+            to = hg[u][:].rearrange("p i r k -> p (i r k)").bitcast(F32).rearrange("p (i r e) -> p i r e", i=2, e=2)
+            if i is None:
+                nc.scalar.copy(out=to, in_=ht[u][:].rearrange("p i e r -> p i r e"))
+            else:
+                nc.scalar.copy(out=to[:, i], in_=ht[u, i][:].rearrange("p e r -> p r e"))
+
+        def h_quant(u):
+            hc[u] = sb([P, 2 * P], U32, "hc%d" % u)
+            hs[u] = sb([P, 2 * P], U8, "hs%d" % u)
+            nc.vector.quantize_mx(out=hc[u][:].bitcast(FP8X4), scales=hs[u][:], in_=hg[u][:].rearrange("p i r k -> p (i r k)"))
+
+        def w_group(j):
+            wg[j] = sb([P, 2, P, 4], BF16, "wg%d" % j)
+            for n in range(2):
+                to = wg[j][:, n].rearrange("p (c i) t -> p c t i", i=4)
+                of = w_raw[j][:, n].rearrange("p t (c i) -> p c t i", i=4)
+                if j == 0:
+                    nc.vector.tensor_copy(out=to, in_=of)
+                else:
+                    nc.scalar.copy(out=to, in_=of)
+
+        def w_quant(j):
+            wc[j] = sb([P, 2 * P], U32, "wc%d" % j)
+            ws[j] = sb([P, 2 * P], U8, "ws%d" % j)
+            nc.vector.quantize_mx(out=wc[j][:].bitcast(FP8X4), scales=ws[j][:], in_=wg[j][:].rearrange("p i r k -> p (i r k)"))
+
+        def decode(u, half):
+            l, j = u // 4, u % 4
+            g = 2 * l + half
+            if g not in x_ps:
+                x_ps[g] = bank(2 + half, [P, MODELS, HALF], "x_ps%d" % g)
+            if True:
+                for i in range(2):
+                    cols = slice(i * P + half * HALF, i * P + half * HALF + HALF)
+                    nc.tensor.matmul_mx(
+                        out=x_ps[2 * l + half][:, 2 * j + i],
+                        lhsT=hc[u][:, i * P : (i + 1) * P].bitcast(FP8X4),
+                        lhsT_scale=hs[u][:, i * P : (i + 1) * P],
+                        rhs=wc[j][:, cols].bitcast(FP8X4),
+                        rhs_scale=ws[j][:, cols],
+                        start=True,
+                        stop=True,
+                    )
+
+        def x_bias(g):
+            half = g % 2
+            xb[g] = sb([P, 2, HALF, 2, 2], BF16, "xb%d" % g)
+            ps = x_ps[g][:].rearrange("b (q u e) p -> b u p q e", q=2, u=2)
+            bs = dec_bias[:, :, half * HALF : (half + 1) * HALF].rearrange("b (q u e) p -> b u p q e", q=2, u=2)
+            for u in range(2):
+                nc.vector.tensor_tensor(out=xb[g][:, u], in0=ps[:, u], in1=bs[:, u], op=ADD)
+
+        def x_turn(g):
+            xt[g] = bank(g % 2, [P, 2, P], "xt%d" % g)
+            for u in range(2):
+                nc.tensor.transpose(xt[g][:, u], xb[g][:, u].rearrange("b p q e -> b (p q e)").bitcast(F32), ident[:])
+
+        def x_out(g):
+            xg[g] = sb([P, P, 4], BF16, "xg%d" % g)
+            nc.scalar.copy(
+                out=xg[g][:].rearrange("p r k -> p (r k)").bitcast(F32).rearrange("p (r e) -> p r e", e=2),
+                in_=xt[g][:].rearrange("p e r -> p r e"),
+            )
+
+        def x_quant(g):
+            xc[g] = sb([P, P], U32, "xc%d" % g)
+            xs[g] = sb([P, P], U8, "xs%d" % g)
+            nc.vector.quantize_mx(out=xc[g][:].bitcast(FP8X4), scales=xs[g][:], in_=xg[g][:].rearrange("p r k -> p (r k)"))
+
+        def time_map(g, s):
+            if g == 0:
+                acc[s] = bank(4 + s, [P, 512], "acc%d" % s)
+            cols = slice(512 * s, 512 * (s + 1))
+            nc.tensor.matmul_mx(
+                out=acc[s][:],
+                lhsT=xc[g][:].bitcast(FP8X4),
+                lhsT_scale=xs[g][:],
+                rhs=ww[g][:, cols].bitcast(FP8X4),
+                rhs_scale=wsc[4 * g : P, cols],
+                start=(g == 0),
+                stop=(g == GROUPS - 1),
+            )
+
+        def finish(s):
+            y = sb([P, 512], F32, "y%d" % s)
+            parts = 2 if s == 3 else 1
+            width = 512 // parts
+            for k in range(parts):
+                here = slice(width * k, width * (k + 1))
+                cols = slice(512 * s + width * k, 512 * s + width * (k + 1))
+                nc.vector.tensor_tensor(out=y[:, here], in0=acc[s][:, here], in1=map_bias[:, cols], op=ADD)
+                nc.sync.dma_start(out=out.rearrange("b c s -> (b c) s")[:, cols], in_=y[:, here])
+
+        for step in ORDER.split():
+            a = [int(c) for c in step.split(".")[1:]]
+            STEPS = {
+                "sct": spread_scale, "bt": spread_bias, "B": bias_out, "D": w_group, "W": w_quant, "M": widen, "T": turn,
+                "E": h_out, "Q": h_quant, "C": decode, "X": x_bias, "xT": x_turn, "xE": x_out, "xQ": x_quant,
+                "K": keep_warm, "G": time_map, "F": finish,
+            }
+            STEPS[step.split(".")[0]](*a)

@@ -21,18 +21,9 @@ BC = 128
 PATCHES = 2
 GROUPS = T // 512
 HALF = 64
+FIRST_MODEL = (0, 4, 2, 6)
 
 FLOPS = 2 * MODELS * BC * PATCHES * D * P + 2 * BC * T * T
-
-
-ORDER = """
-    D.0 sct W.0 M.0.0 M.1.1 M.1.0 T.0.0 T.1.1 M.2.1 D.1 D.2 bt.0 M.3.0 M.0.1 M.3.1 T.1.0 D.3 T.2.1 T.3.0 M.4.0 
-    T.0.1 M.2.0 W.2 B.0 bt.1 E.1 T.3.1 M.4.1 K E.0 Q.0 T.2.0 W.1 E.3 Q.1 E.2 T.4.0 Q.2 bt.2 B.1 M.5.0 T.4.1 
-    C.0.1 Q.3 C.0.0 C.2.0 W.3 C.1.0 C.2.1 C.3.0 E.4 B.2 C.1.1 M.5.1 C.3.1 X.0 M.6.0 T.5.1 M.6.1 xT.0 T.5.0 
-    xE.0 T.6.0 T.6.1 X.1 E.5 xT.1 xQ.0 G.0.0 M.7.0 G.0.2 xE.1 G.0.1 M.7.1 T.7.0 E.6 Q.5 T.7.1 E.7.0 Q.6 G.0.3 
-    C.5.1 Q.4 E.7.1 C.6.0 C.5.0 Q.7 C.4.0 xQ.1 C.7.0 C.7.1 C.4.1 X.2 C.6.1 G.1.1 G.1.2 xT.2 xE.2 X.3 xT.3 
-    G.1.0 xQ.2 xE.3 xQ.3 G.1.3 G.2.0 G.2.2 G.3.0 F.0 G.2.1 G.3.2 F.2 G.3.1 G.2.3 F.1 G.3.3 F.3 
-"""
 
 
 def tile_model_pb_w8_kernel(tc, h_bytes, h_scale, dec_W, dec_b, map_W_words, map_W_scales, map_b, out):
@@ -52,178 +43,165 @@ def tile_model_pb_w8_kernel(tc, h_bytes, h_scale, dec_W, dec_b, map_W_words, map
         scale_col = sb([P, 4], F32, "scale_col")
         nc.sync.dma_start(out=scale_col[:], in_=h_scale.rearrange("a b c d (p j) -> p (a b c d j)", p=P))
 
-        h_view = h_bytes.rearrange("n b c l d -> (b c) l n d")
+        h_view = h_bytes.rearrange("n b c l d -> (b c) n l d")
         hb = {}
         w_raw = {}
 
-        def load_h(u0, u1):
-            l, n0 = u0 // 4, 2 * (u0 % 4)
-            t = sb([P, 2 * (u1 - u0), D], U8, "hb%d" % u0)
-            nc.sync.dma_start(out=t[:], in_=h_view[:, l, n0 : n0 + 2 * (u1 - u0)])
-            for u in range(u0, u1):
-                hb[u] = t[:, 2 * (u - u0) : 2 * (u - u0) + 2]
+        def load_h(k, patches):
+            n0 = FIRST_MODEL[k]
+            t = sb([P, 2, len(patches), D], U8, "hb%d_%d" % (k, patches[0]))
+            nc.sync.dma_start(out=t[:], in_=h_view[:, n0 : n0 + 2, patches[0] : patches[-1] + 1])
+            for a, l in enumerate(patches):
+                for e in range(2):
+                    hb[4 * l + k, e] = t[:, e, a].bitcast(FP8)
 
-        def load_w(n0):
-            t = sb([P, 2, 4, P], BF16, "w_raw%d" % n0)
-            nc.sync.dma_start(out=t[:], in_=dec_W[n0 : n0 + 2].rearrange("n (p j) w -> p n j w", j=4))
-            w_raw[n0 // 2] = t
+        def load_w(k):
+            n0 = FIRST_MODEL[k]
+            w_raw[k] = sb([P, 2, 4, P], BF16, "w_raw%d" % k)
+            nc.sync.dma_start(out=w_raw[k][:], in_=dec_W[n0 : n0 + 2].rearrange("n (p j) w -> p n j w", j=4))
 
         load_w(0)
-        load_h(0, 1)
+        load_h(0, [0])
+        load_w(1)
+        load_h(1, [0, 1])
         load_w(2)
-        load_h(1, 2)
-        load_h(2, 4)
-        load_w(4)
-        load_w(6)
+        load_h(2, [0, 1])
+        load_w(3)
 
         ident = sb([P, P], F32, "ident")
         make_identity(nc, ident[:])
-        rows = sb([P, T + MODELS * P], BF16, "rows")
-        nc.gpsimd.memset(rows[:].bitcast(I32), 0)
         wsc = sb([P, T], U8, "wsc")
         nc.gpsimd.memset(wsc[:].bitcast(I32), 0)
-        ones = sb([P, P], BF16, "ones")
-        nc.gpsimd.memset(ones[:], 1.0)
-        nc.sync.dma_start(out=rows[0:1, 0 : MODELS * P], in_=dec_b.rearrange("(o n) p -> o (n p)", o=1))
-        nc.sync.dma_start(out=rows[0:1, MODELS * P :], in_=map_b.rearrange("(o s) -> o s", o=1))
-        load_h(4, 8)
+
+        load_h(3, [0, 1])
+        load_h(0, [1])
         for q in range(4):
             nc.sync.dma_start(
                 out=wsc[32 * q : 32 * q + 16, :].bitcast(I32),
                 in_=map_W_scales[:, 4 * q : 4 * q + 4, :].bitcast(I32),
             )
+        dec_bias = sb([P, MODELS * P], BF16, "dec_bias")
+        nc.sync.dma_start(out=dec_bias[:], in_=dec_b.rearrange("n p -> (n p)").partition_broadcast(P))
         ww = []
         for g in range(GROUPS):
             t = sb([P, T], I32, "ww%d" % g)
             nc.sync.dma_start(out=t[:], in_=map_W_words[g].rearrange("p n t -> p (n t)").bitcast(I32))
             ww.append(t)
+        map_bias = sb([P, T], BF16, "map_bias")
+        nc.sync.dma_start(out=map_bias[:], in_=map_b.partition_broadcast(P))
+
         scale = sb([P, D], F32, "scale")
-        bias = sb([P, T + MODELS * P], BF16, "bias")
-        dec_bias = bias[:, 0 : MODELS * P].rearrange("b (n p) -> b n p", n=MODELS)
-        map_bias = bias[:, MODELS * P :]
+        dec_bias_by_u = dec_bias[:].rearrange("b (h u e p) -> b u p h e", h=2, u=2, e=2)
 
         hx, ht, hg, hc, hs = {}, {}, {}, {}, {}
         wg, wc, ws = {}, {}, {}
         x_ps, xb, xt, xg, xc, xs = {}, {}, {}, {}, {}, {}
         acc = {}
 
-        bias_ps = {}
-
         def spread_scale():
-            ps = bank(0, [P, D], "scale_ps")
+            ps = bank(2, [P, D], "scale_ps")
             for m in range(4):
                 nc.tensor.transpose(ps[:, m * P : (m + 1) * P], scale_col[:, m : m + 1].to_broadcast([P, P]), ident[:])
             nc.scalar.copy(out=scale[:].rearrange("b (p j) -> b p j", j=4), in_=ps[:].rearrange("b (j p) -> b p j", j=4))
 
-        def spread_bias(b):
-            bias_ps[b] = bank((2, 3, 1)[b], [P, 1024], "bias_ps%d" % b, BF16)
-            for c in range(2):
-                nc.tensor.matmul(
-                    bias_ps[b][:, 512 * c : 512 * (c + 1)],
-                    ones[:],
-                    rows[:, 1024 * b + 512 * c : 1024 * b + 512 * (c + 1)],
+        def widen_scaled(unit, e):
+            hx[unit, e] = sb([P, D], BF16, "hx%d_%d" % (unit, e))
+            nc.vector.tensor_tensor(out=hx[unit, e][:], in0=hb[unit, e], in1=scale[:], op=MULT)
+
+        def widen_plain(unit, e):
+            hx[unit, e] = sb([P, D], BF16, "hx%d_%d" % (unit, e))
+            nc.scalar.copy(out=hx[unit, e][:], in_=hb[unit, e])
+
+        def turn(unit):
+            ht[unit] = bank(unit % 2 if unit < 6 else unit, [P, 2, 2, P], "ht%d" % unit)
+            for e in range(2):
+                words = hx[unit, e][:].bitcast(F32)
+                for v in range(2):
+                    nc.tensor.transpose(ht[unit][:, e, v], words[:, v::2], ident[:])
+
+        def grouped(first, count):
+            t = sb([P, count * P * 4], BF16, "hg%d" % first)
+            for m in range(count):
+                hg[first + m] = t[:, m * 4 * P : (m + 1) * 4 * P]
+            hg[first, count] = t
+
+        def h_out(unit):
+            whole = hg[4 * (unit // 2), 4]
+            to = whole[:, (unit % 2) * 1024 : (unit % 2 + 1) * 1024].bitcast(F32).rearrange("p (e r v) -> p e r v", e=2, v=2)
+            nc.scalar.copy(out=to, in_=ht[unit][:].rearrange("p e v r -> p e r v"))
+
+        def h_out_scaled(unit, e):
+            to = hg[2 * unit + e].rearrange("p (r v z) -> p r v z", v=2, z=2)
+            of = ht[unit][:, e].rearrange("p v r -> p (v r)").bitcast(BF16).rearrange("p (v r z) -> p r v z", v=2, z=2)
+            by = scale_col[:].rearrange("p (o v z) -> p o v z", o=1, v=2).to_broadcast([P, P, 2, 2])
+            nc.vector.tensor_tensor(out=to, in0=of, in1=by, op=MULT)
+
+        def h_quant(first, count):
+            codes = sb([P, count * P], U32, "hc%d" % first)
+            scales = sb([P, count * P], U8, "hs%d" % first)
+            nc.vector.quantize_mx(out=codes[:].bitcast(FP8X4), scales=scales[:], in_=hg[first, count][:])
+            for m in range(count):
+                hc[first + m] = codes[:, m * P : (m + 1) * P]
+                hs[first + m] = scales[:, m * P : (m + 1) * P]
+
+        def w_group(k, e):
+            if e == 0:
+                wg[k] = sb([P, 2, P, 4], BF16, "wg%d" % k)
+            to = wg[k][:, e].rearrange("p (c i) t -> p c t i", i=4)
+            of = w_raw[k][:, e].rearrange("p t (c i) -> p c t i", i=4)
+            if k == 0:
+                nc.vector.tensor_copy(out=to, in_=of)
+            else:
+                nc.scalar.copy(out=to, in_=of)
+
+        def w_quant(k):
+            wc[k] = sb([P, 2 * P], U32, "wc%d" % k)
+            ws[k] = sb([P, 2 * P], U8, "ws%d" % k)
+            nc.vector.quantize_mx(out=wc[k][:].bitcast(FP8X4), scales=ws[k][:], in_=wg[k][:].rearrange("p i r k -> p (i r k)"))
+
+        def decode(unit):
+            l, k = divmod(unit, 4)
+            u, h = divmod(k, 2)
+            if h == 0:
+                x_ps[l, u] = bank(2 + u, [P, 2, 2, P], "x_ps%d_%d" % (l, u))
+            for e in range(2):
+                cols = slice(e * P, (e + 1) * P)
+                nc.tensor.matmul_mx(
+                    out=x_ps[l, u][:, h, e],
+                    lhsT=hc[2 * unit + e].bitcast(FP8X4),
+                    lhsT_scale=hs[2 * unit + e],
+                    rhs=wc[k][:, cols].bitcast(FP8X4),
+                    rhs_scale=ws[k][:, cols],
                     start=True,
                     stop=True,
                 )
 
-        def keep_warm():
-            nc.tensor.matmul(bank(0, [P, 512], "warm")[:], ones[:], rows[:, 0:512], start=True, stop=True)
+        def x_bias(l, u, halves):
+            t = sb([P, len(halves) * HALF, 2, 2], BF16, "xb%d_%d_%d" % (l, u, halves[0]))
+            samples = slice(halves[0] * HALF, (halves[-1] + 1) * HALF)
+            nc.vector.tensor_tensor(
+                out=t[:], in0=x_ps[l, u][:, :, :, samples].rearrange("b h e p -> b p h e"), in1=dec_bias_by_u[:, u, samples], op=ADD
+            )
+            for a, half in enumerate(halves):
+                xb[2 * l + half, u] = t[:, a * HALF : (a + 1) * HALF].rearrange("b p h e -> b (p h e)").bitcast(F32)
 
-        def bias_out(b):
-            nc.scalar.copy(out=bias[:, 1024 * b : 1024 * (b + 1)], in_=bias_ps[b][:])
-
-        def widen(u, i):
-            if u not in hx:
-                hx[u] = sb([P, 2, D], BF16, "hx%d" % u)
-            nc.vector.tensor_tensor(out=hx[u][:, i], in0=hb[u][:, i].bitcast(FP8), in1=scale[:], op=MULT)
-
-        def turn(u, i):
-            if u < 7:
-                if u not in ht:
-                    ht[u] = bank(4 + u if u < 4 else u % 2, [P, 2, 2, P], "ht%d" % u)
-                dst = ht[u][:, i]
-            else:
-                ht[u, i] = bank(1 - i, [P, 2, P], "ht%d_%d" % (u, i))
-                dst = ht[u, i][:]
-            words = hx[u][:, i].bitcast(F32)
-            for e in range(2):
-                nc.tensor.transpose(dst[:, e], words[:, e::2], ident[:])
-
-        def h_out(u, i=None):
-            if u not in hg:
-                hg[u] = sb([P, 2, P, 4], BF16, "hg%d" % u)
-            to = hg[u][:].rearrange("p i r k -> p (i r k)").bitcast(F32).rearrange("p (i r e) -> p i r e", i=2, e=2)
-            if i is None:
-                nc.scalar.copy(out=to, in_=ht[u][:].rearrange("p i e r -> p i r e"))
-            else:
-                nc.scalar.copy(out=to[:, i], in_=ht[u, i][:].rearrange("p e r -> p r e"))
-
-        def h_quant(u):
-            hc[u] = sb([P, 2 * P], U32, "hc%d" % u)
-            hs[u] = sb([P, 2 * P], U8, "hs%d" % u)
-            nc.vector.quantize_mx(out=hc[u][:].bitcast(FP8X4), scales=hs[u][:], in_=hg[u][:].rearrange("p i r k -> p (i r k)"))
-
-        def w_group(j):
-            wg[j] = sb([P, 2, P, 4], BF16, "wg%d" % j)
-            for n in range(2):
-                to = wg[j][:, n].rearrange("p (c i) t -> p c t i", i=4)
-                of = w_raw[j][:, n].rearrange("p t (c i) -> p c t i", i=4)
-                if j == 0:
-                    nc.vector.tensor_copy(out=to, in_=of)
-                else:
-                    nc.scalar.copy(out=to, in_=of)
-
-        def w_quant(j):
-            wc[j] = sb([P, 2 * P], U32, "wc%d" % j)
-            ws[j] = sb([P, 2 * P], U8, "ws%d" % j)
-            nc.vector.quantize_mx(out=wc[j][:].bitcast(FP8X4), scales=ws[j][:], in_=wg[j][:].rearrange("p i r k -> p (i r k)"))
-
-        def decode(u, half):
-            l, j = u // 4, u % 4
-            g = 2 * l + half
-            if g not in x_ps:
-                x_ps[g] = bank(2 + half, [P, MODELS, HALF], "x_ps%d" % g)
-            if True:
-                for i in range(2):
-                    cols = slice(i * P + half * HALF, i * P + half * HALF + HALF)
-                    nc.tensor.matmul_mx(
-                        out=x_ps[2 * l + half][:, 2 * j + i],
-                        lhsT=hc[u][:, i * P : (i + 1) * P].bitcast(FP8X4),
-                        lhsT_scale=hs[u][:, i * P : (i + 1) * P],
-                        rhs=wc[j][:, cols].bitcast(FP8X4),
-                        rhs_scale=ws[j][:, cols],
-                        start=True,
-                        stop=True,
-                    )
-
-        def x_bias(g):
-            half = g % 2
-            xb[g] = sb([P, 2, HALF, 2, 2], BF16, "xb%d" % g)
-            ps = x_ps[g][:].rearrange("b (q u e) p -> b u p q e", q=2, u=2)
-            bs = dec_bias[:, :, half * HALF : (half + 1) * HALF].rearrange("b (q u e) p -> b u p q e", q=2, u=2)
-            for u in range(2):
-                nc.vector.tensor_tensor(out=xb[g][:, u], in0=ps[:, u], in1=bs[:, u], op=ADD)
-
-        def x_turn(g):
-            xt[g] = bank(g % 2, [P, 2, P], "xt%d" % g)
-            for u in range(2):
-                nc.tensor.transpose(xt[g][:, u], xb[g][:, u].rearrange("b p q e -> b (p q e)").bitcast(F32), ident[:])
+        def x_turn(g, u):
+            if u == 0:
+                xt[g] = bank(4 + g, [P, 2, P], "xt%d" % g)
+            nc.tensor.transpose(xt[g][:, u], xb[g, u], ident[:])
 
         def x_out(g):
-            xg[g] = sb([P, P, 4], BF16, "xg%d" % g)
-            nc.scalar.copy(
-                out=xg[g][:].rearrange("p r k -> p (r k)").bitcast(F32).rearrange("p (r e) -> p r e", e=2),
-                in_=xt[g][:].rearrange("p e r -> p r e"),
-            )
+            xg[g] = sb([P, P * 4], BF16, "xg%d" % g)
+            nc.scalar.copy(out=xg[g][:].bitcast(F32).rearrange("p (r u) -> p r u", u=2), in_=xt[g][:].rearrange("p u r -> p r u"))
 
         def x_quant(g):
             xc[g] = sb([P, P], U32, "xc%d" % g)
             xs[g] = sb([P, P], U8, "xs%d" % g)
-            nc.vector.quantize_mx(out=xc[g][:].bitcast(FP8X4), scales=xs[g][:], in_=xg[g][:].rearrange("p r k -> p (r k)"))
+            nc.vector.quantize_mx(out=xc[g][:].bitcast(FP8X4), scales=xs[g][:], in_=xg[g][:])
 
         def time_map(g, s):
             if g == 0:
-                acc[s] = bank(4 + s, [P, 512], "acc%d" % s)
+                acc[s] = bank((4, 5, 0, 1)[s], [P, 512], "acc%d" % s)
             cols = slice(512 * s, 512 * (s + 1))
             nc.tensor.matmul_mx(
                 out=acc[s][:],
@@ -235,9 +213,8 @@ def tile_model_pb_w8_kernel(tc, h_bytes, h_scale, dec_W, dec_b, map_W_words, map
                 stop=(g == GROUPS - 1),
             )
 
-        def finish(s):
+        def finish(s, parts):
             y = sb([P, 512], F32, "y%d" % s)
-            parts = 2 if s == 3 else 1
             width = 512 // parts
             for k in range(parts):
                 here = slice(width * k, width * (k + 1))
@@ -245,11 +222,111 @@ def tile_model_pb_w8_kernel(tc, h_bytes, h_scale, dec_W, dec_b, map_W_words, map
                 nc.vector.tensor_tensor(out=y[:, here], in0=acc[s][:, here], in1=map_bias[:, cols], op=ADD)
                 nc.sync.dma_start(out=out.rearrange("b c s -> (b c) s")[:, cols], in_=y[:, here])
 
-        for step in ORDER.split():
-            a = [int(c) for c in step.split(".")[1:]]
-            STEPS = {
-                "sct": spread_scale, "bt": spread_bias, "B": bias_out, "D": w_group, "W": w_quant, "M": widen, "T": turn,
-                "E": h_out, "Q": h_quant, "C": decode, "X": x_bias, "xT": x_turn, "xE": x_out, "xQ": x_quant,
-                "K": keep_warm, "G": time_map, "F": finish,
-            }
-            STEPS[step.split(".")[0]](*a)
+        for first in (0, 4, 8):
+            grouped(first, 4)
+        grouped(12, 2)
+        grouped(14, 1)
+        grouped(15, 1)
+
+        spread_scale()
+        w_group(0, 0)
+        w_group(0, 1)
+        w_quant(0)
+        w_group(1, 0)
+        w_group(1, 1)
+        widen_scaled(0, 0)
+        widen_scaled(0, 1)
+        turn(0)
+        w_group(2, 0)
+        w_group(2, 1)
+        h_out(0)
+        widen_scaled(1, 0)
+        widen_scaled(1, 1)
+        turn(1)
+        w_group(3, 0)
+        h_out(1)
+        w_quant(1)
+        widen_scaled(2, 0)
+        widen_scaled(2, 1)
+        turn(2)
+        w_group(3, 1)
+        h_out(2)
+        w_quant(2)
+        widen_scaled(3, 0)
+        h_quant(0, 4)
+        widen_scaled(3, 1)
+        decode(0)
+        decode(1)
+        turn(3)
+        widen_plain(6, 0)
+        h_out(3)
+        widen_plain(6, 1)
+        w_quant(3)
+        widen_scaled(4, 0)
+        widen_scaled(4, 1)
+        turn(4)
+        h_out(4)
+        h_quant(4, 4)
+        decode(2)
+        decode(3)
+        x_bias(0, 0, [0, 1])
+        turn(6)
+        x_turn(0, 0)
+        x_turn(1, 0)
+        widen_plain(7, 0)
+        widen_plain(7, 1)
+        widen_scaled(5, 0)
+        x_bias(0, 1, [0, 1])
+        widen_scaled(5, 1)
+        x_turn(0, 1)
+        x_turn(1, 1)
+        turn(5)
+        x_out(0)
+        x_out(1)
+        h_out(5)
+        turn(7)
+        h_out_scaled(6, 0)
+        x_quant(0)
+        x_quant(1)
+        h_out_scaled(6, 1)
+        h_quant(8, 4)
+        time_map(0, 0)
+        time_map(0, 1)
+        time_map(0, 2)
+        decode(4)
+        decode(5)
+        time_map(0, 3)
+        time_map(1, 0)
+        h_out_scaled(7, 0)
+        h_quant(12, 2)
+        decode(6)
+        time_map(1, 1)
+        time_map(1, 2)
+        h_out_scaled(7, 1)
+        h_quant(14, 1)
+        h_quant(15, 1)
+        decode(7)
+        x_bias(1, 0, [0, 1])
+        x_turn(2, 0)
+        x_turn(3, 0)
+        x_bias(1, 1, [0])
+        x_bias(1, 1, [1])
+        x_turn(2, 1)
+        x_turn(3, 1)
+        time_map(1, 3)
+        x_out(2)
+        x_out(3)
+        x_quant(2)
+        x_quant(3)
+        time_map(2, 0)
+        time_map(3, 0)
+        time_map(2, 1)
+        time_map(3, 1)
+        finish(0, 1)
+        finish(1, 1)
+        time_map(2, 2)
+        time_map(3, 2)
+        finish(2, 1)
+        time_map(2, 3)
+        time_map(3, 3)
+        finish(3, 2)

@@ -60,49 +60,68 @@ def tile_model_pb_w8_kernel(tc, h_bytes, h_scale, dec_W, dec_b, map_W_words, map
             w_raw[k] = sb([P, 2, 4, P], BF16, "w_raw%d" % k)
             nc.sync.dma_start(out=w_raw[k][:], in_=dec_W[n0 : n0 + 2].rearrange("n (p j) w -> p n j w", j=4))
 
-        load_w(0)
-        load_h(0, [0])
-        load_w(1)
-        load_h(1, [0, 1])
-        load_w(2)
-        load_h(2, [0, 1])
-        load_w(3)
-
         ident = sb([P, P], F32, "ident")
         make_identity(nc, ident[:])
+        rows = sb([P, T + MODELS * P], BF16, "rows")
+        nc.vector.memset(rows[:].bitcast(I32), 0)
         wsc = sb([P, T], U8, "wsc")
-        nc.gpsimd.memset(wsc[:].bitcast(I32), 0)
+        nc.vector.memset(wsc[:].bitcast(I32), 0)
+        ones = sb([P, P], BF16, "ones")
+        nc.gpsimd.memset(ones[:], 1.0)
 
-        load_h(3, [0, 1])
+        load_w(0)
+        load_h(0, [0])
+        nc.sync.dma_start(out=rows[0:1, 0 : MODELS * P], in_=dec_b.rearrange("(o n) p -> o (n p)", o=1))
+        nc.sync.dma_start(out=rows[0:1, MODELS * P :], in_=map_b.rearrange("(o s) -> o s", o=1))
+        load_w(1)
+        load_h(1, [0, 1])
+        for k in (2, 3):
+            load_w(k)
+            load_h(k, [0, 1])
         load_h(0, [1])
         for q in range(4):
             nc.sync.dma_start(
                 out=wsc[32 * q : 32 * q + 16, :].bitcast(I32),
                 in_=map_W_scales[:, 4 * q : 4 * q + 4, :].bitcast(I32),
             )
-        dec_bias = sb([P, MODELS * P], BF16, "dec_bias")
-        nc.sync.dma_start(out=dec_bias[:], in_=dec_b.rearrange("n p -> (n p)").partition_broadcast(P))
         ww = []
         for g in range(GROUPS):
             t = sb([P, T], I32, "ww%d" % g)
             nc.sync.dma_start(out=t[:], in_=map_W_words[g].rearrange("p n t -> p (n t)").bitcast(I32))
             ww.append(t)
-        map_bias = sb([P, T], BF16, "map_bias")
-        nc.sync.dma_start(out=map_bias[:], in_=map_b.partition_broadcast(P))
 
         scale = sb([P, D], F32, "scale")
-        dec_bias_by_u = dec_bias[:].rearrange("b (h u e p) -> b u p h e", h=2, u=2, e=2)
+        dec_bias = sb([P, 2, P, 2, 2], BF16, "dec_bias")
+        map_bias = sb([P, T], BF16, "map_bias")
 
         hx, ht, hg, hc, hs = {}, {}, {}, {}, {}
         wg, wc, ws = {}, {}, {}
         x_ps, xb, xt, xg, xc, xs = {}, {}, {}, {}, {}, {}
-        acc = {}
+        acc, bias_ps = {}, {}
 
         def spread_scale():
             ps = bank(2, [P, D], "scale_ps")
             for m in range(4):
                 nc.tensor.transpose(ps[:, m * P : (m + 1) * P], scale_col[:, m : m + 1].to_broadcast([P, P]), ident[:])
             nc.scalar.copy(out=scale[:].rearrange("b (p j) -> b p j", j=4), in_=ps[:].rearrange("b (j p) -> b p j", j=4))
+
+        def spread_dec_bias():
+            bias_ps["dec"] = bank(3, [P, 2, 512], "dec_bias_ps", BF16)
+            by_u = rows[:, 0 : MODELS * P].rearrange("k (h u e p) -> k u p h e", h=2, u=2, e=2)
+            for u in range(2):
+                nc.tensor.matmul(bias_ps["dec"][:, u], ones[:], by_u[:, u], start=True, stop=True)
+
+        def dec_bias_out():
+            nc.scalar.copy(out=dec_bias[:].rearrange("b u p h e -> b (u p h e)"), in_=bias_ps["dec"][:].rearrange("b u c -> b (u c)"))
+
+        def spread_map_bias(b):
+            bias_ps[b] = bank((5, 7)[b], [P, 1024], "map_bias_ps%d" % b, BF16)
+            for c in range(2):
+                first = MODELS * P + 1024 * b + 512 * c
+                nc.tensor.matmul(bias_ps[b][:, 512 * c : 512 * (c + 1)], ones[:], rows[:, first : first + 512], start=True, stop=True)
+
+        def map_bias_out(b):
+            nc.scalar.copy(out=map_bias[:, 1024 * b : 1024 * (b + 1)], in_=bias_ps[b][:])
 
         def widen_scaled(unit, e):
             hx[unit, e] = sb([P, D], BF16, "hx%d_%d" % (unit, e))
@@ -113,7 +132,7 @@ def tile_model_pb_w8_kernel(tc, h_bytes, h_scale, dec_W, dec_b, map_W_words, map
             nc.scalar.copy(out=hx[unit, e][:], in_=hb[unit, e])
 
         def turn(unit):
-            ht[unit] = bank(unit % 2 if unit < 6 else unit, [P, 2, 2, P], "ht%d" % unit)
+            ht[unit] = bank((0, 1, 0, 1, 0, 1, 6, 7)[unit], [P, 2, 2, P], "ht%d" % unit)
             for e in range(2):
                 words = hx[unit, e][:].bitcast(F32)
                 for v in range(2):
@@ -123,11 +142,12 @@ def tile_model_pb_w8_kernel(tc, h_bytes, h_scale, dec_W, dec_b, map_W_words, map
             t = sb([P, count * P * 4], BF16, "hg%d" % first)
             for m in range(count):
                 hg[first + m] = t[:, m * 4 * P : (m + 1) * 4 * P]
+            for m in range(0, count - 1, 2):
+                hg["unit", (first + m) // 2] = t[:, m * 4 * P : (m + 2) * 4 * P]
             hg[first, count] = t
 
         def h_out(unit):
-            whole = hg[4 * (unit // 2), 4]
-            to = whole[:, (unit % 2) * 1024 : (unit % 2 + 1) * 1024].bitcast(F32).rearrange("p (e r v) -> p e r v", e=2, v=2)
+            to = hg["unit", unit].bitcast(F32).rearrange("p (e r v) -> p e r v", e=2, v=2)
             nc.scalar.copy(out=to, in_=ht[unit][:].rearrange("p e v r -> p e r v"))
 
         def h_out_scaled(unit, e):
@@ -180,33 +200,38 @@ def tile_model_pb_w8_kernel(tc, h_bytes, h_scale, dec_W, dec_b, map_W_words, map
             t = sb([P, len(halves) * HALF, 2, 2], BF16, "xb%d_%d_%d" % (l, u, halves[0]))
             samples = slice(halves[0] * HALF, (halves[-1] + 1) * HALF)
             nc.vector.tensor_tensor(
-                out=t[:], in0=x_ps[l, u][:, :, :, samples].rearrange("b h e p -> b p h e"), in1=dec_bias_by_u[:, u, samples], op=ADD
+                out=t[:], in0=x_ps[l, u][:, :, :, samples].rearrange("b h e p -> b p h e"), in1=dec_bias[:, u, samples], op=ADD
             )
             for a, half in enumerate(halves):
                 xb[2 * l + half, u] = t[:, a * HALF : (a + 1) * HALF].rearrange("b p h e -> b (p h e)").bitcast(F32)
 
-        def x_turn(g, u):
+        def x_turn(groups, u):
             if u == 0:
-                xt[g] = bank(4 + g, [P, 2, P], "xt%d" % g)
-            nc.tensor.transpose(xt[g][:, u], xb[g, u], ident[:])
+                xt[groups] = bank(4 if groups[0] == 0 else 4 + groups[0], [P, len(groups), 2, P], "xt%d" % groups[0])
+            for a, g in enumerate(groups):
+                nc.tensor.transpose(xt[groups][:, a, u], xb[g, u], ident[:])
 
-        def x_out(g):
-            xg[g] = sb([P, P * 4], BF16, "xg%d" % g)
-            nc.scalar.copy(out=xg[g][:].bitcast(F32).rearrange("p (r u) -> p r u", u=2), in_=xt[g][:].rearrange("p u r -> p r u"))
+        def x_out(groups):
+            xg[groups] = sb([P, len(groups) * P * 4], BF16, "xg%d" % groups[0])
+            to = xg[groups][:].bitcast(F32).rearrange("p (a r u) -> p a r u", a=len(groups), u=2)
+            nc.scalar.copy(out=to, in_=xt[groups][:].rearrange("p a u r -> p a r u"))
 
-        def x_quant(g):
-            xc[g] = sb([P, P], U32, "xc%d" % g)
-            xs[g] = sb([P, P], U8, "xs%d" % g)
-            nc.vector.quantize_mx(out=xc[g][:].bitcast(FP8X4), scales=xs[g][:], in_=xg[g][:])
+        def x_quant(groups):
+            codes = sb([P, len(groups) * P], U32, "xc%d" % groups[0])
+            scales = sb([P, len(groups) * P], U8, "xs%d" % groups[0])
+            nc.vector.quantize_mx(out=codes[:].bitcast(FP8X4), scales=scales[:], in_=xg[groups][:])
+            for a, g in enumerate(groups):
+                xc[g] = codes[:, a * P : (a + 1) * P]
+                xs[g] = scales[:, a * P : (a + 1) * P]
 
         def time_map(g, s):
             if g == 0:
-                acc[s] = bank((4, 5, 0, 1)[s], [P, 512], "acc%d" % s)
+                acc[s] = bank((5, 0, 4, 1)[s], [P, 512], "acc%d" % s)
             cols = slice(512 * s, 512 * (s + 1))
             nc.tensor.matmul_mx(
                 out=acc[s][:],
-                lhsT=xc[g][:].bitcast(FP8X4),
-                lhsT_scale=xs[g][:],
+                lhsT=xc[g].bitcast(FP8X4),
+                lhsT_scale=xs[g],
                 rhs=ww[g][:, cols].bitcast(FP8X4),
                 rhs_scale=wsc[4 * g : P, cols],
                 start=(g == 0),
@@ -222,11 +247,8 @@ def tile_model_pb_w8_kernel(tc, h_bytes, h_scale, dec_W, dec_b, map_W_words, map
                 nc.vector.tensor_tensor(out=y[:, here], in0=acc[s][:, here], in1=map_bias[:, cols], op=ADD)
                 nc.sync.dma_start(out=out.rearrange("b c s -> (b c) s")[:, cols], in_=y[:, here])
 
-        for first in (0, 4, 8):
-            grouped(first, 4)
-        grouped(12, 2)
-        grouped(14, 1)
-        grouped(15, 1)
+        for first, count in ((0, 4), (4, 2), (6, 2), (8, 4), (12, 2), (14, 1), (15, 1)):
+            grouped(first, count)
 
         spread_scale()
         w_group(0, 0)
@@ -234,16 +256,19 @@ def tile_model_pb_w8_kernel(tc, h_bytes, h_scale, dec_W, dec_b, map_W_words, map
         w_quant(0)
         w_group(1, 0)
         w_group(1, 1)
+        spread_dec_bias()
+        spread_map_bias(0)
+        spread_map_bias(1)
         widen_scaled(0, 0)
         widen_scaled(0, 1)
         turn(0)
         w_group(2, 0)
         w_group(2, 1)
+        w_group(3, 0)
         h_out(0)
         widen_scaled(1, 0)
         widen_scaled(1, 1)
         turn(1)
-        w_group(3, 0)
         h_out(1)
         w_quant(1)
         widen_scaled(2, 0)
@@ -251,6 +276,7 @@ def tile_model_pb_w8_kernel(tc, h_bytes, h_scale, dec_W, dec_b, map_W_words, map
         turn(2)
         w_group(3, 1)
         h_out(2)
+        dec_bias_out()
         w_quant(2)
         widen_scaled(3, 0)
         h_quant(0, 4)
@@ -258,66 +284,64 @@ def tile_model_pb_w8_kernel(tc, h_bytes, h_scale, dec_W, dec_b, map_W_words, map
         decode(0)
         decode(1)
         turn(3)
-        widen_plain(6, 0)
         h_out(3)
-        widen_plain(6, 1)
+        map_bias_out(1)
         w_quant(3)
+        x_bias(0, 0, [0, 1])
+        h_quant(4, 2)
         widen_scaled(4, 0)
-        widen_scaled(4, 1)
-        turn(4)
-        h_out(4)
-        h_quant(4, 4)
+        h_quant(6, 2)
         decode(2)
         decode(3)
-        x_bias(0, 0, [0, 1])
-        turn(6)
-        x_turn(0, 0)
-        x_turn(1, 0)
+        widen_scaled(4, 1)
+        turn(4)
         widen_plain(7, 0)
+        h_out(4)
+        x_bias(0, 1, [0, 1])
+        x_turn((0, 1), 0)
+        x_turn((0, 1), 1)
+        x_out((0, 1))
         widen_plain(7, 1)
         widen_scaled(5, 0)
-        x_bias(0, 1, [0, 1])
         widen_scaled(5, 1)
-        x_turn(0, 1)
-        x_turn(1, 1)
         turn(5)
-        x_out(0)
-        x_out(1)
         h_out(5)
+        map_bias_out(0)
         turn(7)
-        h_out_scaled(6, 0)
-        x_quant(0)
-        x_quant(1)
-        h_out_scaled(6, 1)
-        h_quant(8, 4)
+        widen_scaled(6, 0)
+        x_quant((0, 1))
+        widen_scaled(6, 1)
+        turn(6)
+        h_out(6)
         time_map(0, 0)
-        time_map(0, 1)
-        time_map(0, 2)
+        time_map(1, 0)
+        h_quant(8, 4)
         decode(4)
         decode(5)
-        time_map(0, 3)
-        time_map(1, 0)
+        time_map(0, 1)
         h_out_scaled(7, 0)
+        h_out_scaled(7, 1)
         h_quant(12, 2)
         decode(6)
-        time_map(1, 1)
-        time_map(1, 2)
-        h_out_scaled(7, 1)
         h_quant(14, 1)
         h_quant(15, 1)
         decode(7)
         x_bias(1, 0, [0, 1])
-        x_turn(2, 0)
-        x_turn(3, 0)
+        time_map(1, 1)
+        time_map(0, 2)
+        x_turn((2,), 0)
+        x_turn((3,), 0)
         x_bias(1, 1, [0])
         x_bias(1, 1, [1])
-        x_turn(2, 1)
-        x_turn(3, 1)
+        x_turn((2,), 1)
+        x_turn((3,), 1)
+        time_map(1, 2)
+        time_map(0, 3)
         time_map(1, 3)
-        x_out(2)
-        x_out(3)
-        x_quant(2)
-        x_quant(3)
+        x_out((2,))
+        x_out((3,))
+        x_quant((2,))
+        x_quant((3,))
         time_map(2, 0)
         time_map(3, 0)
         time_map(2, 1)

@@ -71,13 +71,13 @@ def tile_model_pb_w8_kernel(tc, h_bytes, h_scale, dec_W, dec_b, map_W_words, map
 
         load_w(0)
         load_h(0, [0])
+        load_h(1, [0, 1])
         nc.sync.dma_start(out=rows[0:1, 0 : MODELS * P], in_=dec_b.rearrange("(o n) p -> o (n p)", o=1))
         nc.sync.dma_start(out=rows[0:1, MODELS * P :], in_=map_b.rearrange("(o s) -> o s", o=1))
         load_w(1)
-        load_h(1, [0, 1])
         for k in (2, 3):
-            load_w(k)
             load_h(k, [0, 1])
+            load_w(k)
         load_h(0, [1])
         for q in range(4):
             nc.sync.dma_start(
@@ -90,7 +90,6 @@ def tile_model_pb_w8_kernel(tc, h_bytes, h_scale, dec_W, dec_b, map_W_words, map
             nc.sync.dma_start(out=t[:], in_=map_W_words[g].rearrange("p n t -> p (n t)").bitcast(I32))
             ww.append(t)
 
-        scale = sb([P, D], F32, "scale")
         dec_bias = sb([P, 2, P, 2, 2], BF16, "dec_bias")
         map_bias = sb([P, T], BF16, "map_bias")
 
@@ -98,12 +97,6 @@ def tile_model_pb_w8_kernel(tc, h_bytes, h_scale, dec_W, dec_b, map_W_words, map
         wg, wc, ws = {}, {}, {}
         x_ps, xb, xt, xg, xc, xs = {}, {}, {}, {}, {}, {}
         acc, bias_ps = {}, {}
-
-        def spread_scale():
-            ps = bank(2, [P, D], "scale_ps")
-            for m in range(4):
-                nc.tensor.transpose(ps[:, m * P : (m + 1) * P], scale_col[:, m : m + 1].to_broadcast([P, P]), ident[:])
-            nc.scalar.copy(out=scale[:].rearrange("b (p j) -> b p j", j=4), in_=ps[:].rearrange("b (j p) -> b p j", j=4))
 
         def spread_dec_bias():
             bias_ps["dec"] = bank(3, [P, 2, 512], "dec_bias_ps", BF16)
@@ -115,7 +108,7 @@ def tile_model_pb_w8_kernel(tc, h_bytes, h_scale, dec_W, dec_b, map_W_words, map
             nc.scalar.copy(out=dec_bias[:].rearrange("b u p h e -> b (u p h e)"), in_=bias_ps["dec"][:].rearrange("b u c -> b (u c)"))
 
         def spread_map_bias(b):
-            bias_ps[b] = bank((5, 7)[b], [P, 1024], "map_bias_ps%d" % b, BF16)
+            bias_ps[b] = bank((5, 6)[b], [P, 1024], "map_bias_ps%d" % b, BF16)
             for c in range(2):
                 first = MODELS * P + 1024 * b + 512 * c
                 nc.tensor.matmul(bias_ps[b][:, 512 * c : 512 * (c + 1)], ones[:], rows[:, first : first + 512], start=True, stop=True)
@@ -123,20 +116,17 @@ def tile_model_pb_w8_kernel(tc, h_bytes, h_scale, dec_W, dec_b, map_W_words, map
         def map_bias_out(b):
             nc.scalar.copy(out=map_bias[:, 1024 * b : 1024 * (b + 1)], in_=bias_ps[b][:])
 
-        def widen_scaled(unit, e):
-            hx[unit, e] = sb([P, D], BF16, "hx%d_%d" % (unit, e))
-            nc.vector.tensor_tensor(out=hx[unit, e][:], in0=hb[unit, e], in1=scale[:], op=MULT)
-
         def widen_plain(unit, e):
             hx[unit, e] = sb([P, D], BF16, "hx%d_%d" % (unit, e))
             nc.scalar.copy(out=hx[unit, e][:], in_=hb[unit, e])
 
-        def turn(unit):
-            ht[unit] = bank((0, 1, 0, 1, 0, 1, 6, 7)[unit], [P, 2, 2, P], "ht%d" % unit)
-            for e in range(2):
-                words = hx[unit, e][:].bitcast(F32)
+        def turn(unit, first=0, count=2):
+            b = (0, 1, 7)[unit % 3] if first == 0 else 2
+            ht[unit, first] = bank(b, [P, 2, count * P], "ht%d_%d" % (unit, first))
+            for e in range(count):
+                words = hx[unit, first + e][:].bitcast(F32)
                 for v in range(2):
-                    nc.tensor.transpose(ht[unit][:, e, v], words[:, v::2], ident[:])
+                    nc.tensor.transpose(ht[unit, first][:, v, e * P : (e + 1) * P], words[:, v::2], ident[:])
 
         def grouped(first, count):
             t = sb([P, count * P * 4], BF16, "hg%d" % first)
@@ -146,14 +136,14 @@ def tile_model_pb_w8_kernel(tc, h_bytes, h_scale, dec_W, dec_b, map_W_words, map
                 hg["unit", (first + m) // 2] = t[:, m * 4 * P : (m + 2) * 4 * P]
             hg[first, count] = t
 
-        def h_out(unit):
-            to = hg["unit", unit].bitcast(F32).rearrange("p (e r v) -> p e r v", e=2, v=2)
-            nc.scalar.copy(out=to, in_=ht[unit][:].rearrange("p e v r -> p e r v"))
-
-        def h_out_scaled(unit, e):
-            to = hg[2 * unit + e].rearrange("p (r v z) -> p r v z", v=2, z=2)
-            of = ht[unit][:, e].rearrange("p v r -> p (v r)").bitcast(BF16).rearrange("p (v r z) -> p r v z", v=2, z=2)
-            by = scale_col[:].rearrange("p (o v z) -> p o v z", o=1, v=2).to_broadcast([P, P, 2, 2])
+        def h_out_scaled(unit, first, count):
+            to = (hg["unit", unit] if count == 2 else hg[2 * unit + first]).rearrange("p (r v z) -> p r v z", v=2, z=2)
+            if (unit, first) in ht and ht[unit, first].shape[2] == count * P:
+                turned, rows_r = ht[unit, first], slice(0, count * P)
+            else:
+                turned, rows_r = ht[unit, 0], slice(first * P, (first + count) * P)
+            of = turned[:].rearrange("p v r -> p (v r)").bitcast(BF16).rearrange("p (v r z) -> p r v z", v=2, z=2)[:, rows_r]
+            by = scale_col[:].rearrange("p (o v z) -> p o v z", o=1, v=2).to_broadcast([P, count * P, 2, 2])
             nc.vector.tensor_tensor(out=to, in0=of, in1=by, op=MULT)
 
         def h_quant(first, count):
@@ -207,7 +197,7 @@ def tile_model_pb_w8_kernel(tc, h_bytes, h_scale, dec_W, dec_b, map_W_words, map
 
         def x_turn(groups, u):
             if u == 0:
-                xt[groups] = bank(4 if groups[0] == 0 else 4 + groups[0], [P, len(groups), 2, P], "xt%d" % groups[0])
+                xt[groups] = bank((4, 4, 0, 1)[groups[0]], [P, len(groups), 2, P], "xt%d" % groups[0])
             for a, g in enumerate(groups):
                 nc.tensor.transpose(xt[groups][:, a, u], xb[g, u], ident[:])
 
@@ -226,7 +216,7 @@ def tile_model_pb_w8_kernel(tc, h_bytes, h_scale, dec_W, dec_b, map_W_words, map
 
         def time_map(g, s):
             if g == 0:
-                acc[s] = bank((5, 0, 4, 1)[s], [P, 512], "acc%d" % s)
+                acc[s] = bank((5, 6, 7, 4)[s], [P, 512], "acc%d" % s)
             cols = slice(512 * s, 512 * (s + 1))
             nc.tensor.matmul_mx(
                 out=acc[s][:],
@@ -247,96 +237,97 @@ def tile_model_pb_w8_kernel(tc, h_bytes, h_scale, dec_W, dec_b, map_W_words, map
                 nc.vector.tensor_tensor(out=y[:, here], in0=acc[s][:, here], in1=map_bias[:, cols], op=ADD)
                 nc.sync.dma_start(out=out.rearrange("b c s -> (b c) s")[:, cols], in_=y[:, here])
 
-        for first, count in ((0, 4), (4, 2), (6, 2), (8, 4), (12, 2), (14, 1), (15, 1)):
+        for first, count in ((0, 4), (4, 4), (8, 4), (12, 2), (14, 1), (15, 1)):
             grouped(first, count)
 
-        spread_scale()
         w_group(0, 0)
         w_group(0, 1)
         w_quant(0)
+        widen_plain(0, 0)
+        widen_plain(0, 1)
+        turn(0, 0, 1)
+        turn(0, 1, 1)
+        widen_plain(1, 0)
+        widen_plain(1, 1)
+        turn(1)
+        spread_dec_bias()
         w_group(1, 0)
         w_group(1, 1)
-        spread_dec_bias()
+        widen_plain(2, 0)
+        widen_plain(2, 1)
+        turn(2)
         spread_map_bias(0)
-        spread_map_bias(1)
-        widen_scaled(0, 0)
-        widen_scaled(0, 1)
-        turn(0)
+        h_out_scaled(0, 0, 1)
+        h_out_scaled(0, 1, 1)
+        h_out_scaled(1, 0, 2)
         w_group(2, 0)
+        widen_plain(3, 0)
+        widen_plain(3, 1)
+        turn(3)
+        spread_map_bias(1)
         w_group(2, 1)
         w_group(3, 0)
-        h_out(0)
-        widen_scaled(1, 0)
-        widen_scaled(1, 1)
-        turn(1)
-        h_out(1)
-        w_quant(1)
-        widen_scaled(2, 0)
-        widen_scaled(2, 1)
-        turn(2)
         w_group(3, 1)
-        h_out(2)
-        dec_bias_out()
-        w_quant(2)
-        widen_scaled(3, 0)
+        w_quant(1)
         h_quant(0, 4)
-        widen_scaled(3, 1)
         decode(0)
         decode(1)
-        turn(3)
-        h_out(3)
-        map_bias_out(1)
+        widen_plain(4, 0)
+        widen_plain(4, 1)
+        turn(4)
+        dec_bias_out()
+        h_out_scaled(2, 0, 2)
+        h_out_scaled(3, 0, 2)
+        widen_plain(5, 0)
+        widen_plain(5, 1)
+        w_quant(2)
         w_quant(3)
-        x_bias(0, 0, [0, 1])
-        h_quant(4, 2)
-        widen_scaled(4, 0)
-        h_quant(6, 2)
+        h_quant(4, 4)
         decode(2)
         decode(3)
-        widen_scaled(4, 1)
-        turn(4)
-        widen_plain(7, 0)
-        h_out(4)
-        x_bias(0, 1, [0, 1])
-        x_turn((0, 1), 0)
-        x_turn((0, 1), 1)
-        x_out((0, 1))
-        widen_plain(7, 1)
-        widen_scaled(5, 0)
-        widen_scaled(5, 1)
         turn(5)
-        h_out(5)
-        map_bias_out(0)
-        turn(7)
-        widen_scaled(6, 0)
-        x_quant((0, 1))
-        widen_scaled(6, 1)
+        widen_plain(6, 0)
+        widen_plain(6, 1)
+        x_bias(0, 0, [0, 1])
         turn(6)
-        h_out(6)
+        widen_plain(7, 0)
+        widen_plain(7, 1)
+        map_bias_out(0)
+        x_turn((0, 1), 0)
+        h_out_scaled(4, 0, 2)
+        x_bias(0, 1, [0, 1])
+        x_turn((0, 1), 1)
+        turn(7)
+        x_out((0, 1))
+        map_bias_out(1)
+        h_out_scaled(5, 0, 2)
+        h_out_scaled(6, 0, 1)
+        x_quant((0, 1))
         time_map(0, 0)
         time_map(1, 0)
+        time_map(0, 1)
+        h_out_scaled(6, 1, 1)
         h_quant(8, 4)
         decode(4)
         decode(5)
-        time_map(0, 1)
-        h_out_scaled(7, 0)
-        h_out_scaled(7, 1)
+        time_map(1, 1)
+        time_map(0, 2)
+        h_out_scaled(7, 0, 1)
         h_quant(12, 2)
         decode(6)
+        time_map(1, 2)
+        h_out_scaled(7, 1, 1)
         h_quant(14, 1)
         h_quant(15, 1)
         decode(7)
         x_bias(1, 0, [0, 1])
-        time_map(1, 1)
-        time_map(0, 2)
+        time_map(0, 3)
         x_turn((2,), 0)
         x_turn((3,), 0)
         x_bias(1, 1, [0])
         x_bias(1, 1, [1])
         x_turn((2,), 1)
         x_turn((3,), 1)
-        time_map(1, 2)
-        time_map(0, 3)
         time_map(1, 3)
         x_out((2,))
         x_out((3,))

@@ -12,6 +12,7 @@ FP8 = mybir.dt.float8_e4m3fn
 FP8X4 = mybir.dt.float8_e4m3fn_x4
 MULT = mybir.AluOpType.mult
 ADD = mybir.AluOpType.add
+COPY = mybir.ActivationFunctionType.Copy
 
 P = 128
 MODELS = 8
@@ -84,22 +85,31 @@ def tile_model_pb_w8_kernel(tc, h_bytes, h_scale, dec_W, dec_b, map_W_words, map
                 out=wsc[32 * q : 32 * q + 16, :].bitcast(I32),
                 in_=map_W_scales[:, 4 * q : 4 * q + 4, :].bitcast(I32),
             )
-        ww = []
-        for g in range(GROUPS):
-            t = sb([P, T], I32, "ww%d" % g)
-            nc.sync.dma_start(out=t[:], in_=map_W_words[g].rearrange("p n t -> p (n t)").bitcast(I32))
-            ww.append(t)
+        ww = {}
+
+        def load_map_w(g, first, count):
+            t = sb([P, 512 * count], I32, "ww%d_%d" % (g, first))
+            words = map_W_words[g].rearrange("p n t -> p (n t)").bitcast(I32)
+            nc.sync.dma_start(out=t[:], in_=words[:, 512 * first : 512 * (first + count)])
+            for s in range(count):
+                ww[g, first + s] = t[:, 512 * s : 512 * (s + 1)]
+
+        for g in (0, 1):
+            load_map_w(g, 0, 4)
+        for first in (0, 2):
+            for g in (2, 3):
+                load_map_w(g, first, 2)
 
         dec_bias = sb([P, 2, P, 2, 2], BF16, "dec_bias")
         map_bias = sb([P, T], BF16, "map_bias")
 
-        hx, ht, hg, hc, hs = {}, {}, {}, {}, {}
+        hx, ht, hw, hg, hc, hs = {}, {}, {}, {}, {}, {}
         wg, wc, ws = {}, {}, {}
         x_ps, xb, xt, xg, xc, xs = {}, {}, {}, {}, {}, {}
         acc, bias_ps = {}, {}
 
         def spread_dec_bias():
-            bias_ps["dec"] = bank(3, [P, 2, 512], "dec_bias_ps", BF16)
+            bias_ps["dec"] = bank(4, [P, 2, 512], "dec_bias_ps", BF16)
             by_u = rows[:, 0 : MODELS * P].rearrange("k (h u e p) -> k u p h e", h=2, u=2, e=2)
             for u in range(2):
                 nc.tensor.matmul(bias_ps["dec"][:, u], ones[:], by_u[:, u], start=True, stop=True)
@@ -146,6 +156,18 @@ def tile_model_pb_w8_kernel(tc, h_bytes, h_scale, dec_W, dec_b, map_W_words, map
             by = scale_col[:].rearrange("p (o v z) -> p o v z", o=1, v=2).to_broadcast([P, count * P, 2, 2])
             nc.vector.tensor_tensor(out=to, in0=of, in1=by, op=MULT)
 
+        def h_out_scalar(unit, v):
+            if v == 0:
+                hw[unit] = sb([P, 2, 2 * P, 2], BF16, "hw%d" % unit)
+            of = ht[unit, 0][:, v].bitcast(BF16).rearrange("p (r z) -> p r z", z=2)
+            for z in range(2):
+                t = 2 * v + z
+                nc.scalar.activation(out=hw[unit][:, v, :, z], in_=of[:, :, z], func=COPY, scale=scale_col[:, t : t + 1])
+
+        def h_join(unit):
+            words = hw[unit][:].rearrange("p v r z -> p (v r z)").bitcast(F32).rearrange("p (v r) -> p r v", v=2)
+            nc.scalar.copy(out=hg["unit", unit].bitcast(F32).rearrange("p (r v) -> p r v", v=2), in_=words)
+
         def h_quant(first, count):
             codes = sb([P, count * P], U32, "hc%d" % first)
             scales = sb([P, count * P], U8, "hs%d" % first)
@@ -172,7 +194,7 @@ def tile_model_pb_w8_kernel(tc, h_bytes, h_scale, dec_W, dec_b, map_W_words, map
         def decode(unit):
             l, k = divmod(unit, 4)
             u, h = divmod(k, 2)
-            if h == 0:
+            if (l, u) not in x_ps:
                 x_ps[l, u] = bank(2 + u, [P, 2, 2, P], "x_ps%d_%d" % (l, u))
             for e in range(2):
                 cols = slice(e * P, (e + 1) * P)
@@ -197,7 +219,7 @@ def tile_model_pb_w8_kernel(tc, h_bytes, h_scale, dec_W, dec_b, map_W_words, map
 
         def x_turn(groups, u):
             if u == 0:
-                xt[groups] = bank((4, 4, 0, 1)[groups[0]], [P, len(groups), 2, P], "xt%d" % groups[0])
+                xt[groups] = bank((4, 4, 5, 6)[groups[0]], [P, len(groups), 2, P], "xt%d" % groups[0])
             for a, g in enumerate(groups):
                 nc.tensor.transpose(xt[groups][:, a, u], xb[g, u], ident[:])
 
@@ -216,13 +238,13 @@ def tile_model_pb_w8_kernel(tc, h_bytes, h_scale, dec_W, dec_b, map_W_words, map
 
         def time_map(g, s):
             if g == 0:
-                acc[s] = bank((5, 6, 7, 4)[s], [P, 512], "acc%d" % s)
+                acc[s] = bank((4, 7, 1, 0)[s], [P, 512], "acc%d" % s)
             cols = slice(512 * s, 512 * (s + 1))
             nc.tensor.matmul_mx(
                 out=acc[s][:],
                 lhsT=xc[g].bitcast(FP8X4),
                 lhsT_scale=xs[g],
-                rhs=ww[g][:, cols].bitcast(FP8X4),
+                rhs=ww[g, s].bitcast(FP8X4),
                 rhs_scale=wsc[4 * g : P, cols],
                 start=(g == 0),
                 stop=(g == GROUPS - 1),
@@ -237,7 +259,7 @@ def tile_model_pb_w8_kernel(tc, h_bytes, h_scale, dec_W, dec_b, map_W_words, map
                 nc.vector.tensor_tensor(out=y[:, here], in0=acc[s][:, here], in1=map_bias[:, cols], op=ADD)
                 nc.sync.dma_start(out=out.rearrange("b c s -> (b c) s")[:, cols], in_=y[:, here])
 
-        for first, count in ((0, 4), (4, 4), (8, 4), (12, 2), (14, 1), (15, 1)):
+        for first, count in ((0, 4), (4, 2), (6, 2), (8, 4), (12, 2), (14, 1), (15, 1)):
             grouped(first, count)
 
         w_group(0, 0)
@@ -274,61 +296,64 @@ def tile_model_pb_w8_kernel(tc, h_bytes, h_scale, dec_W, dec_b, map_W_words, map
         decode(1)
         widen_plain(4, 0)
         widen_plain(4, 1)
-        turn(4)
         dec_bias_out()
         h_out_scaled(2, 0, 2)
+        w_quant(2)
+        h_quant(4, 2)
+        decode(2)
+        turn(4)
         h_out_scaled(3, 0, 2)
         widen_plain(5, 0)
         widen_plain(5, 1)
-        w_quant(2)
         w_quant(3)
-        h_quant(4, 4)
-        decode(2)
+        h_quant(6, 2)
         decode(3)
         turn(5)
         widen_plain(6, 0)
         widen_plain(6, 1)
         x_bias(0, 0, [0, 1])
+        x_turn((0, 1), 0)
+        x_bias(0, 1, [0, 1])
+        x_turn((0, 1), 1)
         turn(6)
         widen_plain(7, 0)
         widen_plain(7, 1)
-        map_bias_out(0)
-        x_turn((0, 1), 0)
-        h_out_scaled(4, 0, 2)
-        x_bias(0, 1, [0, 1])
-        x_turn((0, 1), 1)
-        turn(7)
         x_out((0, 1))
+        h_out_scalar(6, 0)
+        h_out_scalar(6, 1)
+        h_join(6)
+        map_bias_out(0)
         map_bias_out(1)
-        h_out_scaled(5, 0, 2)
-        h_out_scaled(6, 0, 1)
+        h_out_scaled(4, 0, 2)
+        turn(7)
+        h_out_scaled(5, 0, 1)
         x_quant((0, 1))
         time_map(0, 0)
         time_map(1, 0)
+        h_out_scaled(5, 1, 1)
         time_map(0, 1)
-        h_out_scaled(6, 1, 1)
+        time_map(1, 1)
+        h_out_scaled(7, 0, 1)
         h_quant(8, 4)
         decode(4)
         decode(5)
-        time_map(1, 1)
-        time_map(0, 2)
-        h_out_scaled(7, 0, 1)
         h_quant(12, 2)
         decode(6)
-        time_map(1, 2)
         h_out_scaled(7, 1, 1)
+        time_map(0, 3)
         h_quant(14, 1)
         h_quant(15, 1)
         decode(7)
         x_bias(1, 0, [0, 1])
-        time_map(0, 3)
+        time_map(1, 3)
         x_turn((2,), 0)
         x_turn((3,), 0)
         x_bias(1, 1, [0])
         x_bias(1, 1, [1])
         x_turn((2,), 1)
         x_turn((3,), 1)
-        time_map(1, 3)
+        time_map(0, 2)
+        time_map(1, 2)
         x_out((2,))
         x_out((3,))
         x_quant((2,))

@@ -138,8 +138,8 @@ def tile_model_pb_w8_kernel(tc, h_bytes, h_scale, dec_W, dec_b, map_W_words, map
                 for v in range(2):
                     nc.tensor.transpose(ht[unit, first][:, v, e * P : (e + 1) * P], words[:, v::2], ident[:])
 
-        def grouped(first, count):
-            t = sb([P, count * P * 4], BF16, "hg%d" % first)
+        def grouped(first, count, tag):
+            t = keep.tile([P, count * P * 4], BF16, name="hg%d" % first, tag=tag, align_bytes=64)
             for m in range(count):
                 hg[first + m] = t[:, m * 4 * P : (m + 1) * 4 * P]
             for m in range(0, count - 1, 2):
@@ -156,17 +156,14 @@ def tile_model_pb_w8_kernel(tc, h_bytes, h_scale, dec_W, dec_b, map_W_words, map
             by = scale_col[:].rearrange("p (o v z) -> p o v z", o=1, v=2).to_broadcast([P, count * P, 2, 2])
             nc.vector.tensor_tensor(out=to, in0=of, in1=by, op=MULT)
 
-        def h_out_scalar(unit, v):
-            if v == 0:
-                hw[unit] = sb([P, 2, 2 * P, 2], BF16, "hw%d" % unit)
-            of = ht[unit, 0][:, v].bitcast(BF16).rearrange("p (r z) -> p r z", z=2)
-            for z in range(2):
-                t = 2 * v + z
-                nc.scalar.activation(out=hw[unit][:, v, :, z], in_=of[:, :, z], func=COPY, scale=scale_col[:, t : t + 1])
+        def h_out_plain(unit):
+            hw[unit] = sb([P, 2 * P, 4], BF16, "hw%d" % unit)
+            to = hw[unit][:].rearrange("p r t -> p (r t)").bitcast(F32).rearrange("p (r v) -> p r v", v=2)
+            nc.scalar.copy(out=to, in_=ht[unit, 0][:].rearrange("p v r -> p r v"))
 
-        def h_join(unit):
-            words = hw[unit][:].rearrange("p v r z -> p (v r z)").bitcast(F32).rearrange("p (v r) -> p r v", v=2)
-            nc.scalar.copy(out=hg["unit", unit].bitcast(F32).rearrange("p (r v) -> p r v", v=2), in_=words)
+        def h_scale_pool(unit):
+            by = scale_col[:].rearrange("p (o t) -> p o t", o=1).to_broadcast([P, 2 * P, 4])
+            nc.gpsimd.tensor_tensor(out=hg["unit", unit].rearrange("p (r t) -> p r t", t=4), in0=hw[unit][:], in1=by, op=MULT)
 
         def h_quant(first, count):
             codes = sb([P, count * P], U32, "hc%d" % first)
@@ -219,7 +216,7 @@ def tile_model_pb_w8_kernel(tc, h_bytes, h_scale, dec_W, dec_b, map_W_words, map
 
         def x_turn(groups, u):
             if u == 0:
-                xt[groups] = bank((4, 4, 5, 6)[groups[0]], [P, len(groups), 2, P], "xt%d" % groups[0])
+                xt[groups] = bank((4, 4, 0, 1)[groups[0]], [P, len(groups), 2, P], "xt%d" % groups[0])
             for a, g in enumerate(groups):
                 nc.tensor.transpose(xt[groups][:, a, u], xb[g, u], ident[:])
 
@@ -238,7 +235,7 @@ def tile_model_pb_w8_kernel(tc, h_bytes, h_scale, dec_W, dec_b, map_W_words, map
 
         def time_map(g, s):
             if g == 0:
-                acc[s] = bank((4, 7, 1, 0)[s], [P, 512], "acc%d" % s)
+                acc[s] = bank((4, 7, 6, 5)[s], [P, 512], "acc%d" % s)
             cols = slice(512 * s, 512 * (s + 1))
             nc.tensor.matmul_mx(
                 out=acc[s][:],
@@ -259,8 +256,8 @@ def tile_model_pb_w8_kernel(tc, h_bytes, h_scale, dec_W, dec_b, map_W_words, map
                 nc.vector.tensor_tensor(out=y[:, here], in0=acc[s][:, here], in1=map_bias[:, cols], op=ADD)
                 nc.sync.dma_start(out=out.rearrange("b c s -> (b c) s")[:, cols], in_=y[:, here])
 
-        for first, count in ((0, 4), (4, 2), (6, 2), (8, 4), (12, 2), (14, 1), (15, 1)):
-            grouped(first, count)
+        for first, count in ((0, 4), (4, 2), (6, 2), (10, 2), (12, 2), (14, 1), (15, 1)):
+            grouped(first, count, "hg%d" % first)
 
         w_group(0, 0)
         w_group(0, 1)
@@ -278,7 +275,6 @@ def tile_model_pb_w8_kernel(tc, h_bytes, h_scale, dec_W, dec_b, map_W_words, map
         widen_plain(2, 0)
         widen_plain(2, 1)
         turn(2)
-        spread_map_bias(0)
         h_out_scaled(0, 0, 1)
         h_out_scaled(0, 1, 1)
         h_out_scaled(1, 0, 2)
@@ -305,10 +301,13 @@ def tile_model_pb_w8_kernel(tc, h_bytes, h_scale, dec_W, dec_b, map_W_words, map
         h_out_scaled(3, 0, 2)
         widen_plain(5, 0)
         widen_plain(5, 1)
+        h_out_plain(4)
         w_quant(3)
         h_quant(6, 2)
         decode(3)
         turn(5)
+        grouped(8, 2, "hg6")
+        h_scale_pool(4)
         widen_plain(6, 0)
         widen_plain(6, 1)
         x_bias(0, 0, [0, 1])
@@ -319,41 +318,40 @@ def tile_model_pb_w8_kernel(tc, h_bytes, h_scale, dec_W, dec_b, map_W_words, map
         widen_plain(7, 0)
         widen_plain(7, 1)
         x_out((0, 1))
-        h_out_scalar(6, 0)
-        h_out_scalar(6, 1)
-        h_join(6)
-        map_bias_out(0)
         map_bias_out(1)
-        h_out_scaled(4, 0, 2)
         turn(7)
-        h_out_scaled(5, 0, 1)
+        spread_map_bias(0)
+        map_bias_out(0)
+        h_out_scaled(5, 0, 2)
+        h_out_scaled(6, 0, 1)
         x_quant((0, 1))
         time_map(0, 0)
         time_map(1, 0)
-        h_out_scaled(5, 1, 1)
         time_map(0, 1)
+        h_out_scaled(6, 1, 1)
+        h_quant(10, 2)
+        h_quant(8, 2)
+        decode(5)
+        decode(4)
         time_map(1, 1)
         h_out_scaled(7, 0, 1)
-        h_quant(8, 4)
-        decode(4)
-        decode(5)
         h_quant(12, 2)
+        time_map(0, 2)
         decode(6)
         h_out_scaled(7, 1, 1)
-        time_map(0, 3)
         h_quant(14, 1)
         h_quant(15, 1)
         decode(7)
         x_bias(1, 0, [0, 1])
-        time_map(1, 3)
+        time_map(1, 2)
         x_turn((2,), 0)
         x_turn((3,), 0)
         x_bias(1, 1, [0])
         x_bias(1, 1, [1])
         x_turn((2,), 1)
         x_turn((3,), 1)
-        time_map(0, 2)
-        time_map(1, 2)
+        time_map(0, 3)
+        time_map(1, 3)
         x_out((2,))
         x_out((3,))
         x_quant((2,))

@@ -67,15 +67,17 @@ def tile_model_pb_w8_kernel(tc, h_bytes, h_scale, dec_W, dec_b, map_W_words, map
         nc.vector.memset(rows[:].bitcast(I32), 0)
         wsc = sb([P, T], U8, "wsc")
         nc.vector.memset(wsc[:].bitcast(I32), 0)
+        ident_bf = sb([P, P], BF16, "ident_bf")
+        nc.gpsimd.tensor_copy(out=ident_bf[:], in_=ident[:])
         ones = sb([P, P], BF16, "ones")
         nc.gpsimd.memset(ones[:], 1.0)
 
         load_w(0)
         load_h(0, [0])
         load_h(1, [0, 1])
+        load_w(1)
         nc.sync.dma_start(out=rows[0:1, 0 : MODELS * P], in_=dec_b.rearrange("(o n) p -> o (n p)", o=1))
         nc.sync.dma_start(out=rows[0:1, MODELS * P :], in_=map_b.rearrange("(o s) -> o s", o=1))
-        load_w(1)
         for k in (2, 3):
             load_h(k, [0, 1])
             load_w(k)
@@ -103,16 +105,15 @@ def tile_model_pb_w8_kernel(tc, h_bytes, h_scale, dec_W, dec_b, map_W_words, map
         dec_bias = sb([P, 2, P, 2, 2], BF16, "dec_bias")
         map_bias = sb([P, T], BF16, "map_bias")
 
-        hx, ht, hw, hg, hc, hs = {}, {}, {}, {}, {}, {}
-        wg, wc, ws = {}, {}, {}
-        x_ps, xb, xt, xg, xc, xs = {}, {}, {}, {}, {}, {}
-        acc, bias_ps = {}, {}
+        hx, ht, hw = {}, {}, {}
+        batches, place, codes, scales = {}, {}, {}, {}
+        x_ps, xb, xt, acc, bias_ps = {}, {}, {}, {}, {}
 
-        def spread_dec_bias():
-            bias_ps["dec"] = bank(4, [P, 2, 512], "dec_bias_ps", BF16)
+        def spread_dec_bias(u):
+            if u == 0:
+                bias_ps["dec"] = bank(4, [P, 2, 512], "dec_bias_ps", BF16)
             by_u = rows[:, 0 : MODELS * P].rearrange("k (h u e p) -> k u p h e", h=2, u=2, e=2)
-            for u in range(2):
-                nc.tensor.matmul(bias_ps["dec"][:, u], ones[:], by_u[:, u], start=True, stop=True)
+            nc.tensor.matmul(bias_ps["dec"][:, u], ones[:], by_u[:, u], start=True, stop=True)
 
         def dec_bias_out():
             nc.scalar.copy(out=dec_bias[:].rearrange("b u p h e -> b (u p h e)"), in_=bias_ps["dec"][:].rearrange("b u c -> b (u c)"))
@@ -131,23 +132,34 @@ def tile_model_pb_w8_kernel(tc, h_bytes, h_scale, dec_W, dec_b, map_W_words, map
             nc.scalar.copy(out=hx[unit, e][:], in_=hb[unit, e])
 
         def turn(unit, first=0, count=2):
-            b = (0, 1, 7)[unit % 3] if first == 0 else 2
+            b = (0, 1, 0, 1, 7, 7, 0, 1)[unit] if first == 0 else 2
             ht[unit, first] = bank(b, [P, 2, count * P], "ht%d_%d" % (unit, first))
             for e in range(count):
                 words = hx[unit, first + e][:].bitcast(F32)
                 for v in range(2):
                     nc.tensor.transpose(ht[unit, first][:, v, e * P : (e + 1) * P], words[:, v::2], ident[:])
 
-        def grouped(first, count, tag):
-            t = keep.tile([P, count * P * 4], BF16, name="hg%d" % first, tag=tag, align_bytes=64)
-            for m in range(count):
-                hg[first + m] = t[:, m * 4 * P : (m + 1) * 4 * P]
-            for m in range(0, count - 1, 2):
-                hg["unit", (first + m) // 2] = t[:, m * 4 * P : (m + 2) * 4 * P]
-            hg[first, count] = t
+        def batch(name, keys, tag=None):
+            t = keep.tile([P, len(keys) * D], BF16, name="in_" + name, tag=tag or "in_" + name, align_bytes=64)
+            batches[name] = (t, keys)
+            for m, key in enumerate(keys):
+                place[key] = (t, m)
+
+        def slots(key, count):
+            t, m = place[key]
+            return t[:, m * D : (m + count) * D]
+
+        def quantise(name):
+            t, keys = batches[name]
+            words = sb([P, len(keys) * P], U32, "codes_" + name)
+            plane = sb([P, len(keys) * P], U8, "scales_" + name)
+            nc.vector.quantize_mx(out=words[:].bitcast(FP8X4), scales=plane[:], in_=t[:])
+            for m, key in enumerate(keys):
+                codes[key] = words[:, m * P : (m + 1) * P].bitcast(FP8X4)
+                scales[key] = plane[:, m * P : (m + 1) * P]
 
         def h_out_scaled(unit, first, count):
-            to = (hg["unit", unit] if count == 2 else hg[2 * unit + first]).rearrange("p (r v z) -> p r v z", v=2, z=2)
+            to = slots(("h", unit, first), count).rearrange("p (r v z) -> p r v z", v=2, z=2)
             if (unit, first) in ht and ht[unit, first].shape[2] == count * P:
                 turned, rows_r = ht[unit, first], slice(0, count * P)
             else:
@@ -156,37 +168,32 @@ def tile_model_pb_w8_kernel(tc, h_bytes, h_scale, dec_W, dec_b, map_W_words, map
             by = scale_col[:].rearrange("p (o v z) -> p o v z", o=1, v=2).to_broadcast([P, count * P, 2, 2])
             nc.vector.tensor_tensor(out=to, in0=of, in1=by, op=MULT)
 
-        def h_out_plain(unit):
-            hw[unit] = sb([P, 2 * P, 4], BF16, "hw%d" % unit)
+        def h_out_plain(unit, count):
+            hw[unit] = sb([P, count * P, 4], BF16, "hw%d" % unit)
             to = hw[unit][:].rearrange("p r t -> p (r t)").bitcast(F32).rearrange("p (r v) -> p r v", v=2)
-            nc.scalar.copy(out=to, in_=ht[unit, 0][:].rearrange("p v r -> p r v"))
+            nc.scalar.copy(out=to, in_=ht[unit, 0][:, :, 0 : count * P].rearrange("p v r -> p r v"))
 
-        def h_scale_pool(unit):
-            by = scale_col[:].rearrange("p (o t) -> p o t", o=1).to_broadcast([P, 2 * P, 4])
-            nc.gpsimd.tensor_tensor(out=hg["unit", unit].rearrange("p (r t) -> p r t", t=4), in0=hw[unit][:], in1=by, op=MULT)
+        def h_scale_pool(unit, count):
+            by = scale_col[:].rearrange("p (o t) -> p o t", o=1).to_broadcast([P, count * P, 4])
+            nc.gpsimd.tensor_tensor(out=slots(("h", unit, 0), count).rearrange("p (r t) -> p r t", t=4), in0=hw[unit][:], in1=by, op=MULT)
 
-        def h_quant(first, count):
-            codes = sb([P, count * P], U32, "hc%d" % first)
-            scales = sb([P, count * P], U8, "hs%d" % first)
-            nc.vector.quantize_mx(out=codes[:].bitcast(FP8X4), scales=scales[:], in_=hg[first, count][:])
-            for m in range(count):
-                hc[first + m] = codes[:, m * P : (m + 1) * P]
-                hs[first + m] = scales[:, m * P : (m + 1) * P]
+        def w_group(engine_copy, k, first, count):
+            to = slots(("w", k, first), count).rearrange("p (e c i t) -> p e c t i", e=count, i=4, t=4)
+            of = w_raw[k][:, first : first + count].rearrange("p e t (c i) -> p e c t i", i=4)
+            engine_copy(out=to, in_=of)
 
-        def w_group(k, e):
-            if e == 0:
-                wg[k] = sb([P, 2, P, 4], BF16, "wg%d" % k)
-            to = wg[k][:, e].rearrange("p (c i) t -> p c t i", i=4)
-            of = w_raw[k][:, e].rearrange("p t (c i) -> p c t i", i=4)
-            if k == 0:
-                nc.vector.tensor_copy(out=to, in_=of)
-            else:
-                nc.scalar.copy(out=to, in_=of)
+        def w_group_pool(k):
+            to = slots(("w", k, 0), 2).rearrange("p (e c t) -> p e c t", e=2, t=4)
+            of = w_raw[k][:].rearrange("p e t c -> p e c t")
+            nc.gpsimd.tensor_scalar(out=to, in0=of, scalar1=1.0, scalar2=0.0, op0=MULT, op1=ADD)
 
-        def w_quant(k):
-            wc[k] = sb([P, 2 * P], U32, "wc%d" % k)
-            ws[k] = sb([P, 2 * P], U8, "ws%d" % k)
-            nc.vector.quantize_mx(out=wc[k][:].bitcast(FP8X4), scales=ws[k][:], in_=wg[k][:].rearrange("p i r k -> p (i r k)"))
+        def w_group_tensor(k):
+            bias_ps["w", k] = bank(5, [P, 2, 512], "w_ps%d" % k, BF16)
+            for e in range(2):
+                nc.tensor.matmul(bias_ps["w", k][:, e], ident_bf[:], w_raw[k][:, e].rearrange("p t c -> p c t"), start=True, stop=True)
+
+        def w_out(k):
+            nc.scalar.copy(out=slots(("w", k, 0), 2), in_=bias_ps["w", k][:].rearrange("p e x -> p (e x)"))
 
         def decode(unit):
             l, k = divmod(unit, 4)
@@ -194,13 +201,12 @@ def tile_model_pb_w8_kernel(tc, h_bytes, h_scale, dec_W, dec_b, map_W_words, map
             if (l, u) not in x_ps:
                 x_ps[l, u] = bank(2 + u, [P, 2, 2, P], "x_ps%d_%d" % (l, u))
             for e in range(2):
-                cols = slice(e * P, (e + 1) * P)
                 nc.tensor.matmul_mx(
                     out=x_ps[l, u][:, h, e],
-                    lhsT=hc[2 * unit + e].bitcast(FP8X4),
-                    lhsT_scale=hs[2 * unit + e],
-                    rhs=wc[k][:, cols].bitcast(FP8X4),
-                    rhs_scale=ws[k][:, cols],
+                    lhsT=codes["h", unit, e],
+                    lhsT_scale=scales["h", unit, e],
+                    rhs=codes["w", k, e],
+                    rhs_scale=scales["w", k, e],
                     start=True,
                     stop=True,
                 )
@@ -221,17 +227,8 @@ def tile_model_pb_w8_kernel(tc, h_bytes, h_scale, dec_W, dec_b, map_W_words, map
                 nc.tensor.transpose(xt[groups][:, a, u], xb[g, u], ident[:])
 
         def x_out(groups):
-            xg[groups] = sb([P, len(groups) * P * 4], BF16, "xg%d" % groups[0])
-            to = xg[groups][:].bitcast(F32).rearrange("p (a r u) -> p a r u", a=len(groups), u=2)
+            to = slots(("x", groups[0]), len(groups)).bitcast(F32).rearrange("p (a r u) -> p a r u", a=len(groups), u=2)
             nc.scalar.copy(out=to, in_=xt[groups][:].rearrange("p a u r -> p a r u"))
-
-        def x_quant(groups):
-            codes = sb([P, len(groups) * P], U32, "xc%d" % groups[0])
-            scales = sb([P, len(groups) * P], U8, "xs%d" % groups[0])
-            nc.vector.quantize_mx(out=codes[:].bitcast(FP8X4), scales=scales[:], in_=xg[groups][:])
-            for a, g in enumerate(groups):
-                xc[g] = codes[:, a * P : (a + 1) * P]
-                xs[g] = scales[:, a * P : (a + 1) * P]
 
         def time_map(g, s):
             if g == 0:
@@ -239,8 +236,8 @@ def tile_model_pb_w8_kernel(tc, h_bytes, h_scale, dec_W, dec_b, map_W_words, map
             cols = slice(512 * s, 512 * (s + 1))
             nc.tensor.matmul_mx(
                 out=acc[s][:],
-                lhsT=xc[g].bitcast(FP8X4),
-                lhsT_scale=xs[g],
+                lhsT=codes["x", g],
+                lhsT_scale=scales["x", g],
                 rhs=ww[g, s].bitcast(FP8X4),
                 rhs_scale=wsc[4 * g : P, cols],
                 start=(g == 0),
@@ -256,12 +253,22 @@ def tile_model_pb_w8_kernel(tc, h_bytes, h_scale, dec_W, dec_b, map_W_words, map
                 nc.vector.tensor_tensor(out=y[:, here], in0=acc[s][:, here], in1=map_bias[:, cols], op=ADD)
                 nc.sync.dma_start(out=out.rearrange("b c s -> (b c) s")[:, cols], in_=y[:, here])
 
-        for first, count in ((0, 4), (4, 2), (6, 2), (10, 2), (12, 2), (14, 1), (15, 1)):
-            grouped(first, count, "hg%d" % first)
+        def h_keys(*units):
+            return [("h", unit, e) for unit in units for e in range(2)]
 
-        w_group(0, 0)
-        w_group(0, 1)
-        w_quant(0)
+        def w_keys(k):
+            return [("w", k, e) for e in range(2)]
+
+        batch("w0", w_keys(0))
+        batch("x01", [("x", 0), ("x", 1)])
+        batch("x2", [("x", 2)])
+        batch("x3", [("x", 3)])
+
+        w_group(nc.vector.tensor_copy, 0, 0, 2)
+        quantise("w0")
+        batch("a", h_keys(0, 1) + w_keys(1) + w_keys(2), "in_w0")
+        batch("b", h_keys(2, 3, 5) + w_keys(3))
+        w_group_pool(1)
         widen_plain(0, 0)
         widen_plain(0, 1)
         turn(0, 0, 1)
@@ -269,80 +276,72 @@ def tile_model_pb_w8_kernel(tc, h_bytes, h_scale, dec_W, dec_b, map_W_words, map
         widen_plain(1, 0)
         widen_plain(1, 1)
         turn(1)
-        spread_dec_bias()
-        w_group(1, 0)
-        w_group(1, 1)
+        widen_plain(5, 0)
+        widen_plain(5, 1)
+        turn(5)
         widen_plain(2, 0)
         widen_plain(2, 1)
-        turn(2)
+        h_out_plain(5, 2)
+        h_scale_pool(5, 2)
         h_out_scaled(0, 0, 1)
+        turn(2)
+        spread_dec_bias(0)
         h_out_scaled(0, 1, 1)
         h_out_scaled(1, 0, 2)
-        w_group(2, 0)
         widen_plain(3, 0)
         widen_plain(3, 1)
         turn(3)
-        spread_map_bias(1)
-        w_group(2, 1)
-        w_group(3, 0)
-        w_group(3, 1)
-        w_quant(1)
-        h_quant(0, 4)
-        decode(0)
-        decode(1)
+        w_group_tensor(3)
+        w_group(nc.scalar.copy, 2, 0, 2)
         widen_plain(4, 0)
         widen_plain(4, 1)
-        dec_bias_out()
-        h_out_scaled(2, 0, 2)
-        w_quant(2)
-        h_quant(4, 2)
-        decode(2)
         turn(4)
-        h_out_scaled(3, 0, 2)
-        widen_plain(5, 0)
-        widen_plain(5, 1)
-        h_out_plain(4)
-        w_quant(3)
-        h_quant(6, 2)
-        decode(3)
-        turn(5)
-        grouped(8, 2, "hg6")
-        h_scale_pool(4)
+        h_out_scaled(2, 0, 2)
         widen_plain(6, 0)
         widen_plain(6, 1)
-        x_bias(0, 0, [0, 1])
-        x_turn((0, 1), 0)
-        x_bias(0, 1, [0, 1])
-        x_turn((0, 1), 1)
+        spread_dec_bias(1)
         turn(6)
+        w_out(3)
+        h_out_scaled(3, 0, 2)
+        dec_bias_out()
+        h_out_plain(4, 2)
         widen_plain(7, 0)
         widen_plain(7, 1)
-        x_out((0, 1))
+        quantise("a")
+        decode(0)
+        decode(1)
+        spread_map_bias(1)
         map_bias_out(1)
+        quantise("b")
+        decode(2)
+        decode(3)
+        batch("h46", h_keys(4, 6), "in_b")
+        h_scale_pool(4, 2)
         turn(7)
+        x_bias(0, 0, [0, 1])
+        x_bias(0, 1, [0, 1])
+        x_turn((0, 1), 0)
+        x_turn((0, 1), 1)
+        x_out((0, 1))
         spread_map_bias(0)
         map_bias_out(0)
-        h_out_scaled(5, 0, 2)
-        h_out_scaled(6, 0, 1)
-        x_quant((0, 1))
+        h_out_scaled(6, 0, 2)
+        batch("h7", h_keys(7))
+        h_out_scaled(7, 0, 1)
+        quantise("x01")
         time_map(0, 0)
         time_map(1, 0)
-        time_map(0, 1)
-        h_out_scaled(6, 1, 1)
-        h_quant(10, 2)
-        h_quant(8, 2)
         decode(5)
-        decode(4)
+        time_map(0, 1)
         time_map(1, 1)
-        h_out_scaled(7, 0, 1)
-        h_quant(12, 2)
-        time_map(0, 2)
-        decode(6)
         h_out_scaled(7, 1, 1)
-        h_quant(14, 1)
-        h_quant(15, 1)
+        quantise("h46")
+        decode(4)
+        decode(6)
+        quantise("h7")
         decode(7)
         x_bias(1, 0, [0, 1])
+        time_map(0, 2)
         time_map(1, 2)
         x_turn((2,), 0)
         x_turn((3,), 0)
@@ -354,8 +353,8 @@ def tile_model_pb_w8_kernel(tc, h_bytes, h_scale, dec_W, dec_b, map_W_words, map
         time_map(1, 3)
         x_out((2,))
         x_out((3,))
-        x_quant((2,))
-        x_quant((3,))
+        quantise("x2")
+        quantise("x3")
         time_map(2, 0)
         time_map(3, 0)
         time_map(2, 1)

@@ -72,15 +72,15 @@ def tile_model_pb_w8_kernel(tc, h_bytes, h_scale, dec_W, dec_b, map_W_words, map
         ones = sb([P, P], BF16, "ones")
         nc.gpsimd.memset(ones[:], 1.0)
 
-        load_w(0)
         load_h(0, [0])
+        load_w(0)
         load_h(1, [0, 1])
-        load_w(1)
-        nc.sync.dma_start(out=rows[0:1, 0 : MODELS * P], in_=dec_b.rearrange("(o n) p -> o (n p)", o=1))
-        nc.sync.dma_start(out=rows[0:1, MODELS * P :], in_=map_b.rearrange("(o s) -> o s", o=1))
         for k in (2, 3):
             load_h(k, [0, 1])
-            load_w(k)
+            load_w(k - 1)
+        load_w(3)
+        nc.sync.dma_start(out=rows[0:1, 0 : MODELS * P], in_=dec_b.rearrange("(o n) p -> o (n p)", o=1))
+        nc.sync.dma_start(out=rows[0:1, MODELS * P :], in_=map_b.rearrange("(o s) -> o s", o=1))
         load_h(0, [1])
         for q in range(4):
             nc.sync.dma_start(
@@ -127,12 +127,13 @@ def tile_model_pb_w8_kernel(tc, h_bytes, h_scale, dec_W, dec_b, map_W_words, map
         def map_bias_out(b):
             nc.scalar.copy(out=map_bias[:, 1024 * b : 1024 * (b + 1)], in_=bias_ps[b][:])
 
-        def widen_plain(unit, e):
-            hx[unit, e] = sb([P, D], BF16, "hx%d_%d" % (unit, e))
-            nc.scalar.copy(out=hx[unit, e][:], in_=hb[unit, e])
+        def widen(engine_copy, unit, models=(0, 1)):
+            for e in models:
+                hx[unit, e] = sb([P, D], BF16, "hx%d_%d" % (unit, e))
+                engine_copy(out=hx[unit, e][:], in_=hb[unit, e])
 
         def turn(unit, first=0, count=2):
-            b = (0, 1, 0, 1, 7, 7, 0, 1)[unit] if first == 0 else 2
+            b = (0, 1, 7, 0, 7, 1, 0, 1)[unit] if first == 0 else 2
             ht[unit, first] = bank(b, [P, 2, count * P], "ht%d_%d" % (unit, first))
             for e in range(count):
                 words = hx[unit, first + e][:].bitcast(F32)
@@ -259,89 +260,84 @@ def tile_model_pb_w8_kernel(tc, h_bytes, h_scale, dec_W, dec_b, map_W_words, map
         def w_keys(k):
             return [("w", k, e) for e in range(2)]
 
-        batch("w0", w_keys(0))
         batch("x01", [("x", 0), ("x", 1)])
         batch("x2", [("x", 2)])
         batch("x3", [("x", 3)])
 
-        w_group(nc.vector.tensor_copy, 0, 0, 2)
-        quantise("w0")
-        batch("a", h_keys(0, 1) + w_keys(1) + w_keys(2), "in_w0")
-        batch("b", h_keys(2, 3, 5) + w_keys(3))
-        w_group_pool(1)
-        widen_plain(0, 0)
-        widen_plain(0, 1)
+        batch("wh0", w_keys(0) + h_keys(0))
+        widen(nc.vector.tensor_copy, 0)
         turn(0, 0, 1)
         turn(0, 1, 1)
-        widen_plain(1, 0)
-        widen_plain(1, 1)
+        w_group(nc.vector.tensor_copy, 0, 0, 2)
+        batch("wh1", w_keys(1) + h_keys(1), "w_raw0")
+        batch("wh2", w_keys(2) + h_keys(2))
+        batch("wh3", w_keys(3) + h_keys(3))
+        w_group_pool(1)
+        w_group_pool(2)
+        widen(nc.scalar.copy, 1, [0])
+        widen(nc.vector.tensor_copy, 1, [1])
         turn(1)
-        widen_plain(5, 0)
-        widen_plain(5, 1)
-        turn(5)
-        widen_plain(2, 0)
-        widen_plain(2, 1)
-        h_out_plain(5, 2)
-        h_scale_pool(5, 2)
-        h_out_scaled(0, 0, 1)
+        widen(nc.scalar.copy, 2)
         turn(2)
-        spread_dec_bias(0)
+        h_out_scaled(0, 0, 1)
         h_out_scaled(0, 1, 1)
-        h_out_scaled(1, 0, 2)
-        widen_plain(3, 0)
-        widen_plain(3, 1)
+        widen(nc.scalar.copy, 3)
         turn(3)
         w_group_tensor(3)
-        w_group(nc.scalar.copy, 2, 0, 2)
-        widen_plain(4, 0)
-        widen_plain(4, 1)
-        turn(4)
-        h_out_scaled(2, 0, 2)
-        widen_plain(6, 0)
-        widen_plain(6, 1)
+        h_out_scaled(1, 0, 2)
+        widen(nc.scalar.copy, 5)
+        turn(5)
+        spread_dec_bias(0)
         spread_dec_bias(1)
-        turn(6)
+        h_out_scaled(2, 0, 2)
+        widen(nc.scalar.copy, 4)
         w_out(3)
-        h_out_scaled(3, 0, 2)
+        h_out_plain(5, 2)
         dec_bias_out()
-        h_out_plain(4, 2)
-        widen_plain(7, 0)
-        widen_plain(7, 1)
-        quantise("a")
+        h_out_scaled(3, 0, 2)
+        quantise("wh0")
+        quantise("wh1")
+        turn(4)
         decode(0)
         decode(1)
-        spread_map_bias(1)
-        map_bias_out(1)
-        quantise("b")
+        widen(nc.scalar.copy, 6)
+        quantise("wh2")
+        quantise("wh3")
         decode(2)
         decode(3)
-        batch("h46", h_keys(4, 6), "in_b")
-        h_scale_pool(4, 2)
-        turn(7)
+        batch("h45", h_keys(4, 5), "in_wh3")
+        h_scale_pool(5, 2)
+        widen(nc.scalar.copy, 7)
         x_bias(0, 0, [0, 1])
         x_bias(0, 1, [0, 1])
+        turn(6)
         x_turn((0, 1), 0)
         x_turn((0, 1), 1)
         x_out((0, 1))
+        turn(7)
+        spread_map_bias(1)
+        map_bias_out(1)
         spread_map_bias(0)
         map_bias_out(0)
-        h_out_scaled(6, 0, 2)
+        h_out_scaled(4, 0, 2)
+        batch("h6", h_keys(6))
         batch("h7", h_keys(7))
-        h_out_scaled(7, 0, 1)
+        h_out_scaled(6, 0, 2)
         quantise("x01")
+        quantise("h45")
         time_map(0, 0)
         time_map(1, 0)
+        decode(4)
         decode(5)
         time_map(0, 1)
         time_map(1, 1)
-        h_out_scaled(7, 1, 1)
-        quantise("h46")
-        decode(4)
-        decode(6)
+        time_map(0, 2)
+        h_out_scaled(7, 0, 2)
+        quantise("h6")
         quantise("h7")
+        decode(6)
         decode(7)
         x_bias(1, 0, [0, 1])
-        time_map(0, 2)
         time_map(1, 2)
         x_turn((2,), 0)
         x_turn((3,), 0)

@@ -82,11 +82,6 @@ def tile_model_pb_w8_kernel(tc, h_bytes, h_scale, dec_W, dec_b, map_W_words, map
         nc.sync.dma_start(out=rows[0:1, 0 : MODELS * P], in_=dec_b.rearrange("(o n) p -> o (n p)", o=1))
         nc.sync.dma_start(out=rows[0:1, MODELS * P :], in_=map_b.rearrange("(o s) -> o s", o=1))
         load_h(0, [1])
-        for q in range(4):
-            nc.sync.dma_start(
-                out=wsc[32 * q : 32 * q + 16, :].bitcast(I32),
-                in_=map_W_scales[:, 4 * q : 4 * q + 4, :].bitcast(I32),
-            )
         ww = {}
 
         def load_map_w(g, first, count):
@@ -96,8 +91,13 @@ def tile_model_pb_w8_kernel(tc, h_bytes, h_scale, dec_W, dec_b, map_W_words, map
             for s in range(count):
                 ww[g, first + s] = t[:, 512 * s : 512 * (s + 1)]
 
-        for g in (0, 1):
-            load_map_w(g, 0, 4)
+        load_map_w(0, 0, 4)
+        for q in range(4):
+            nc.sync.dma_start(
+                out=wsc[32 * q : 32 * q + 16, :].bitcast(I32),
+                in_=map_W_scales[:, 4 * q : 4 * q + 4, :].bitcast(I32),
+            )
+        load_map_w(1, 0, 4)
         for first in (0, 2):
             for g in (2, 3):
                 load_map_w(g, first, 2)

@@ -41,48 +41,19 @@ def tile_model_pb_w8_kernel(tc, h_bytes, h_scale, dec_W, dec_b, map_W_words, map
         def bank(i, shape, name, dtype=F32):
             return psum.tile(shape, dtype, name=name, tag="bank%d" % i)
 
-        scale_col = sb([P, 4], F32, "scale_col")
-        nc.sync.dma_start(out=scale_col[:], in_=h_scale.rearrange("a b c d (p j) -> p (a b c d j)", p=P))
-
         h_view = h_bytes.rearrange("n b c l d -> (b c) n l d")
-        hb = {}
-        w_raw = {}
+        hb, w_raw, ww = {}, {}, {}
 
-        def load_h(k, patches):
+        def load_h(unit):
+            l, k = divmod(unit, 4)
             n0 = FIRST_MODEL[k]
-            t = sb([P, 2, len(patches), D], U8, "hb%d_%d" % (k, patches[0]))
-            nc.sync.dma_start(out=t[:], in_=h_view[:, n0 : n0 + 2, patches[0] : patches[-1] + 1])
-            for a, l in enumerate(patches):
-                for e in range(2):
-                    hb[4 * l + k, e] = t[:, e, a].bitcast(FP8)
+            hb[unit] = sb([P, 2, D], U8, "hb%d" % unit)
+            nc.sync.dma_start(out=hb[unit][:], in_=h_view[:, n0 : n0 + 2, l])
 
         def load_w(k):
             n0 = FIRST_MODEL[k]
             w_raw[k] = sb([P, 2, 4, P], BF16, "w_raw%d" % k)
             nc.sync.dma_start(out=w_raw[k][:], in_=dec_W[n0 : n0 + 2].rearrange("n (p j) w -> p n j w", j=4))
-
-        ident = sb([P, P], F32, "ident")
-        make_identity(nc, ident[:])
-        rows = sb([P, T + MODELS * P], BF16, "rows")
-        nc.vector.memset(rows[:].bitcast(I32), 0)
-        wsc = sb([P, T], U8, "wsc")
-        nc.vector.memset(wsc[:].bitcast(I32), 0)
-        ident_bf = sb([P, P], BF16, "ident_bf")
-        nc.gpsimd.tensor_copy(out=ident_bf[:], in_=ident[:])
-        ones = sb([P, P], BF16, "ones")
-        nc.gpsimd.memset(ones[:], 1.0)
-
-        load_h(0, [0])
-        load_w(0)
-        load_h(1, [0, 1])
-        for k in (2, 3):
-            load_h(k, [0, 1])
-            load_w(k - 1)
-        load_w(3)
-        nc.sync.dma_start(out=rows[0:1, 0 : MODELS * P], in_=dec_b.rearrange("(o n) p -> o (n p)", o=1))
-        nc.sync.dma_start(out=rows[0:1, MODELS * P :], in_=map_b.rearrange("(o s) -> o s", o=1))
-        load_h(0, [1])
-        ww = {}
 
         def load_map_w(g, first, count):
             t = sb([P, 512 * count], I32, "ww%d_%d" % (g, first))
@@ -91,52 +62,63 @@ def tile_model_pb_w8_kernel(tc, h_bytes, h_scale, dec_W, dec_b, map_W_words, map
             for s in range(count):
                 ww[g, first + s] = t[:, 512 * s : 512 * (s + 1)]
 
-        load_map_w(0, 0, 4)
-        for q in range(4):
-            nc.sync.dma_start(
-                out=wsc[32 * q : 32 * q + 16, :].bitcast(I32),
-                in_=map_W_scales[:, 4 * q : 4 * q + 4, :].bitcast(I32),
-            )
-        load_map_w(1, 0, 4)
-        for first in (0, 2):
-            for g in (2, 3):
-                load_map_w(g, first, 2)
+        def load_map_scales():
+            for q in range(4):
+                nc.sync.dma_start(
+                    out=wsc[32 * q : 32 * q + 16, :].bitcast(I32),
+                    in_=map_W_scales[:, 4 * q : 4 * q + 4, :].bitcast(I32),
+                )
 
+        scale_col = sb([P, 4], F32, "scale_col")
+        ident = sb([P, P], F32, "ident")
+        ident_bf = sb([P, P], BF16, "ident_bf")
+        dec_rows = sb([P, P], BF16, "dec_rows")
+        dec_cols = sb([P, MODELS], BF16, "dec_cols")
+        map_cols = sb([P, T // P], BF16, "map_cols")
+        wsc = sb([P, T], U8, "wsc")
         dec_bias = sb([P, 2, P, 2, 2], BF16, "dec_bias")
         map_bias = sb([P, T], BF16, "map_bias")
 
         hx, ht, hw = {}, {}, {}
         batches, place, codes, scales = {}, {}, {}, {}
-        x_ps, xb, xt, acc, bias_ps = {}, {}, {}, {}, {}
+        x_ps, xb, xt, acc, side_ps = {}, {}, {}, {}, {}
 
-        def spread_dec_bias(u):
-            if u == 0:
-                bias_ps["dec"] = bank(4, [P, 2, 512], "dec_bias_ps", BF16)
-            by_u = rows[:, 0 : MODELS * P].rearrange("k (h u e p) -> k u p h e", h=2, u=2, e=2)
-            nc.tensor.matmul(bias_ps["dec"][:, u], ones[:], by_u[:, u], start=True, stop=True)
+        def turn_dec_rows(b):
+            side_ps["rows"] = bank(b, [P, P], "dec_rows_ps", BF16)
+            nc.tensor.transpose(side_ps["rows"][:], dec_rows[:], ident_bf[:])
+
+        def dec_cols_out():
+            nc.scalar.copy(out=dec_cols[:], in_=side_ps["rows"][:, 0:MODELS])
+
+        def spread(b, name, words):
+            side_ps[name] = bank(b, [P, 4, P], name)
+            for m in range(4):
+                nc.tensor.transpose(side_ps[name][:, m], words[:, m : m + 1].to_broadcast([P, P]), ident[:])
+
+        def spread_dec_bias(b):
+            spread(b, "dec_bias_ps", dec_cols[:].bitcast(F32))
 
         def dec_bias_out():
-            nc.scalar.copy(out=dec_bias[:].rearrange("b u p h e -> b (u p h e)"), in_=bias_ps["dec"][:].rearrange("b u c -> b (u c)"))
+            to = dec_bias[:].rearrange("b u p h e -> b (u p h e)").bitcast(F32).rearrange("b (u p h) -> b u p h", u=2, h=2)
+            nc.scalar.copy(out=to, in_=side_ps["dec_bias_ps"][:].rearrange("b (h u) p -> b u p h", u=2))
 
-        def spread_map_bias(b):
-            bias_ps[b] = bank((5, 6)[b], [P, 1024], "map_bias_ps%d" % b, BF16)
-            for c in range(2):
-                first = MODELS * P + 1024 * b + 512 * c
-                nc.tensor.matmul(bias_ps[b][:, 512 * c : 512 * (c + 1)], ones[:], rows[:, first : first + 512], start=True, stop=True)
+        def spread_map_bias(c, b):
+            spread(b, "map_bias_ps%d" % c, map_cols[:].bitcast(F32)[:, 4 * c : 4 * c + 4])
 
-        def map_bias_out(b):
-            nc.scalar.copy(out=map_bias[:, 1024 * b : 1024 * (b + 1)], in_=bias_ps[b][:])
+        def map_bias_out(c):
+            to = map_bias[:].bitcast(F32).rearrange("b (n c m) -> b n c m", c=2, m=4)[:, :, c]
+            nc.scalar.copy(out=to, in_=side_ps["map_bias_ps%d" % c][:].rearrange("b m n -> b n m"))
 
         def widen(engine_copy, unit, models=(0, 1)):
-            for e in models:
-                hx[unit, e] = sb([P, D], BF16, "hx%d_%d" % (unit, e))
-                engine_copy(out=hx[unit, e][:], in_=hb[unit, e])
+            t = sb([P, len(models), D], BF16, "hx%d_%d" % (unit, models[0]))
+            engine_copy(out=t[:], in_=hb[unit][:, models[0] : models[-1] + 1].bitcast(FP8))
+            for a, e in enumerate(models):
+                hx[unit, e] = t[:, a]
 
-        def turn(unit, first=0, count=2):
-            b = (0, 1, 7, 0, 7, 1, 0, 1)[unit] if first == 0 else 2
+        def turn(unit, b, first=0, count=2):
             ht[unit, first] = bank(b, [P, 2, count * P], "ht%d_%d" % (unit, first))
             for e in range(count):
-                words = hx[unit, first + e][:].bitcast(F32)
+                words = hx[unit, first + e].bitcast(F32)
                 for v in range(2):
                     nc.tensor.transpose(ht[unit, first][:, v, e * P : (e + 1) * P], words[:, v::2], ident[:])
 
@@ -159,42 +141,34 @@ def tile_model_pb_w8_kernel(tc, h_bytes, h_scale, dec_W, dec_b, map_W_words, map
                 codes[key] = words[:, m * P : (m + 1) * P].bitcast(FP8X4)
                 scales[key] = plane[:, m * P : (m + 1) * P]
 
-        def h_out_scaled(unit, first, count):
+        def h_out_scaled(unit, first=0, count=2):
             to = slots(("h", unit, first), count).rearrange("p (r v z) -> p r v z", v=2, z=2)
-            if (unit, first) in ht and ht[unit, first].shape[2] == count * P:
-                turned, rows_r = ht[unit, first], slice(0, count * P)
-            else:
-                turned, rows_r = ht[unit, 0], slice(first * P, (first + count) * P)
-            of = turned[:].rearrange("p v r -> p (v r)").bitcast(BF16).rearrange("p (v r z) -> p r v z", v=2, z=2)[:, rows_r]
+            of = ht[unit, first][:].rearrange("p v r -> p (v r)").bitcast(BF16).rearrange("p (v r z) -> p r v z", v=2, z=2)
             by = scale_col[:].rearrange("p (o v z) -> p o v z", o=1, v=2).to_broadcast([P, count * P, 2, 2])
             nc.vector.tensor_tensor(out=to, in0=of, in1=by, op=MULT)
 
-        def h_out_plain(unit, count):
-            hw[unit] = sb([P, count * P, 4], BF16, "hw%d" % unit)
+        def h_out_plain(unit):
+            hw[unit] = sb([P, 2 * P, 4], BF16, "hw%d" % unit)
             to = hw[unit][:].rearrange("p r t -> p (r t)").bitcast(F32).rearrange("p (r v) -> p r v", v=2)
-            nc.scalar.copy(out=to, in_=ht[unit, 0][:, :, 0 : count * P].rearrange("p v r -> p r v"))
+            nc.scalar.copy(out=to, in_=ht[unit, 0][:].rearrange("p v r -> p r v"))
 
-        def h_scale_pool(unit, count):
-            by = scale_col[:].rearrange("p (o t) -> p o t", o=1).to_broadcast([P, count * P, 4])
-            nc.gpsimd.tensor_tensor(out=slots(("h", unit, 0), count).rearrange("p (r t) -> p r t", t=4), in0=hw[unit][:], in1=by, op=MULT)
+        def h_scale_pool(unit):
+            by = scale_col[:].rearrange("p (o t) -> p o t", o=1).to_broadcast([P, 2 * P, 4])
+            nc.gpsimd.tensor_tensor(out=slots(("h", unit, 0), 2).rearrange("p (r t) -> p r t", t=4), in0=hw[unit][:], in1=by, op=MULT)
 
-        def w_group(engine_copy, k, first, count):
-            to = slots(("w", k, first), count).rearrange("p (e c i t) -> p e c t i", e=count, i=4, t=4)
-            of = w_raw[k][:, first : first + count].rearrange("p e t (c i) -> p e c t i", i=4)
-            engine_copy(out=to, in_=of)
+        def w_group(k, b, models=(0, 1)):
+            for e in models:
+                if ("w", k) not in side_ps:
+                    side_ps["w", k] = bank(b, [P, 2, 512], "w_ps%d" % k, BF16)
+                nc.tensor.matmul(side_ps["w", k][:, e], ident_bf[:], w_raw[k][:, e].rearrange("p t c -> p c t"), start=True, stop=True)
+
+        def w_out(k, first=0):
+            nc.scalar.copy(out=slots(("w", k, first), 2 - first), in_=side_ps["w", k][:, first:].rearrange("p e x -> p (e x)"))
 
         def w_group_pool(k):
-            to = slots(("w", k, 0), 2).rearrange("p (e c t) -> p e c t", e=2, t=4)
-            of = w_raw[k][:].rearrange("p e t c -> p e c t")
-            nc.gpsimd.tensor_scalar(out=to, in0=of, scalar1=1.0, scalar2=0.0, op0=MULT, op1=ADD)
+            to = slots(("w", k, 0), 1).rearrange("p (c t) -> p c t", t=4)
+            nc.gpsimd.tensor_scalar(out=to, in0=w_raw[k][:, 0].rearrange("p t c -> p c t"), scalar1=1.0, scalar2=0.0, op0=MULT, op1=ADD)
 
-        def w_group_tensor(k):
-            bias_ps["w", k] = bank(5, [P, 2, 512], "w_ps%d" % k, BF16)
-            for e in range(2):
-                nc.tensor.matmul(bias_ps["w", k][:, e], ident_bf[:], w_raw[k][:, e].rearrange("p t c -> p c t"), start=True, stop=True)
-
-        def w_out(k):
-            nc.scalar.copy(out=slots(("w", k, 0), 2), in_=bias_ps["w", k][:].rearrange("p e x -> p (e x)"))
 
         def decode(unit):
             l, k = divmod(unit, 4)
@@ -221,9 +195,9 @@ def tile_model_pb_w8_kernel(tc, h_bytes, h_scale, dec_W, dec_b, map_W_words, map
             for a, half in enumerate(halves):
                 xb[2 * l + half, u] = t[:, a * HALF : (a + 1) * HALF].rearrange("b p h e -> b (p h e)").bitcast(F32)
 
-        def x_turn(groups, u):
+        def x_turn(groups, u, b):
             if u == 0:
-                xt[groups] = bank((4, 4, 0, 1)[groups[0]], [P, len(groups), 2, P], "xt%d" % groups[0])
+                xt[groups] = bank(b, [P, len(groups), 2, P], "xt%d" % groups[0])
             for a, g in enumerate(groups):
                 nc.tensor.transpose(xt[groups][:, a, u], xb[g, u], ident[:])
 
@@ -233,7 +207,7 @@ def tile_model_pb_w8_kernel(tc, h_bytes, h_scale, dec_W, dec_b, map_W_words, map
 
         def time_map(g, s):
             if g == 0:
-                acc[s] = bank((4, 7, 6, 5)[s], [P, 512], "acc%d" % s)
+                acc[s] = bank(4 + s, [P, 512], "acc%d" % s)
             cols = slice(512 * s, 512 * (s + 1))
             nc.tensor.matmul_mx(
                 out=acc[s][:],
@@ -260,106 +234,129 @@ def tile_model_pb_w8_kernel(tc, h_bytes, h_scale, dec_W, dec_b, map_W_words, map
         def w_keys(k):
             return [("w", k, e) for e in range(2)]
 
+        nc.vector.memset(ident[:], 0.0)
+        make_identity(nc, ident[:], nomemset=True)
+        nc.vector.memset(dec_rows[:].bitcast(I32), 0)
+        nc.vector.memset(wsc[:].bitcast(I32), 0)
+        nc.vector.tensor_copy(out=ident_bf[:], in_=ident[:])
+
+        load_h(0)
+        nc.sync.dma_start(out=scale_col[:], in_=h_scale.rearrange("a b c d (p j) -> p (a b c d j)", p=P))
+        load_h(1)
+        load_h(2)
+        load_h(3)
+        load_w(0)
+        load_h(4)
+        load_w(1)
+        load_h(6)
+        nc.sync.dma_start(out=dec_rows[0:MODELS, :], in_=dec_b)
+        load_w(2)
+        load_w(3)
+        load_h(5)
+        load_h(7)
+        nc.sync.dma_start(out=map_cols[:], in_=map_b.rearrange("(n m) -> n m", n=P))
+        load_map_w(0, 0, 4)
+        load_map_scales()
+        load_map_w(1, 0, 4)
+        for first in (0, 2):
+            for g in (2, 3):
+                load_map_w(g, first, 2)
+
+        batch("wh01", w_keys(0) + h_keys(0) + w_keys(1) + h_keys(1))
+        batch("wh23", w_keys(2) + h_keys(2) + w_keys(3) + h_keys(3))
+        batch("h45", h_keys(4, 5))
         batch("x01", [("x", 0), ("x", 1)])
+        batch("h7", h_keys(7))
         batch("x2", [("x", 2)])
         batch("x3", [("x", 3)])
 
-        batch("wh0", w_keys(0) + h_keys(0))
-        widen(nc.vector.tensor_copy, 0)
-        turn(0, 0, 1)
-        turn(0, 1, 1)
-        w_group(nc.vector.tensor_copy, 0, 0, 2)
-        batch("wh1", w_keys(1) + h_keys(1), "w_raw0")
-        batch("wh2", w_keys(2) + h_keys(2))
-        batch("wh3", w_keys(3) + h_keys(3))
-        w_group_pool(1)
-        w_group_pool(2)
-        widen(nc.scalar.copy, 1, [0])
-        widen(nc.vector.tensor_copy, 1, [1])
-        turn(1)
+        widen(nc.vector.tensor_copy, 0, [0])
+        widen(nc.scalar.copy, 0, [1])
+        turn(0, 0, 0, 1)
+        turn(0, 1, 1, 1)
+        widen(nc.vector.tensor_copy, 1)
         widen(nc.scalar.copy, 2)
-        turn(2)
+        widen(nc.scalar.copy, 3)
+        turn(1, 4)
+        turn(2, 5)
         h_out_scaled(0, 0, 1)
         h_out_scaled(0, 1, 1)
-        widen(nc.scalar.copy, 3)
-        turn(3)
-        w_group_tensor(3)
-        h_out_scaled(1, 0, 2)
-        widen(nc.scalar.copy, 5)
-        turn(5)
-        spread_dec_bias(0)
-        spread_dec_bias(1)
-        h_out_scaled(2, 0, 2)
+        h_out_plain(1)
+        w_group_pool(0)
+        h_scale_pool(1)
+        w_group(0, 6, [1])
+        turn(3, 0)
+        h_out_scaled(2)
         widen(nc.scalar.copy, 4)
+        w_group(1, 7)
+        w_out(0, 1)
+        w_out(1)
+        turn(4, 1)
+        widen(nc.scalar.copy, 6)
+        h_out_scaled(3)
+        w_group(2, 6)
+        turn_dec_rows(4)
+        w_group(3, 7)
+        turn(6, 5)
+        h_out_scaled(4)
+        w_out(2)
         w_out(3)
-        h_out_plain(5, 2)
+        spread_map_bias(0, 6)
+        dec_cols_out()
+        widen(nc.scalar.copy, 5)
+        h_out_plain(6)
+        spread_dec_bias(4)
+        spread_map_bias(1, 7)
+        turn(5, 0)
         dec_bias_out()
-        h_out_scaled(3, 0, 2)
-        quantise("wh0")
-        quantise("wh1")
-        turn(4)
+        widen(nc.scalar.copy, 7)
+        map_bias_out(0)
+        map_bias_out(1)
+        quantise("wh01")
+        quantise("wh23")
+        batch("h6", h_keys(6), "in_wh23")
+        h_scale_pool(6)
         decode(0)
         decode(1)
-        widen(nc.scalar.copy, 6)
-        quantise("wh2")
-        quantise("wh3")
         decode(2)
         decode(3)
-        batch("h45", h_keys(4, 5), "in_wh3")
-        h_scale_pool(5, 2)
-        widen(nc.scalar.copy, 7)
+        h_out_scaled(5)
         x_bias(0, 0, [0, 1])
         x_bias(0, 1, [0, 1])
-        turn(6)
-        x_turn((0, 1), 0)
-        x_turn((0, 1), 1)
+        turn(7, 1)
+        x_turn((0, 1), 0, 4)
+        x_turn((0, 1), 1, 4)
         x_out((0, 1))
-        turn(7)
-        spread_map_bias(1)
-        map_bias_out(1)
-        spread_map_bias(0)
-        map_bias_out(0)
-        h_out_scaled(4, 0, 2)
-        batch("h6", h_keys(6))
-        batch("h7", h_keys(7))
-        h_out_scaled(6, 0, 2)
+        h_out_scaled(7)
         quantise("x01")
         quantise("h45")
+        quantise("h6")
+        quantise("h7")
         time_map(0, 0)
         time_map(1, 0)
         decode(4)
         decode(5)
-        time_map(0, 1)
-        time_map(1, 1)
-        time_map(0, 2)
-        h_out_scaled(7, 0, 2)
-        quantise("h6")
-        quantise("h7")
         decode(6)
         decode(7)
         x_bias(1, 0, [0, 1])
-        time_map(1, 2)
-        x_turn((2,), 0)
-        x_turn((3,), 0)
+        time_map(0, 1)
+        time_map(1, 1)
+        x_turn((2,), 0, 0)
+        x_turn((3,), 0, 1)
         x_bias(1, 1, [0])
         x_bias(1, 1, [1])
-        x_turn((2,), 1)
-        x_turn((3,), 1)
+        x_turn((2,), 1, 0)
+        x_turn((3,), 1, 1)
+        time_map(0, 2)
+        time_map(1, 2)
         time_map(0, 3)
-        time_map(1, 3)
         x_out((2,))
         x_out((3,))
         quantise("x2")
         quantise("x3")
-        time_map(2, 0)
-        time_map(3, 0)
-        time_map(2, 1)
-        time_map(3, 1)
-        finish(0, 1)
-        finish(1, 1)
-        time_map(2, 2)
-        time_map(3, 2)
-        finish(2, 1)
-        time_map(2, 3)
-        time_map(3, 3)
-        finish(3, 2)
+        for s in range(4):
+            if s == 3:
+                time_map(1, 3)
+            time_map(2, s)
+            time_map(3, s)
+            finish(s, 2 if s == 3 else 1)

@@ -74,7 +74,8 @@ def tile_model_pb_w8_kernel(tc, h_bytes, h_scale, dec_W, dec_b, map_W_words, map
         ident_bf = sb([P, P], BF16, "ident_bf")
         dec_rows = sb([P, P], BF16, "dec_rows")
         dec_cols = sb([P, MODELS], BF16, "dec_cols")
-        map_cols = sb([P, T // P], BF16, "map_cols")
+        map_row = sb([P, T], BF16, "map_row")
+        ones = sb([P, P], BF16, "ones")
         wsc = sb([P, T], U8, "wsc")
         dec_bias = sb([P, 2, P, 2, 2], BF16, "dec_bias")
         map_bias = sb([P, T], BF16, "map_bias")
@@ -103,11 +104,13 @@ def tile_model_pb_w8_kernel(tc, h_bytes, h_scale, dec_W, dec_b, map_W_words, map
             nc.scalar.copy(out=to, in_=side_ps["dec_bias_ps"][:].rearrange("b (h u) p -> b u p h", u=2))
 
         def spread_map_bias(c, b):
-            spread(b, "map_bias_ps%d" % c, map_cols[:].bitcast(F32)[:, 4 * c : 4 * c + 4])
+            side_ps["map", c] = bank(b, [P, 1024], "map_bias_ps%d" % c, BF16)
+            for a in range(2):
+                first = 1024 * c + 512 * a
+                nc.tensor.matmul(side_ps["map", c][:, 512 * a : 512 * (a + 1)], ones[:], map_row[:, first : first + 512], start=True, stop=True)
 
         def map_bias_out(c):
-            to = map_bias[:].bitcast(F32).rearrange("b (n c m) -> b n c m", c=2, m=4)[:, :, c]
-            nc.scalar.copy(out=to, in_=side_ps["map_bias_ps%d" % c][:].rearrange("b m n -> b n m"))
+            nc.scalar.copy(out=map_bias[:, 1024 * c : 1024 * (c + 1)], in_=side_ps["map", c][:])
 
         def widen(engine_copy, unit, models=(0, 1)):
             t = sb([P, len(models), D], BF16, "hx%d_%d" % (unit, models[0]))
@@ -166,8 +169,8 @@ def tile_model_pb_w8_kernel(tc, h_bytes, h_scale, dec_W, dec_b, map_W_words, map
             nc.scalar.copy(out=slots(("w", k, first), 2 - first), in_=side_ps["w", k][:, first:].rearrange("p e x -> p (e x)"))
 
         def w_group_pool(k):
-            to = slots(("w", k, 0), 1).rearrange("p (c t) -> p c t", t=4)
-            nc.gpsimd.tensor_scalar(out=to, in0=w_raw[k][:, 0].rearrange("p t c -> p c t"), scalar1=1.0, scalar2=0.0, op0=MULT, op1=ADD)
+            to = slots(("w", k, 0), 2).rearrange("p (e c t) -> p e c t", e=2, t=4)
+            nc.gpsimd.tensor_scalar(out=to, in0=w_raw[k][:].rearrange("p e t c -> p e c t"), scalar1=1.0, scalar2=0.0, op0=MULT, op1=ADD)
 
 
         def decode(unit):
@@ -236,25 +239,27 @@ def tile_model_pb_w8_kernel(tc, h_bytes, h_scale, dec_W, dec_b, map_W_words, map
 
         nc.vector.memset(ident[:], 0.0)
         make_identity(nc, ident[:], nomemset=True)
+        nc.vector.memset(ones[:], 1.0)
         nc.vector.memset(dec_rows[:].bitcast(I32), 0)
         nc.vector.memset(wsc[:].bitcast(I32), 0)
+        nc.vector.memset(map_row[:].bitcast(I32), 0)
         nc.vector.tensor_copy(out=ident_bf[:], in_=ident[:])
 
         load_h(0)
-        nc.sync.dma_start(out=scale_col[:], in_=h_scale.rearrange("a b c d (p j) -> p (a b c d j)", p=P))
         load_h(1)
+        nc.sync.dma_start(out=scale_col[:], in_=h_scale.rearrange("a b c d (p j) -> p (a b c d j)", p=P))
         load_h(2)
-        load_h(3)
         load_w(0)
-        load_h(4)
+        load_h(3)
         load_w(1)
-        load_h(6)
-        nc.sync.dma_start(out=dec_rows[0:MODELS, :], in_=dec_b)
+        load_h(4)
         load_w(2)
-        load_w(3)
         load_h(5)
+        nc.sync.dma_start(out=dec_rows[0:MODELS, :], in_=dec_b)
+        load_w(3)
+        load_h(6)
         load_h(7)
-        nc.sync.dma_start(out=map_cols[:], in_=map_b.rearrange("(n m) -> n m", n=P))
+        nc.sync.dma_start(out=map_row[0:1, :], in_=map_b.rearrange("(o s) -> o s", o=1))
         load_map_w(0, 0, 4)
         load_map_scales()
         load_map_w(1, 0, 4)
@@ -264,9 +269,9 @@ def tile_model_pb_w8_kernel(tc, h_bytes, h_scale, dec_W, dec_b, map_W_words, map
 
         batch("wh01", w_keys(0) + h_keys(0) + w_keys(1) + h_keys(1))
         batch("wh23", w_keys(2) + h_keys(2) + w_keys(3) + h_keys(3))
-        batch("h45", h_keys(4, 5))
-        batch("x01", [("x", 0), ("x", 1)])
+        batch("h6", h_keys(6))
         batch("h7", h_keys(7))
+        batch("x01", [("x", 0), ("x", 1)])
         batch("x2", [("x", 2)])
         batch("x3", [("x", 3)])
 
@@ -278,85 +283,80 @@ def tile_model_pb_w8_kernel(tc, h_bytes, h_scale, dec_W, dec_b, map_W_words, map
         widen(nc.scalar.copy, 2)
         widen(nc.scalar.copy, 3)
         turn(1, 4)
-        turn(2, 5)
+        w_group_pool(0)
+        w_group_pool(1)
         h_out_scaled(0, 0, 1)
         h_out_scaled(0, 1, 1)
-        h_out_plain(1)
-        w_group_pool(0)
-        h_scale_pool(1)
-        w_group(0, 6, [1])
+        turn(2, 5)
+        h_out_scaled(1)
+        widen(nc.scalar.copy, 4)
         turn(3, 0)
         h_out_scaled(2)
-        widen(nc.scalar.copy, 4)
-        w_group(1, 7)
-        w_out(0, 1)
-        w_out(1)
-        turn(4, 1)
-        widen(nc.scalar.copy, 6)
-        h_out_scaled(3)
-        w_group(2, 6)
-        turn_dec_rows(4)
-        w_group(3, 7)
-        turn(6, 5)
-        h_out_scaled(4)
-        w_out(2)
-        w_out(3)
-        spread_map_bias(0, 6)
-        dec_cols_out()
         widen(nc.scalar.copy, 5)
-        h_out_plain(6)
+        w_group(2, 6)
+        w_group(3, 7)
+        turn_dec_rows(4)
+        turn(5, 5)
+        h_out_scaled(3)
+        w_out(2)
+        turn(4, 1)
+        w_out(3)
+        dec_cols_out()
+        h_out_plain(5)
         spread_dec_bias(4)
-        spread_map_bias(1, 7)
-        turn(5, 0)
         dec_bias_out()
+        widen(nc.scalar.copy, 6)
         widen(nc.scalar.copy, 7)
-        map_bias_out(0)
-        map_bias_out(1)
         quantise("wh01")
         quantise("wh23")
-        batch("h6", h_keys(6), "in_wh23")
-        h_scale_pool(6)
+        batch("h45", h_keys(4, 5), "in_wh23")
+        h_scale_pool(5)
         decode(0)
         decode(1)
         decode(2)
         decode(3)
-        h_out_scaled(5)
+        spread_map_bias(0, 6)
+        h_out_scaled(4)
         x_bias(0, 0, [0, 1])
         x_bias(0, 1, [0, 1])
-        turn(7, 1)
+        turn(6, 0)
         x_turn((0, 1), 0, 4)
         x_turn((0, 1), 1, 4)
+        turn(7, 1)
         x_out((0, 1))
-        h_out_scaled(7)
-        quantise("x01")
+        spread_map_bias(1, 7)
+        map_bias_out(0)
+        map_bias_out(1)
+        h_out_scaled(6)
         quantise("h45")
-        quantise("h6")
-        quantise("h7")
-        time_map(0, 0)
-        time_map(1, 0)
+        quantise("x01")
         decode(4)
         decode(5)
+        time_map(0, 0)
+        time_map(1, 0)
+        time_map(0, 1)
+        time_map(1, 1)
+        h_out_scaled(7)
+        quantise("h6")
+        quantise("h7")
+        time_map(0, 2)
         decode(6)
         decode(7)
         x_bias(1, 0, [0, 1])
-        time_map(0, 1)
-        time_map(1, 1)
+        time_map(1, 2)
         x_turn((2,), 0, 0)
         x_turn((3,), 0, 1)
         x_bias(1, 1, [0])
         x_bias(1, 1, [1])
         x_turn((2,), 1, 0)
         x_turn((3,), 1, 1)
-        time_map(0, 2)
-        time_map(1, 2)
         time_map(0, 3)
+        time_map(1, 3)
         x_out((2,))
         x_out((3,))
         quantise("x2")
         quantise("x3")
         for s in range(4):
-            if s == 3:
-                time_map(1, 3)
             time_map(2, s)
             time_map(3, s)
             finish(s, 2 if s == 3 else 1)

@@ -44,11 +44,13 @@ def tile_model_pb_w8_kernel(tc, h_bytes, h_scale, dec_W, dec_b, map_W_words, map
         h_view = h_bytes.rearrange("n b c l d -> (b c) n l d")
         hb, w_raw, ww = {}, {}, {}
 
-        def load_h(unit):
-            l, k = divmod(unit, 4)
-            n0 = FIRST_MODEL[k]
-            hb[unit] = sb([P, 2, D], U8, "hb%d" % unit)
-            nc.sync.dma_start(out=hb[unit][:], in_=h_view[:, n0 : n0 + 2, l])
+        def load_h(k, models=(0, 1)):
+            n0 = FIRST_MODEL[k] + models[0]
+            t = sb([P, len(models), PATCHES, D], U8, "hb%d_%d" % (k, models[0]))
+            nc.sync.dma_start(out=t[:], in_=h_view[:, n0 : n0 + len(models)])
+            for a, e in enumerate(models):
+                for l in range(PATCHES):
+                    hb[4 * l + k, e] = t[:, a, l].bitcast(FP8)
 
         def load_w(k):
             n0 = FIRST_MODEL[k]
@@ -113,10 +115,10 @@ def tile_model_pb_w8_kernel(tc, h_bytes, h_scale, dec_W, dec_b, map_W_words, map
             nc.scalar.copy(out=map_bias[:, 1024 * c : 1024 * (c + 1)], in_=side_ps["map", c][:])
 
         def widen(engine_copy, unit, models=(0, 1)):
-            t = sb([P, len(models), D], BF16, "hx%d_%d" % (unit, models[0]))
-            engine_copy(out=t[:], in_=hb[unit][:, models[0] : models[-1] + 1].bitcast(FP8))
-            for a, e in enumerate(models):
-                hx[unit, e] = t[:, a]
+            for e in models:
+                t = sb([P, D], BF16, "hx%d_%d" % (unit, e))
+                engine_copy(out=t[:], in_=hb[unit, e])
+                hx[unit, e] = t[:]
 
         def turn(unit, b, first=0, count=2):
             ht[unit, first] = bank(b, [P, 2, count * P], "ht%d_%d" % (unit, first))
@@ -245,20 +247,17 @@ def tile_model_pb_w8_kernel(tc, h_bytes, h_scale, dec_W, dec_b, map_W_words, map
         nc.vector.memset(map_row[:].bitcast(I32), 0)
         nc.vector.tensor_copy(out=ident_bf[:], in_=ident[:])
 
-        load_h(0)
-        load_h(1)
+        load_h(0, [0])
+        load_h(0, [1])
         nc.sync.dma_start(out=scale_col[:], in_=h_scale.rearrange("a b c d (p j) -> p (a b c d j)", p=P))
+        load_h(1)
         load_h(2)
         load_w(0)
         load_h(3)
         load_w(1)
-        load_h(4)
-        load_w(2)
-        load_h(5)
         nc.sync.dma_start(out=dec_rows[0:MODELS, :], in_=dec_b)
+        load_w(2)
         load_w(3)
-        load_h(6)
-        load_h(7)
         nc.sync.dma_start(out=map_row[0:1, :], in_=map_b.rearrange("(o s) -> o s", o=1))
         load_map_w(0, 0, 4)
         load_map_scales()
@@ -269,7 +268,7 @@ def tile_model_pb_w8_kernel(tc, h_bytes, h_scale, dec_W, dec_b, map_W_words, map
 
         batch("wh01", w_keys(0) + h_keys(0) + w_keys(1) + h_keys(1))
         batch("wh23", w_keys(2) + h_keys(2) + w_keys(3) + h_keys(3))
-        batch("h6", h_keys(6))
+        batch("h4", h_keys(4))
         batch("h7", h_keys(7))
         batch("x01", [("x", 0), ("x", 1)])
         batch("x2", [("x", 2)])
@@ -279,84 +278,86 @@ def tile_model_pb_w8_kernel(tc, h_bytes, h_scale, dec_W, dec_b, map_W_words, map
         widen(nc.scalar.copy, 0, [1])
         turn(0, 0, 0, 1)
         turn(0, 1, 1, 1)
-        widen(nc.vector.tensor_copy, 1)
-        widen(nc.scalar.copy, 2)
-        widen(nc.scalar.copy, 3)
-        turn(1, 4)
-        w_group_pool(0)
-        w_group_pool(1)
+        widen(nc.vector.tensor_copy, 4, [0])
+        widen(nc.scalar.copy, 4, [1])
+        turn(4, 4)
+        widen(nc.scalar.copy, 1)
+        turn(1, 5)
         h_out_scaled(0, 0, 1)
         h_out_scaled(0, 1, 1)
-        turn(2, 5)
+        widen(nc.scalar.copy, 2)
+        w_group_pool(0)
+        w_group_pool(1)
+        turn(2, 0)
+        h_out_scaled(4)
+        widen(nc.scalar.copy, 3)
+        turn(3, 1)
         h_out_scaled(1)
-        widen(nc.scalar.copy, 4)
-        turn(3, 0)
-        h_out_scaled(2)
         widen(nc.scalar.copy, 5)
-        w_group(2, 6)
-        w_group(3, 7)
-        turn_dec_rows(4)
-        turn(5, 5)
-        h_out_scaled(3)
-        w_out(2)
-        turn(4, 1)
-        w_out(3)
-        dec_cols_out()
-        h_out_plain(5)
-        spread_dec_bias(4)
-        dec_bias_out()
         widen(nc.scalar.copy, 6)
         widen(nc.scalar.copy, 7)
+        turn_dec_rows(4)
+        w_group(2, 6)
+        dec_cols_out()
+        h_out_scaled(2)
+        w_group(3, 7)
+        turn(6, 5)
+        spread_dec_bias(4)
+        turn(5, 0)
+        h_out_scaled(3)
+        w_out(2)
+        w_out(3)
+        h_out_plain(6)
+        dec_bias_out()
         quantise("wh01")
+        quantise("h4")
         quantise("wh23")
-        batch("h45", h_keys(4, 5), "in_wh23")
-        h_scale_pool(5)
+        batch("h56", h_keys(5, 6), "in_wh23")
+        h_scale_pool(6)
         decode(0)
         decode(1)
+        turn(7, 1)
         decode(2)
         decode(3)
         spread_map_bias(0, 6)
-        h_out_scaled(4)
+        map_bias_out(0)
+        h_out_scaled(5)
         x_bias(0, 0, [0, 1])
         x_bias(0, 1, [0, 1])
-        turn(6, 0)
         x_turn((0, 1), 0, 4)
         x_turn((0, 1), 1, 4)
-        turn(7, 1)
         x_out((0, 1))
-        spread_map_bias(1, 7)
-        map_bias_out(0)
-        map_bias_out(1)
-        h_out_scaled(6)
-        quantise("h45")
-        quantise("x01")
         decode(4)
-        decode(5)
-        time_map(0, 0)
-        time_map(1, 0)
-        time_map(0, 1)
-        time_map(1, 1)
+        spread_map_bias(1, 7)
+        map_bias_out(1)
         h_out_scaled(7)
-        quantise("h6")
+        quantise("h56")
         quantise("h7")
-        time_map(0, 2)
+        quantise("x01")
+        decode(5)
         decode(6)
         decode(7)
         x_bias(1, 0, [0, 1])
-        time_map(1, 2)
+        time_map(0, 0)
+        time_map(1, 0)
         x_turn((2,), 0, 0)
         x_turn((3,), 0, 1)
         x_bias(1, 1, [0])
         x_bias(1, 1, [1])
         x_turn((2,), 1, 0)
         x_turn((3,), 1, 1)
-        time_map(0, 3)
-        time_map(1, 3)
+        time_map(0, 1)
+        time_map(1, 1)
+        time_map(0, 2)
+        time_map(1, 2)
         x_out((2,))
         x_out((3,))
         quantise("x2")
         quantise("x3")
         for s in range(4):
+            if s == 3:
+                time_map(0, 3)
+                time_map(1, 3)
             time_map(2, s)
             time_map(3, s)
-            finish(s, 2 if s == 3 else 1)
+            finish(s, 2 if s in (0, 3) else 1)

@@ -64,9 +64,9 @@ def tile_model_pb_w8_kernel(tc, h_bytes, h_scale, dec_W, dec_b, map_W_words, map
             for s in range(count):
                 ww[g, first + s] = t[:, 512 * s : 512 * (s + 1)]
 
-        def load_map_scales():
-            for q in range(4):
-                nc.sync.dma_start(
+        def load_map_scales(queue, quadrants):
+            for q in quadrants:
+                queue.dma_start(
                     out=wsc[32 * q : 32 * q + 16, :].bitcast(I32),
                     in_=map_W_scales[:, 4 * q : 4 * q + 4, :].bitcast(I32),
                 )
@@ -152,14 +152,15 @@ def tile_model_pb_w8_kernel(tc, h_bytes, h_scale, dec_W, dec_b, map_W_words, map
             by = scale_col[:].rearrange("p (o v z) -> p o v z", o=1, v=2).to_broadcast([P, count * P, 2, 2])
             nc.vector.tensor_tensor(out=to, in0=of, in1=by, op=MULT)
 
-        def h_out_plain(unit):
-            hw[unit] = sb([P, 2 * P, 4], BF16, "hw%d" % unit)
-            to = hw[unit][:].rearrange("p r t -> p (r t)").bitcast(F32).rearrange("p (r v) -> p r v", v=2)
-            nc.scalar.copy(out=to, in_=ht[unit, 0][:].rearrange("p v r -> p r v"))
+        def h_out_planes(unit):
+            hw[unit] = sb([P, 4, 2 * P], BF16, "hw%d" % unit)
+            of = ht[unit, 0][:].rearrange("p v r -> p (v r)").bitcast(BF16).rearrange("p (v r z) -> p v z r", v=2, z=2)
+            for t in range(4):
+                nc.scalar.activation(out=hw[unit][:, t], in_=of[:, t // 2, t % 2], func=COPY, scale=scale_col[:, t : t + 1])
 
-        def h_scale_pool(unit):
-            by = scale_col[:].rearrange("p (o t) -> p o t", o=1).to_broadcast([P, 2 * P, 4])
-            nc.gpsimd.tensor_tensor(out=slots(("h", unit, 0), 2).rearrange("p (r t) -> p r t", t=4), in0=hw[unit][:], in1=by, op=MULT)
+        def h_group_pool(unit):
+            to = slots(("h", unit, 0), 2).rearrange("p (r t) -> p r t", t=4)
+            nc.gpsimd.tensor_scalar(out=to, in0=hw[unit][:].rearrange("p t r -> p r t"), scalar1=1.0, scalar2=0.0, op0=MULT, op1=ADD)
 
         def w_group(k, b, models=(0, 1)):
             for e in models:
@@ -240,10 +241,10 @@ def tile_model_pb_w8_kernel(tc, h_bytes, h_scale, dec_W, dec_b, map_W_words, map
             return [("w", k, e) for e in range(2)]
 
         nc.vector.memset(ident[:], 0.0)
+        nc.vector.memset(wsc[:].bitcast(I32), 0)
         make_identity(nc, ident[:], nomemset=True)
         nc.vector.memset(ones[:], 1.0)
         nc.vector.memset(dec_rows[:].bitcast(I32), 0)
-        nc.vector.memset(wsc[:].bitcast(I32), 0)
         nc.vector.memset(map_row[:].bitcast(I32), 0)
         nc.vector.tensor_copy(out=ident_bf[:], in_=ident[:])
 
@@ -260,11 +261,13 @@ def tile_model_pb_w8_kernel(tc, h_bytes, h_scale, dec_W, dec_b, map_W_words, map
         load_w(3)
         nc.sync.dma_start(out=map_row[0:1, :], in_=map_b.rearrange("(o s) -> o s", o=1))
         load_map_w(0, 0, 4)
-        load_map_scales()
+        load_map_scales(nc.sync, range(4))
         load_map_w(1, 0, 4)
-        for first in (0, 2):
-            for g in (2, 3):
-                load_map_w(g, first, 2)
+        load_map_w(2, 0, 2)
+        load_map_w(3, 0, 2)
+        load_map_w(2, 2, 2)
+        load_map_w(3, 2, 1)
+        load_map_w(3, 3, 1)
 
         batch("wh01", w_keys(0) + h_keys(0) + w_keys(1) + h_keys(1))
         batch("wh23", w_keys(2) + h_keys(2) + w_keys(3) + h_keys(3))
@@ -278,8 +281,7 @@ def tile_model_pb_w8_kernel(tc, h_bytes, h_scale, dec_W, dec_b, map_W_words, map
         widen(nc.scalar.copy, 0, [1])
         turn(0, 0, 0, 1)
         turn(0, 1, 1, 1)
-        widen(nc.vector.tensor_copy, 4, [0])
-        widen(nc.scalar.copy, 4, [1])
+        widen(nc.vector.tensor_copy, 4)
         turn(4, 4)
         widen(nc.scalar.copy, 1)
         turn(1, 5)
@@ -293,9 +295,8 @@ def tile_model_pb_w8_kernel(tc, h_bytes, h_scale, dec_W, dec_b, map_W_words, map
         widen(nc.scalar.copy, 3)
         turn(3, 1)
         h_out_scaled(1)
-        widen(nc.scalar.copy, 5)
         widen(nc.scalar.copy, 6)
-        widen(nc.scalar.copy, 7)
+        widen(nc.scalar.copy, 5)
         turn_dec_rows(4)
         w_group(2, 6)
         dec_cols_out()
@@ -307,25 +308,26 @@ def tile_model_pb_w8_kernel(tc, h_bytes, h_scale, dec_W, dec_b, map_W_words, map
         h_out_scaled(3)
         w_out(2)
         w_out(3)
-        h_out_plain(6)
+        h_out_planes(6)
         dec_bias_out()
+        widen(nc.scalar.copy, 7)
         quantise("wh01")
         quantise("h4")
         quantise("wh23")
         batch("h56", h_keys(5, 6), "in_wh23")
-        h_scale_pool(6)
+        h_group_pool(6)
         decode(0)
         decode(1)
-        turn(7, 1)
+        spread_map_bias(0, 6)
         decode(2)
         decode(3)
-        spread_map_bias(0, 6)
-        map_bias_out(0)
+        turn(7, 1)
         h_out_scaled(5)
         x_bias(0, 0, [0, 1])
         x_bias(0, 1, [0, 1])
         x_turn((0, 1), 0, 4)
         x_turn((0, 1), 1, 4)
+        map_bias_out(0)
         x_out((0, 1))
         decode(4)
         spread_map_bias(1, 7)
@@ -339,16 +341,16 @@ def tile_model_pb_w8_kernel(tc, h_bytes, h_scale, dec_W, dec_b, map_W_words, map
         decode(7)
         x_bias(1, 0, [0, 1])
         time_map(0, 0)
-        time_map(1, 0)
+        time_map(0, 1)
         x_turn((2,), 0, 0)
         x_turn((3,), 0, 1)
         x_bias(1, 1, [0])
         x_bias(1, 1, [1])
         x_turn((2,), 1, 0)
         x_turn((3,), 1, 1)
-        time_map(0, 1)
-        time_map(1, 1)
         time_map(0, 2)
+        time_map(1, 0)
+        time_map(1, 1)
         time_map(1, 2)
         x_out((2,))
         x_out((3,))
@@ -360,4 +362,4 @@ def tile_model_pb_w8_kernel(tc, h_bytes, h_scale, dec_W, dec_b, map_W_words, map
                 time_map(1, 3)
             time_map(2, s)
             time_map(3, s)
-            finish(s, 2 if s in (0, 3) else 1)
+            finish(s, 2 if s == 3 else 1)

@@ -105,11 +105,11 @@ def tile_model_pb_w8_kernel(tc, h_bytes, h_scale, dec_W, dec_b, map_W_words, map
             to = dec_bias[:].rearrange("b u p h e -> b (u p h e)").bitcast(F32).rearrange("b (u p h) -> b u p h", u=2, h=2)
             nc.scalar.copy(out=to, in_=side_ps["dec_bias_ps"][:].rearrange("b (h u) p -> b u p h", u=2))
 
-        def spread_map_bias(c, b):
-            side_ps["map", c] = bank(b, [P, 1024], "map_bias_ps%d" % c, BF16)
-            for a in range(2):
-                first = 1024 * c + 512 * a
-                nc.tensor.matmul(side_ps["map", c][:, 512 * a : 512 * (a + 1)], ones[:], map_row[:, first : first + 512], start=True, stop=True)
+        def spread_map_bias(c, a, b):
+            if a == 0:
+                side_ps["map", c] = bank(b, [P, 1024], "map_bias_ps%d" % c, BF16)
+            first = 1024 * c + 512 * a
+            nc.tensor.matmul(side_ps["map", c][:, 512 * a : 512 * (a + 1)], ones[:], map_row[:, first : first + 512], start=True, stop=True)
 
         def map_bias_out(c):
             nc.scalar.copy(out=map_bias[:, 1024 * c : 1024 * (c + 1)], in_=side_ps["map", c][:])
@@ -121,11 +121,12 @@ def tile_model_pb_w8_kernel(tc, h_bytes, h_scale, dec_W, dec_b, map_W_words, map
                 hx[unit, e] = t[:]
 
         def turn(unit, b, first=0, count=2):
-            ht[unit, first] = bank(b, [P, 2, count * P], "ht%d_%d" % (unit, first))
+            turned = bank(b, [P, 2, count * P], "ht%d_%d" % (unit, first))
             for e in range(count):
+                ht[unit, first + e] = (turned, e * P)
                 words = hx[unit, first + e].bitcast(F32)
                 for v in range(2):
-                    nc.tensor.transpose(ht[unit, first][:, v, e * P : (e + 1) * P], words[:, v::2], ident[:])
+                    nc.tensor.transpose(turned[:, v, e * P : (e + 1) * P], words[:, v::2], ident[:])
 
         def batch(name, keys, tag=None):
             t = keep.tile([P, len(keys) * D], BF16, name="in_" + name, tag=tag or "in_" + name, align_bytes=64)
@@ -147,15 +148,17 @@ def tile_model_pb_w8_kernel(tc, h_bytes, h_scale, dec_W, dec_b, map_W_words, map
                 scales[key] = plane[:, m * P : (m + 1) * P]
 
         def h_out_scaled(unit, first=0, count=2):
+            turned, column = ht[unit, first]
             to = slots(("h", unit, first), count).rearrange("p (r v z) -> p r v z", v=2, z=2)
-            of = ht[unit, first][:].rearrange("p v r -> p (v r)").bitcast(BF16).rearrange("p (v r z) -> p r v z", v=2, z=2)
+            of = turned[:].rearrange("p v r -> p (v r)").bitcast(BF16).rearrange("p (v r z) -> p r v z", v=2, z=2)
             by = scale_col[:].rearrange("p (o v z) -> p o v z", o=1, v=2).to_broadcast([P, count * P, 2, 2])
-            nc.vector.tensor_tensor(out=to, in0=of, in1=by, op=MULT)
+            nc.vector.tensor_tensor(out=to, in0=of[:, column : column + count * P], in1=by, op=MULT)
 
-        def h_out_planes(unit):
-            hw[unit] = sb([P, 4, 2 * P], BF16, "hw%d" % unit)
-            of = ht[unit, 0][:].rearrange("p v r -> p (v r)").bitcast(BF16).rearrange("p (v r z) -> p v z r", v=2, z=2)
-            for t in range(4):
+        def h_out_planes(unit, planes=range(4)):
+            if unit not in hw:
+                hw[unit] = sb([P, 4, 2 * P], BF16, "hw%d" % unit)
+            of = ht[unit, 0][0][:].rearrange("p v r -> p (v r)").bitcast(BF16).rearrange("p (v r z) -> p v z r", v=2, z=2)
+            for t in planes:
                 nc.scalar.activation(out=hw[unit][:, t], in_=of[:, t // 2, t % 2], func=COPY, scale=scale_col[:, t : t + 1])
 
         def h_group_pool(unit):
@@ -253,10 +256,10 @@ def tile_model_pb_w8_kernel(tc, h_bytes, h_scale, dec_W, dec_b, map_W_words, map
         nc.sync.dma_start(out=scale_col[:], in_=h_scale.rearrange("a b c d (p j) -> p (a b c d j)", p=P))
         load_h(1)
         load_h(2)
+        nc.sync.dma_start(out=dec_rows[0:MODELS, :], in_=dec_b)
         load_w(0)
         load_h(3)
         load_w(1)
-        nc.sync.dma_start(out=dec_rows[0:MODELS, :], in_=dec_b)
         load_w(2)
         load_w(3)
         nc.sync.dma_start(out=map_row[0:1, :], in_=map_b.rearrange("(o s) -> o s", o=1))
@@ -282,34 +285,37 @@ def tile_model_pb_w8_kernel(tc, h_bytes, h_scale, dec_W, dec_b, map_W_words, map
         turn(0, 0, 0, 1)
         turn(0, 1, 1, 1)
         widen(nc.vector.tensor_copy, 4)
+        widen(nc.vector.tensor_copy, 1, [0])
+        widen(nc.scalar.copy, 1, [1])
         turn(4, 4)
-        widen(nc.scalar.copy, 1)
         turn(1, 5)
         h_out_scaled(0, 0, 1)
         h_out_scaled(0, 1, 1)
         widen(nc.scalar.copy, 2)
+        turn(2, 0)
+        turn_dec_rows(2)
+        h_out_planes(4, [0, 1])
+        widen(nc.scalar.copy, 3)
+        h_out_planes(4, [2, 3])
         w_group_pool(0)
         w_group_pool(1)
-        turn(2, 0)
-        h_out_scaled(4)
-        widen(nc.scalar.copy, 3)
-        turn(3, 1)
+        h_group_pool(4)
         h_out_scaled(1)
+        turn(3, 1)
+        dec_cols_out()
         widen(nc.scalar.copy, 6)
         widen(nc.scalar.copy, 5)
-        turn_dec_rows(4)
         w_group(2, 6)
-        dec_cols_out()
         h_out_scaled(2)
         w_group(3, 7)
         turn(6, 5)
-        spread_dec_bias(4)
+        spread_dec_bias(3)
         turn(5, 0)
         h_out_scaled(3)
         w_out(2)
         w_out(3)
-        h_out_planes(6)
         dec_bias_out()
+        h_out_planes(6)
         widen(nc.scalar.copy, 7)
         quantise("wh01")
         quantise("h4")
@@ -318,37 +324,39 @@ def tile_model_pb_w8_kernel(tc, h_bytes, h_scale, dec_W, dec_b, map_W_words, map
         h_group_pool(6)
         decode(0)
         decode(1)
-        spread_map_bias(0, 6)
+        spread_map_bias(0, 0, 6)
+        spread_map_bias(0, 1, 6)
         decode(2)
         decode(3)
-        turn(7, 1)
-        h_out_scaled(5)
         x_bias(0, 0, [0, 1])
+        h_out_scaled(5)
         x_bias(0, 1, [0, 1])
+        turn(7, 1)
+        decode(4)
+        spread_map_bias(1, 0, 7)
         x_turn((0, 1), 0, 4)
         x_turn((0, 1), 1, 4)
+        spread_map_bias(1, 1, 7)
         map_bias_out(0)
         x_out((0, 1))
-        decode(4)
-        spread_map_bias(1, 7)
         map_bias_out(1)
-        h_out_scaled(7)
         quantise("h56")
-        quantise("h7")
-        quantise("x01")
         decode(5)
         decode(6)
+        h_out_scaled(7)
+        quantise("x01")
+        quantise("h7")
+        time_map(0, 0)
         decode(7)
         x_bias(1, 0, [0, 1])
-        time_map(0, 0)
         time_map(0, 1)
-        x_turn((2,), 0, 0)
-        x_turn((3,), 0, 1)
+        time_map(0, 2)
+        time_map(0, 3)
         x_bias(1, 1, [0])
         x_bias(1, 1, [1])
-        x_turn((2,), 1, 0)
-        x_turn((3,), 1, 1)
-        time_map(0, 2)
+        for g in (2, 3):
+            for u in range(2):
+                x_turn((g,), u, g - 2)
         time_map(1, 0)
         time_map(1, 1)
         time_map(1, 2)
@@ -358,7 +366,6 @@ def tile_model_pb_w8_kernel(tc, h_bytes, h_scale, dec_W, dec_b, map_W_words, map
         quantise("x3")
         for s in range(4):
             if s == 3:
-                time_map(0, 3)
                 time_map(1, 3)
             time_map(2, s)
             time_map(3, s)

@@ -369,4 +369,4 @@ def tile_model_pb_w8_kernel(tc, h_bytes, h_scale, dec_W, dec_b, map_W_words, map
                 time_map(1, 3)
             time_map(2, s)
             time_map(3, s)
-            finish(s, 2 if s == 3 else 1)
+            finish(s, 2 if s in (0, 3) else 1)

@@ -76,8 +76,7 @@ def tile_model_pb_w8_kernel(tc, h_bytes, h_scale, dec_W, dec_b, map_W_words, map
         ident_bf = sb([P, P], BF16, "ident_bf")
         dec_rows = sb([P, P], BF16, "dec_rows")
         dec_cols = sb([P, MODELS], BF16, "dec_cols")
-        map_row = sb([P, T], BF16, "map_row")
-        ones = sb([P, P], BF16, "ones")
+        map_rows = sb([P, 512], BF16, "map_rows")
         wsc = sb([P, T], U8, "wsc")
         dec_bias = sb([P, 2, P, 2, 2], BF16, "dec_bias")
         map_bias = sb([P, T], BF16, "map_bias")
@@ -108,8 +107,9 @@ def tile_model_pb_w8_kernel(tc, h_bytes, h_scale, dec_W, dec_b, map_W_words, map
         def spread_map_bias(c, a, b):
             if a == 0:
                 side_ps["map", c] = bank(b, [P, 1024], "map_bias_ps%d" % c, BF16)
-            first = 1024 * c + 512 * a
-            nc.tensor.matmul(side_ps["map", c][:, 512 * a : 512 * (a + 1)], ones[:], map_row[:, first : first + 512], start=True, stop=True)
+            row = 2 * c + a
+            pick = ident_bf[:, row : row + 1].to_broadcast([P, P])
+            nc.tensor.matmul(side_ps["map", c][:, 512 * a : 512 * (a + 1)], pick, map_rows[:], start=True, stop=True)
 
         def map_bias_out(c):
             nc.scalar.copy(out=map_bias[:, 1024 * c : 1024 * (c + 1)], in_=side_ps["map", c][:])
@@ -179,6 +179,17 @@ def tile_model_pb_w8_kernel(tc, h_bytes, h_scale, dec_W, dec_b, map_W_words, map
             nc.gpsimd.tensor_scalar(out=to, in0=w_raw[k][:].rearrange("p e t c -> p e c t"), scalar1=1.0, scalar2=0.0, op0=MULT, op1=ADD)
 
 
+        def w_group_scalar(k, e):
+            to = slots(("w", k, e), 1).rearrange("p (c t) -> p c t", t=4)
+            nc.scalar.copy(out=to, in_=w_raw[k][:, e].rearrange("p t c -> p c t"))
+
+        def warm_up(b, count):
+            zeros = sb([P, P], F32, "zeros")
+            nc.vector.memset(zeros[:], 0.0)
+            spare = bank(b, [P, P], "spare")
+            for a in range(count):
+                nc.tensor.matmul(spare[:], zeros[:], zeros[:], start=True, stop=True)
+
         def decode(unit):
             l, k = divmod(unit, 4)
             u, h = divmod(k, 2)
@@ -244,25 +255,24 @@ def tile_model_pb_w8_kernel(tc, h_bytes, h_scale, dec_W, dec_b, map_W_words, map
             return [("w", k, e) for e in range(2)]
 
         nc.vector.memset(ident[:], 0.0)
-        nc.vector.memset(wsc[:].bitcast(I32), 0)
         make_identity(nc, ident[:], nomemset=True)
-        nc.vector.memset(ones[:], 1.0)
+        nc.vector.memset(map_rows[:].bitcast(I32), 0)
         nc.vector.memset(dec_rows[:].bitcast(I32), 0)
-        nc.vector.memset(map_row[:].bitcast(I32), 0)
         nc.vector.tensor_copy(out=ident_bf[:], in_=ident[:])
+        nc.vector.memset(wsc[:].bitcast(I32), 0)
 
         load_h(0, [0])
         load_h(0, [1])
         nc.sync.dma_start(out=scale_col[:], in_=h_scale.rearrange("a b c d (p j) -> p (a b c d j)", p=P))
         load_h(1)
-        load_h(2)
-        nc.sync.dma_start(out=dec_rows[0:MODELS, :], in_=dec_b)
+        nc.sync.dma_start(out=map_rows[0:4, :], in_=map_b.rearrange("(q s) -> q s", q=4))
         load_w(0)
-        load_h(3)
-        load_w(1)
+        load_h(2)
         load_w(2)
+        load_h(3)
+        nc.sync.dma_start(out=dec_rows[0:MODELS, :], in_=dec_b)
+        load_w(1)
         load_w(3)
-        nc.sync.dma_start(out=map_row[0:1, :], in_=map_b.rearrange("(o s) -> o s", o=1))
         load_map_w(0, 0, 4)
         load_map_scales(nc.sync, range(4))
         load_map_w(1, 0, 4)
@@ -274,99 +284,99 @@ def tile_model_pb_w8_kernel(tc, h_bytes, h_scale, dec_W, dec_b, map_W_words, map
 
         batch("wh01", w_keys(0) + h_keys(0) + w_keys(1) + h_keys(1))
         batch("wh23", w_keys(2) + h_keys(2) + w_keys(3) + h_keys(3))
-        batch("h4", h_keys(4))
-        batch("h7", h_keys(7))
-        batch("x01", [("x", 0), ("x", 1)])
-        batch("x2", [("x", 2)])
-        batch("x3", [("x", 3)])
+        batch("h45", h_keys(4, 5))
+        for g in range(GROUPS):
+            batch("x%d" % g, [("x", g)])
 
         widen(nc.vector.tensor_copy, 0, [0])
+        widen(nc.vector.tensor_copy, 4, [0])
         widen(nc.scalar.copy, 0, [1])
+        widen(nc.scalar.copy, 4, [1])
         turn(0, 0, 0, 1)
         turn(0, 1, 1, 1)
-        widen(nc.vector.tensor_copy, 4)
-        widen(nc.vector.tensor_copy, 1, [0])
-        widen(nc.scalar.copy, 1, [1])
         turn(4, 4)
-        turn(1, 5)
         h_out_scaled(0, 0, 1)
         h_out_scaled(0, 1, 1)
-        widen(nc.scalar.copy, 2)
-        turn(2, 0)
-        turn_dec_rows(2)
-        h_out_planes(4, [0, 1])
-        widen(nc.scalar.copy, 3)
-        h_out_planes(4, [2, 3])
+        widen(nc.scalar.copy, 1)
+        turn(1, 5)
+        spread_map_bias(0, 0, 6)
         w_group_pool(0)
-        w_group_pool(1)
+        widen(nc.scalar.copy, 5)
+        turn(5, 0)
+        spread_map_bias(0, 1, 6)
+        h_out_planes(4)
         h_group_pool(4)
+        w_group_pool(1)
         h_out_scaled(1)
-        turn(3, 1)
+        w_group(2, 3, [1])
+        widen(nc.scalar.copy, 2)
+        turn(2, 1)
+        h_out_scaled(5)
+        spread_map_bias(1, 0, 7)
+        widen(nc.scalar.copy, 3)
+        turn(3, 4)
+        turn_dec_rows(2)
+        w_group(3, 5)
+        h_out_scaled(2)
+        w_out(2, 1)
+        w_group_scalar(2, 0)
         dec_cols_out()
         widen(nc.scalar.copy, 6)
-        widen(nc.scalar.copy, 5)
-        w_group(2, 6)
-        h_out_scaled(2)
-        w_group(3, 7)
-        turn(6, 5)
-        spread_dec_bias(3)
-        turn(5, 0)
         h_out_scaled(3)
-        w_out(2)
+        turn(6, 0)
+        spread_dec_bias(1)
         w_out(3)
-        dec_bias_out()
-        h_out_planes(6)
         widen(nc.scalar.copy, 7)
+        dec_bias_out()
         quantise("wh01")
-        quantise("h4")
-        quantise("wh23")
-        batch("h56", h_keys(5, 6), "in_wh23")
-        h_group_pool(6)
         decode(0)
         decode(1)
-        spread_map_bias(0, 0, 6)
-        spread_map_bias(0, 1, 6)
+        turn(7, 4)
+        h_out_planes(6)
+        quantise("wh23")
         decode(2)
         decode(3)
         x_bias(0, 0, [0, 1])
-        h_out_scaled(5)
+        quantise("h45")
+        batch("h67", h_keys(6, 7), "in_h45")
+        h_group_pool(6)
         x_bias(0, 1, [0, 1])
-        turn(7, 1)
-        decode(4)
-        spread_map_bias(1, 0, 7)
-        x_turn((0, 1), 0, 4)
-        x_turn((0, 1), 1, 4)
-        spread_map_bias(1, 1, 7)
         map_bias_out(0)
-        x_out((0, 1))
-        map_bias_out(1)
-        quantise("h56")
+        x_turn((0,), 0, 1)
+        x_turn((1,), 0, 5)
+        decode(4)
         decode(5)
-        decode(6)
+        x_turn((0,), 1, 1)
+        x_turn((1,), 1, 5)
+        spread_map_bias(1, 1, 7)
         h_out_scaled(7)
-        quantise("x01")
-        quantise("h7")
-        time_map(0, 0)
-        decode(7)
+        x_out((0,))
+        x_out((1,))
+        map_bias_out(1)
         x_bias(1, 0, [0, 1])
+        quantise("x0")
+        quantise("h67")
+        quantise("x1")
+        time_map(0, 0)
         time_map(0, 1)
         time_map(0, 2)
+        decode(6)
+        decode(7)
         time_map(0, 3)
+        time_map(1, 0)
         x_bias(1, 1, [0])
         x_bias(1, 1, [1])
         for g in (2, 3):
             for u in range(2):
                 x_turn((g,), u, g - 2)
-        time_map(1, 0)
         time_map(1, 1)
         time_map(1, 2)
+        time_map(1, 3)
         x_out((2,))
         x_out((3,))
         quantise("x2")
         quantise("x3")
         for s in range(4):
-            if s == 3:
-                time_map(1, 3)
             time_map(2, s)
             time_map(3, s)
             finish(s, 2 if s in (0, 3) else 1)

@@ -77,6 +77,7 @@ def tile_model_pb_w8_kernel(tc, h_bytes, h_scale, dec_W, dec_b, map_W_words, map
         dec_rows = sb([P, P], BF16, "dec_rows")
         dec_cols = sb([P, MODELS], BF16, "dec_cols")
         map_rows = sb([P, 512], BF16, "map_rows")
+        map_cols = sb([P, 8], BF16, "map_cols")
         wsc = sb([P, T], U8, "wsc")
         dec_bias = sb([P, 2, P, 2, 2], BF16, "dec_bias")
         map_bias = sb([P, T], BF16, "map_bias")
@@ -107,9 +108,16 @@ def tile_model_pb_w8_kernel(tc, h_bytes, h_scale, dec_W, dec_b, map_W_words, map
         def spread_map_bias(c, a, b):
             if a == 0:
                 side_ps["map", c] = bank(b, [P, 1024], "map_bias_ps%d" % c, BF16)
-            row = 2 * c + a
+            row = a
             pick = ident_bf[:, row : row + 1].to_broadcast([P, P])
             nc.tensor.matmul(side_ps["map", c][:, 512 * a : 512 * (a + 1)], pick, map_rows[:], start=True, stop=True)
+
+        def turn_map_bias(b):
+            spread(b, "map_turned", map_cols[:].bitcast(F32))
+
+        def map_turned_out():
+            to = map_bias[:, 0:1024].bitcast(F32).rearrange("b (p c) -> b p c", c=4)
+            nc.scalar.copy(out=to, in_=side_ps["map_turned"][:].rearrange("b c p -> b p c"))
 
         def map_bias_out(c):
             nc.scalar.copy(out=map_bias[:, 1024 * c : 1024 * (c + 1)], in_=side_ps["map", c][:])
@@ -164,6 +172,15 @@ def tile_model_pb_w8_kernel(tc, h_bytes, h_scale, dec_W, dec_b, map_W_words, map
         def h_group_pool(unit):
             to = slots(("h", unit, 0), 2).rearrange("p (r t) -> p r t", t=4)
             nc.gpsimd.tensor_scalar(out=to, in0=hw[unit][:].rearrange("p t r -> p r t"), scalar1=1.0, scalar2=0.0, op0=MULT, op1=ADD)
+
+        def h_group(unit, b):
+            side_ps["h", unit] = bank(b, [P, 2, 512], "h_ps%d" % unit, BF16)
+            for e in range(2):
+                planes = hw[unit][:, :, e * P : (e + 1) * P].rearrange("p t r -> p r t")
+                nc.tensor.matmul(side_ps["h", unit][:, e], ident_bf[:], planes, start=True, stop=True)
+
+        def h_group_out(unit):
+            nc.scalar.copy(out=slots(("h", unit, 0), 2), in_=side_ps["h", unit][:].rearrange("p e x -> p (e x)"))
 
         def w_group(k, b, models=(0, 1)):
             for e in models:
@@ -256,23 +273,24 @@ def tile_model_pb_w8_kernel(tc, h_bytes, h_scale, dec_W, dec_b, map_W_words, map
 
         nc.vector.memset(ident[:], 0.0)
         make_identity(nc, ident[:], nomemset=True)
-        nc.vector.memset(map_rows[:].bitcast(I32), 0)
         nc.vector.memset(dec_rows[:].bitcast(I32), 0)
+        nc.vector.memset(map_rows[:].bitcast(I32), 0)
         nc.vector.tensor_copy(out=ident_bf[:], in_=ident[:])
         nc.vector.memset(wsc[:].bitcast(I32), 0)
 
+        nc.sync.dma_start(out=map_cols[:], in_=map_b[0:1024].rearrange("(p c) -> p c", p=P))
         load_h(0, [0])
+        nc.sync.dma_start(out=dec_rows[0:MODELS, :], in_=dec_b)
         load_h(0, [1])
         nc.sync.dma_start(out=scale_col[:], in_=h_scale.rearrange("a b c d (p j) -> p (a b c d j)", p=P))
-        load_h(1)
-        nc.sync.dma_start(out=map_rows[0:4, :], in_=map_b.rearrange("(q s) -> q s", q=4))
         load_w(0)
+        load_h(1)
         load_h(2)
-        load_w(2)
-        load_h(3)
-        nc.sync.dma_start(out=dec_rows[0:MODELS, :], in_=dec_b)
         load_w(1)
+        load_h(3)
+        load_w(2)
         load_w(3)
+        nc.sync.dma_start(out=map_rows[0:2, :], in_=map_b[1024:T].rearrange("(q s) -> q s", q=2))
         load_map_w(0, 0, 4)
         load_map_scales(nc.sync, range(4))
         load_map_w(1, 0, 4)
@@ -285,98 +303,100 @@ def tile_model_pb_w8_kernel(tc, h_bytes, h_scale, dec_W, dec_b, map_W_words, map
         batch("wh01", w_keys(0) + h_keys(0) + w_keys(1) + h_keys(1))
         batch("wh23", w_keys(2) + h_keys(2) + w_keys(3) + h_keys(3))
         batch("h45", h_keys(4, 5))
+        batch("h67", h_keys(6, 7))
         for g in range(GROUPS):
             batch("x%d" % g, [("x", g)])
 
+        turn_map_bias(7)
+        turn_dec_rows(2)
         widen(nc.vector.tensor_copy, 0, [0])
         widen(nc.vector.tensor_copy, 4, [0])
         widen(nc.scalar.copy, 0, [1])
         widen(nc.scalar.copy, 4, [1])
+        dec_cols_out()
         turn(0, 0, 0, 1)
         turn(0, 1, 1, 1)
         turn(4, 4)
+        spread_dec_bias(3)
+        map_turned_out()
         h_out_scaled(0, 0, 1)
+        w_group_pool(0)
         h_out_scaled(0, 1, 1)
         widen(nc.scalar.copy, 1)
         turn(1, 5)
-        spread_map_bias(0, 0, 6)
-        w_group_pool(0)
-        widen(nc.scalar.copy, 5)
-        turn(5, 0)
-        spread_map_bias(0, 1, 6)
-        h_out_planes(4)
-        h_group_pool(4)
-        w_group_pool(1)
-        h_out_scaled(1)
-        w_group(2, 3, [1])
+        h_out_scaled(4)
         widen(nc.scalar.copy, 2)
-        turn(2, 1)
-        h_out_scaled(5)
-        spread_map_bias(1, 0, 7)
+        turn(2, 6)
+        w_group_pool(1)
+        widen(nc.scalar.copy, 5)
+        turn(5, 7)
+        dec_bias_out()
+        h_out_scaled(1)
         widen(nc.scalar.copy, 3)
-        turn(3, 4)
-        turn_dec_rows(2)
-        w_group(3, 5)
+        turn(3, 0)
+        w_group_pool(2)
         h_out_scaled(2)
-        w_out(2, 1)
-        w_group_scalar(2, 0)
-        dec_cols_out()
-        widen(nc.scalar.copy, 6)
+        h_out_planes(5)
+        w_group(3, 1)
         h_out_scaled(3)
-        turn(6, 0)
-        spread_dec_bias(1)
+        widen(nc.scalar.copy, 6)
+        turn(6, 5)
+        h_group(5, 4)
         w_out(3)
         widen(nc.scalar.copy, 7)
-        dec_bias_out()
         quantise("wh01")
         decode(0)
         decode(1)
-        turn(7, 4)
+        turn(7, 7)
         h_out_planes(6)
+        h_group_out(5)
         quantise("wh23")
         decode(2)
         decode(3)
         x_bias(0, 0, [0, 1])
-        quantise("h45")
-        batch("h67", h_keys(6, 7), "in_h45")
-        h_group_pool(6)
+        h_group(6, 6)
+        x_turn((0,), 0, 0)
+        x_turn((1,), 0, 1)
+        h_out_scaled(7, 0, 1)
         x_bias(0, 1, [0, 1])
-        map_bias_out(0)
-        x_turn((0,), 0, 1)
-        x_turn((1,), 0, 5)
-        decode(4)
-        decode(5)
-        x_turn((0,), 1, 1)
-        x_turn((1,), 1, 5)
-        spread_map_bias(1, 1, 7)
-        h_out_scaled(7)
+        x_turn((0,), 1, 0)
+        x_turn((1,), 1, 1)
+        spread_map_bias(1, 0, 5)
+        spread_map_bias(1, 1, 5)
+        h_out_scaled(7, 1, 1)
+        h_group_out(6)
         x_out((0,))
         x_out((1,))
         map_bias_out(1)
-        x_bias(1, 0, [0, 1])
+        quantise("h45")
         quantise("x0")
         quantise("h67")
         quantise("x1")
+        decode(4)
+        decode(5)
         time_map(0, 0)
-        time_map(0, 1)
-        time_map(0, 2)
+        time_map(0, 3)
         decode(6)
         decode(7)
-        time_map(0, 3)
-        time_map(1, 0)
+        time_map(0, 2)
+        time_map(0, 1)
+        x_bias(1, 0, [0, 1])
         x_bias(1, 1, [0])
         x_bias(1, 1, [1])
-        for g in (2, 3):
-            for u in range(2):
-                x_turn((g,), u, g - 2)
+        x_turn((2,), 0, 0)
+        x_turn((3,), 0, 1)
+        x_turn((2,), 1, 0)
+        x_turn((3,), 1, 1)
+        time_map(1, 0)
         time_map(1, 1)
         time_map(1, 2)
-        time_map(1, 3)
         x_out((2,))
         x_out((3,))
         quantise("x2")
         quantise("x3")
         for s in range(4):
+            if s == 3:
+                time_map(1, s)
             time_map(2, s)
             time_map(3, s)
             finish(s, 2 if s in (0, 3) else 1)

@@ -101,9 +101,9 @@ def tile_model_pb_w8_kernel(tc, h_bytes, h_scale, dec_W, dec_b, map_W_words, map
         def spread_dec_bias(b):
             spread(b, "dec_bias_ps", dec_cols[:].bitcast(F32))
 
-        def dec_bias_out():
+        def dec_bias_out(copy):
             to = dec_bias[:].rearrange("b u p h e -> b (u p h e)").bitcast(F32).rearrange("b (u p h) -> b u p h", u=2, h=2)
-            nc.scalar.copy(out=to, in_=side_ps["dec_bias_ps"][:].rearrange("b (h u) p -> b u p h", u=2))
+            copy(out=to, in_=side_ps["dec_bias_ps"][:].rearrange("b (h u) p -> b u p h", u=2))
 
         def spread_map_bias(c, a, b):
             if a == 0:
@@ -115,9 +115,9 @@ def tile_model_pb_w8_kernel(tc, h_bytes, h_scale, dec_W, dec_b, map_W_words, map
         def turn_map_bias(b):
             spread(b, "map_turned", map_cols[:].bitcast(F32))
 
-        def map_turned_out():
+        def map_turned_out(copy):
             to = map_bias[:, 0:1024].bitcast(F32).rearrange("b (p c) -> b p c", c=4)
-            nc.scalar.copy(out=to, in_=side_ps["map_turned"][:].rearrange("b c p -> b p c"))
+            copy(out=to, in_=side_ps["map_turned"][:].rearrange("b c p -> b p c"))
 
         def map_bias_out(c):
             nc.scalar.copy(out=map_bias[:, 1024 * c : 1024 * (c + 1)], in_=side_ps["map", c][:])
@@ -162,34 +162,36 @@ def tile_model_pb_w8_kernel(tc, h_bytes, h_scale, dec_W, dec_b, map_W_words, map
             by = scale_col[:].rearrange("p (o v z) -> p o v z", o=1, v=2).to_broadcast([P, count * P, 2, 2])
             nc.vector.tensor_tensor(out=to, in0=of[:, column : column + count * P], in1=by, op=MULT)
 
-        def h_out_planes(unit, planes=range(4)):
+        def h_out_planes(unit, planes=range(4), first=0):
             if unit not in hw:
-                hw[unit] = sb([P, 4, 2 * P], BF16, "hw%d" % unit)
+                hw[unit] = sb([P, 4, (2 - first) * P], BF16, "hw%d" % unit)
             of = ht[unit, 0][0][:].rearrange("p v r -> p (v r)").bitcast(BF16).rearrange("p (v r z) -> p v z r", v=2, z=2)
             for t in planes:
-                nc.scalar.activation(out=hw[unit][:, t], in_=of[:, t // 2, t % 2], func=COPY, scale=scale_col[:, t : t + 1])
+                nc.scalar.activation(out=hw[unit][:, t], in_=of[:, t // 2, t % 2, first * P :], func=COPY, scale=scale_col[:, t : t + 1])
 
-        def h_group_pool(unit):
-            to = slots(("h", unit, 0), 2).rearrange("p (r t) -> p r t", t=4)
+        def h_group_pool(unit, first=0):
+            to = slots(("h", unit, first), 2 - first).rearrange("p (r t) -> p r t", t=4)
             nc.gpsimd.tensor_scalar(out=to, in0=hw[unit][:].rearrange("p t r -> p r t"), scalar1=1.0, scalar2=0.0, op0=MULT, op1=ADD)
 
-        def h_group(unit, b):
-            side_ps["h", unit] = bank(b, [P, 2, 512], "h_ps%d" % unit, BF16)
-            for e in range(2):
+        def h_group_scalar(unit):
+            to = slots(("h", unit, 0), 2).rearrange("p (r t) -> p r t", t=4)
+            nc.scalar.copy(out=to, in_=hw[unit][:].rearrange("p t r -> p r t"))
+
+        def h_group(unit, b, first=0):
+            side_ps["h", unit] = bank(b, [P, 2 - first, 512], "h_ps%d" % unit, BF16)
+            for e in range(2 - first):
                 planes = hw[unit][:, :, e * P : (e + 1) * P].rearrange("p t r -> p r t")
                 nc.tensor.matmul(side_ps["h", unit][:, e], ident_bf[:], planes, start=True, stop=True)
 
-        def h_group_out(unit):
-            nc.scalar.copy(out=slots(("h", unit, 0), 2), in_=side_ps["h", unit][:].rearrange("p e x -> p (e x)"))
+        def h_group_out(unit, first=0):
+            nc.scalar.copy(out=slots(("h", unit, first), 2 - first), in_=side_ps["h", unit][:].rearrange("p e x -> p (e x)"))
 
-        def w_group(k, b, models=(0, 1)):
-            for e in models:
-                if ("w", k) not in side_ps:
-                    side_ps["w", k] = bank(b, [P, 2, 512], "w_ps%d" % k, BF16)
-                nc.tensor.matmul(side_ps["w", k][:, e], ident_bf[:], w_raw[k][:, e].rearrange("p t c -> p c t"), start=True, stop=True)
+        def w_group(k, e, b):
+            side_ps["w", k, e] = bank(b, [P, 512], "w_ps%d_%d" % (k, e), BF16)
+            nc.tensor.matmul(side_ps["w", k, e][:], ident_bf[:], w_raw[k][:, e].rearrange("p t c -> p c t"), start=True, stop=True)
 
-        def w_out(k, first=0):
-            nc.scalar.copy(out=slots(("w", k, first), 2 - first), in_=side_ps["w", k][:, first:].rearrange("p e x -> p (e x)"))
+        def w_out(k, e):
+            nc.scalar.copy(out=slots(("w", k, e), 1), in_=side_ps["w", k, e][:])
 
         def w_group_pool(k):
             to = slots(("w", k, 0), 2).rearrange("p (e c t) -> p e c t", e=2, t=4)
@@ -233,7 +235,7 @@ def tile_model_pb_w8_kernel(tc, h_bytes, h_scale, dec_W, dec_b, map_W_words, map
                 xb[2 * l + half, u] = t[:, a * HALF : (a + 1) * HALF].rearrange("b p h e -> b (p h e)").bitcast(F32)
 
         def x_turn(groups, u, b):
-            if u == 0:
+            if groups not in xt:
                 xt[groups] = bank(b, [P, len(groups), 2, P], "xt%d" % groups[0])
             for a, g in enumerate(groups):
                 nc.tensor.transpose(xt[groups][:, a, u], xb[g, u], ident[:])
@@ -283,8 +285,8 @@ def tile_model_pb_w8_kernel(tc, h_bytes, h_scale, dec_W, dec_b, map_W_words, map
         nc.sync.dma_start(out=dec_rows[0:MODELS, :], in_=dec_b)
         load_h(0, [1])
         nc.sync.dma_start(out=scale_col[:], in_=h_scale.rearrange("a b c d (p j) -> p (a b c d j)", p=P))
-        load_w(0)
         load_h(1)
+        load_w(0)
         load_h(2)
         load_w(1)
         load_h(3)
@@ -302,7 +304,7 @@ def tile_model_pb_w8_kernel(tc, h_bytes, h_scale, dec_W, dec_b, map_W_words, map
 
         batch("wh01", w_keys(0) + h_keys(0) + w_keys(1) + h_keys(1))
         batch("wh23", w_keys(2) + h_keys(2) + w_keys(3) + h_keys(3))
-        batch("h45", h_keys(4, 5))
+        batch("h4", h_keys(4))
         batch("h67", h_keys(6, 7))
         for g in range(GROUPS):
             batch("x%d" % g, [("x", g)])
@@ -312,74 +314,77 @@ def tile_model_pb_w8_kernel(tc, h_bytes, h_scale, dec_W, dec_b, map_W_words, map
         widen(nc.vector.tensor_copy, 0, [0])
         widen(nc.vector.tensor_copy, 4, [0])
         widen(nc.scalar.copy, 0, [1])
-        widen(nc.scalar.copy, 4, [1])
+        widen(nc.vector.tensor_copy, 4, [1])
         dec_cols_out()
         turn(0, 0, 0, 1)
         turn(0, 1, 1, 1)
         turn(4, 4)
-        spread_dec_bias(3)
-        map_turned_out()
         h_out_scaled(0, 0, 1)
-        w_group_pool(0)
         h_out_scaled(0, 1, 1)
         widen(nc.scalar.copy, 1)
         turn(1, 5)
+        spread_dec_bias(3)
+        widen(nc.scalar.copy, 5)
+        w_group_pool(0)
         h_out_scaled(4)
         widen(nc.scalar.copy, 2)
         turn(2, 6)
+        turn(5, 0)
+        widen(nc.scalar.copy, 6)
+        turn(6, 4)
         w_group_pool(1)
-        widen(nc.scalar.copy, 5)
-        turn(5, 7)
-        dec_bias_out()
         h_out_scaled(1)
         widen(nc.scalar.copy, 3)
-        turn(3, 0)
-        w_group_pool(2)
+        turn(3, 1)
         h_out_scaled(2)
-        h_out_planes(5)
-        w_group(3, 1)
-        h_out_scaled(3)
-        widen(nc.scalar.copy, 6)
-        turn(6, 5)
-        h_group(5, 4)
-        w_out(3)
+        dec_bias_out(nc.vector.tensor_copy)
+        w_group_pool(2)
         widen(nc.scalar.copy, 7)
+        w_group(3, 0, 5)
+        w_group(3, 1, 6)
+        h_out_scaled(3)
+        h_out_planes(6)
+        turn(7, 4)
+        w_out(3, 0)
+        w_out(3, 1)
+        h_group(6, 1)
+        h_out_planes(5)
         quantise("wh01")
         decode(0)
         decode(1)
-        turn(7, 7)
-        h_out_planes(6)
-        h_group_out(5)
+        h_group_out(6)
+        map_turned_out(nc.scalar.copy)
         quantise("wh23")
+        batch("h5", h_keys(5), "in_wh23")
+        h_group_pool(5)
         decode(2)
         decode(3)
         x_bias(0, 0, [0, 1])
-        h_group(6, 6)
+        spread_map_bias(1, 0, 7)
         x_turn((0,), 0, 0)
-        x_turn((1,), 0, 1)
+        x_turn((1,), 0, 6)
         h_out_scaled(7, 0, 1)
         x_bias(0, 1, [0, 1])
         x_turn((0,), 1, 0)
-        x_turn((1,), 1, 1)
-        spread_map_bias(1, 0, 5)
-        spread_map_bias(1, 1, 5)
+        x_turn((1,), 1, 6)
+        spread_map_bias(1, 1, 7)
         h_out_scaled(7, 1, 1)
-        h_group_out(6)
         x_out((0,))
         x_out((1,))
         map_bias_out(1)
-        quantise("h45")
+        quantise("h4")
+        quantise("h5")
         quantise("x0")
         quantise("h67")
         quantise("x1")
         decode(4)
         decode(5)
         time_map(0, 0)
-        time_map(0, 3)
+        time_map(0, 1)
         decode(6)
         decode(7)
         time_map(0, 2)
-        time_map(0, 1)
+        time_map(0, 3)
         x_bias(1, 0, [0, 1])
         x_bias(1, 1, [0])
         x_bias(1, 1, [1])

@@ -23,6 +23,7 @@ PATCHES = 2
 GROUPS = T // 512
 HALF = 64
 FIRST_MODEL = (0, 4, 2, 6)
+ACC_BANK = {0: 4, 512: 5, 1024: 6, 1536: 7, 1792: 2}
 
 FLOPS = 2 * MODELS * BC * PATCHES * D * P + 2 * BC * T * T
 
@@ -41,28 +42,29 @@ def tile_model_pb_w8_kernel(tc, h_bytes, h_scale, dec_W, dec_b, map_W_words, map
         def bank(i, shape, name, dtype=F32):
             return psum.tile(shape, dtype, name=name, tag="bank%d" % i)
 
-        h_view = h_bytes.rearrange("n b c l d -> (b c) n l d")
         hb, w_raw, ww = {}, {}, {}
 
-        def load_h(k, models=(0, 1)):
-            n0 = FIRST_MODEL[k] + models[0]
-            t = sb([P, len(models), PATCHES, D], U8, "hb%d_%d" % (k, models[0]))
-            nc.sync.dma_start(out=t[:], in_=h_view[:, n0 : n0 + len(models)])
-            for a, e in enumerate(models):
+        def load_h(k, parts=1):
+            n0 = FIRST_MODEL[k]
+            t = sb([P, 2, PATCHES, D], U8, "hb%d" % k)
+            rows = h_bytes[n0 : n0 + 2].rearrange("n b (c r) l d -> (n b c) r l d", r=2)
+            for a in range(parts):
+                of = slice(a * 2 // parts, (a + 1) * 2 // parts)
+                nc.sync.dma_start(out=t[:, of], in_=rows[:, of])
+            for r in range(2):
                 for l in range(PATCHES):
-                    hb[4 * l + k, e] = t[:, a, l].bitcast(FP8)
+                    hb[4 * l + k, r] = t[:, r, l].bitcast(FP8)
 
         def load_w(k):
             n0 = FIRST_MODEL[k]
             w_raw[k] = sb([P, 2, 4, P], BF16, "w_raw%d" % k)
             nc.sync.dma_start(out=w_raw[k][:], in_=dec_W[n0 : n0 + 2].rearrange("n (p j) w -> p n j w", j=4))
 
-        def load_map_w(g, first, count):
-            t = sb([P, 512 * count], I32, "ww%d_%d" % (g, first))
+        def load_map_w(g, first, width):
+            if g not in ww:
+                ww[g] = sb([P, T], I32, "ww%d" % g)
             words = map_W_words[g].rearrange("p n t -> p (n t)").bitcast(I32)
-            nc.sync.dma_start(out=t[:], in_=words[:, 512 * first : 512 * (first + count)])
-            for s in range(count):
-                ww[g, first + s] = t[:, 512 * s : 512 * (s + 1)]
+            nc.sync.dma_start(out=ww[g][:, first : first + width], in_=words[:, first : first + width])
 
         def load_map_scales(queue, quadrants):
             for q in quadrants:
@@ -77,10 +79,11 @@ def tile_model_pb_w8_kernel(tc, h_bytes, h_scale, dec_W, dec_b, map_W_words, map
         dec_rows = sb([P, P], BF16, "dec_rows")
         dec_cols = sb([P, MODELS], BF16, "dec_cols")
         map_rows = sb([P, 512], BF16, "map_rows")
-        map_cols = sb([P, 8], BF16, "map_cols")
         wsc = sb([P, T], U8, "wsc")
         dec_bias = sb([P, 2, P, 2, 2], BF16, "dec_bias")
         map_bias = sb([P, T], BF16, "map_bias")
+
+        y = sb([P, T], F32, "y")
 
         hx, ht, hw = {}, {}, {}
         batches, place, codes, scales = {}, {}, {}, {}
@@ -108,16 +111,9 @@ def tile_model_pb_w8_kernel(tc, h_bytes, h_scale, dec_W, dec_b, map_W_words, map
         def spread_map_bias(c, a, b):
             if a == 0:
                 side_ps["map", c] = bank(b, [P, 1024], "map_bias_ps%d" % c, BF16)
-            row = a
+            row = 2 * c + a
             pick = ident_bf[:, row : row + 1].to_broadcast([P, P])
             nc.tensor.matmul(side_ps["map", c][:, 512 * a : 512 * (a + 1)], pick, map_rows[:], start=True, stop=True)
-
-        def turn_map_bias(b):
-            spread(b, "map_turned", map_cols[:].bitcast(F32))
-
-        def map_turned_out(copy):
-            to = map_bias[:, 0:1024].bitcast(F32).rearrange("b (p c) -> b p c", c=4)
-            copy(out=to, in_=side_ps["map_turned"][:].rearrange("b c p -> b p c"))
 
         def map_bias_out(c):
             nc.scalar.copy(out=map_bias[:, 1024 * c : 1024 * (c + 1)], in_=side_ps["map", c][:])
@@ -128,13 +124,12 @@ def tile_model_pb_w8_kernel(tc, h_bytes, h_scale, dec_W, dec_b, map_W_words, map
                 engine_copy(out=t[:], in_=hb[unit, e])
                 hx[unit, e] = t[:]
 
-        def turn(unit, b, first=0, count=2):
-            turned = bank(b, [P, 2, count * P], "ht%d_%d" % (unit, first))
-            for e in range(count):
-                ht[unit, first + e] = (turned, e * P)
-                words = hx[unit, first + e].bitcast(F32)
+        def turn(unit, b, rows=(0, 1)):
+            ht[unit] = bank(b, [P, 2, 2, 2, HALF], "ht%d_%d" % (unit, rows[0]))
+            for r in rows:
+                words = hx[unit, r].bitcast(F32)
                 for v in range(2):
-                    nc.tensor.transpose(turned[:, v, e * P : (e + 1) * P], words[:, v::2], ident[:])
+                    nc.tensor.transpose(ht[unit][:, v, :, r], words[:, v::2], ident[:])
 
         def batch(name, keys, tag=None):
             t = keep.tile([P, len(keys) * D], BF16, name="in_" + name, tag=tag or "in_" + name, align_bytes=64)
@@ -156,16 +151,23 @@ def tile_model_pb_w8_kernel(tc, h_bytes, h_scale, dec_W, dec_b, map_W_words, map
                 scales[key] = plane[:, m * P : (m + 1) * P]
 
         def h_out_scaled(unit, first=0, count=2):
-            turned, column = ht[unit, first]
+            column = first * P
             to = slots(("h", unit, first), count).rearrange("p (r v z) -> p r v z", v=2, z=2)
-            of = turned[:].rearrange("p v r -> p (v r)").bitcast(BF16).rearrange("p (v r z) -> p r v z", v=2, z=2)
+            of = ht[unit][:].rearrange("p v e r c -> p (v e r c)").bitcast(BF16).rearrange("p (v r z) -> p r v z", v=2, z=2)
             by = scale_col[:].rearrange("p (o v z) -> p o v z", o=1, v=2).to_broadcast([P, count * P, 2, 2])
             nc.vector.tensor_tensor(out=to, in0=of[:, column : column + count * P], in1=by, op=MULT)
+
+        def h_out_scaled_half(unit, r):
+            for e in range(2):
+                of = ht[unit][:, :, e, r].bitcast(BF16).rearrange("p v (c z) -> p c v z", z=2)
+                to = slots(("h", unit, e), 1)[:, 256 * r : 256 * (r + 1)].rearrange("p (c v z) -> p c v z", v=2, z=2)
+                by = scale_col[:].rearrange("p (o v z) -> p o v z", o=1, v=2).to_broadcast([P, HALF, 2, 2])
+                nc.vector.tensor_tensor(out=to, in0=of, in1=by, op=MULT)
 
         def h_out_planes(unit, planes=range(4), first=0):
             if unit not in hw:
                 hw[unit] = sb([P, 4, (2 - first) * P], BF16, "hw%d" % unit)
-            of = ht[unit, 0][0][:].rearrange("p v r -> p (v r)").bitcast(BF16).rearrange("p (v r z) -> p v z r", v=2, z=2)
+            of = ht[unit][:].rearrange("p v e r c -> p (v e r c)").bitcast(BF16).rearrange("p (v r z) -> p v z r", v=2, z=2)
             for t in planes:
                 nc.scalar.activation(out=hw[unit][:, t], in_=of[:, t // 2, t % 2, first * P :], func=COPY, scale=scale_col[:, t : t + 1])
 
@@ -177,11 +179,11 @@ def tile_model_pb_w8_kernel(tc, h_bytes, h_scale, dec_W, dec_b, map_W_words, map
             to = slots(("h", unit, 0), 2).rearrange("p (r t) -> p r t", t=4)
             nc.scalar.copy(out=to, in_=hw[unit][:].rearrange("p t r -> p r t"))
 
-        def h_group(unit, b, first=0):
-            side_ps["h", unit] = bank(b, [P, 2 - first, 512], "h_ps%d" % unit, BF16)
-            for e in range(2 - first):
-                planes = hw[unit][:, :, e * P : (e + 1) * P].rearrange("p t r -> p r t")
-                nc.tensor.matmul(side_ps["h", unit][:, e], ident_bf[:], planes, start=True, stop=True)
+        def h_group(unit, e, b):
+            if e == 0:
+                side_ps["h", unit] = bank(b, [P, 2, 512], "h_ps%d" % unit, BF16)
+            planes = hw[unit][:, :, e * P : (e + 1) * P].rearrange("p t r -> p r t")
+            nc.tensor.matmul(side_ps["h", unit][:, e], ident_bf[:], planes, start=True, stop=True)
 
         def h_group_out(unit, first=0):
             nc.scalar.copy(out=slots(("h", unit, first), 2 - first), in_=side_ps["h", unit][:].rearrange("p e x -> p (e x)"))
@@ -193,9 +195,9 @@ def tile_model_pb_w8_kernel(tc, h_bytes, h_scale, dec_W, dec_b, map_W_words, map
         def w_out(k, e):
             nc.scalar.copy(out=slots(("w", k, e), 1), in_=side_ps["w", k, e][:])
 
-        def w_group_pool(k):
-            to = slots(("w", k, 0), 2).rearrange("p (e c t) -> p e c t", e=2, t=4)
-            nc.gpsimd.tensor_scalar(out=to, in0=w_raw[k][:].rearrange("p e t c -> p e c t"), scalar1=1.0, scalar2=0.0, op0=MULT, op1=ADD)
+        def w_group_pool(k, count=2):
+            to = slots(("w", k, 0), count).rearrange("p (e c t) -> p e c t", e=count, t=4)
+            nc.gpsimd.tensor_scalar(out=to, in0=w_raw[k][:, 0:count].rearrange("p e t c -> p e c t"), scalar1=1.0, scalar2=0.0, op0=MULT, op1=ADD)
 
 
         def w_group_scalar(k, e):
@@ -241,31 +243,27 @@ def tile_model_pb_w8_kernel(tc, h_bytes, h_scale, dec_W, dec_b, map_W_words, map
                 nc.tensor.transpose(xt[groups][:, a, u], xb[g, u], ident[:])
 
         def x_out(groups):
-            to = slots(("x", groups[0]), len(groups)).bitcast(F32).rearrange("p (a r u) -> p a r u", a=len(groups), u=2)
-            nc.scalar.copy(out=to, in_=xt[groups][:].rearrange("p a u r -> p a r u"))
+            to = slots(("x", groups[0]), 1).bitcast(F32).rearrange("p (c r u) -> p c r u", r=2, u=2)
+            nc.scalar.copy(out=to, in_=xt[groups][:, 0].rearrange("p u (r c) -> p c r u", r=2))
 
-        def time_map(g, s):
+        def time_map(g, first, width=512):
             if g == 0:
-                acc[s] = bank(4 + s, [P, 512], "acc%d" % s)
-            cols = slice(512 * s, 512 * (s + 1))
+                acc[first] = bank(ACC_BANK[first], [P, width], "acc%d" % first)
+            cols = slice(first, first + width)
             nc.tensor.matmul_mx(
-                out=acc[s][:],
+                out=acc[first][:],
                 lhsT=codes["x", g],
                 lhsT_scale=scales["x", g],
-                rhs=ww[g, s].bitcast(FP8X4),
+                rhs=ww[g][:, cols].bitcast(FP8X4),
                 rhs_scale=wsc[4 * g : P, cols],
                 start=(g == 0),
                 stop=(g == GROUPS - 1),
             )
 
-        def finish(s, parts):
-            y = sb([P, 512], F32, "y%d" % s)
-            width = 512 // parts
-            for k in range(parts):
-                here = slice(width * k, width * (k + 1))
-                cols = slice(512 * s + width * k, 512 * s + width * (k + 1))
-                nc.vector.tensor_tensor(out=y[:, here], in0=acc[s][:, here], in1=map_bias[:, cols], op=ADD)
-                nc.sync.dma_start(out=out.rearrange("b c s -> (b c) s")[:, cols], in_=y[:, here])
+        def finish(first, width, start=0):
+            cols = slice(first + start, first + start + width)
+            nc.vector.tensor_tensor(out=y[:, cols], in0=acc[first][:, start : start + width], in1=map_bias[:, cols], op=ADD)
+            nc.sync.dma_start(out=out.rearrange("b c s -> (b c) s")[:, cols], in_=y[:, cols])
 
         def h_keys(*units):
             return [("h", unit, e) for unit in units for e in range(2)]
@@ -280,10 +278,8 @@ def tile_model_pb_w8_kernel(tc, h_bytes, h_scale, dec_W, dec_b, map_W_words, map
         nc.vector.tensor_copy(out=ident_bf[:], in_=ident[:])
         nc.vector.memset(wsc[:].bitcast(I32), 0)
 
-        nc.sync.dma_start(out=map_cols[:], in_=map_b[0:1024].rearrange("(p c) -> p c", p=P))
-        load_h(0, [0])
+        load_h(0, 2)
         nc.sync.dma_start(out=dec_rows[0:MODELS, :], in_=dec_b)
-        load_h(0, [1])
         nc.sync.dma_start(out=scale_col[:], in_=h_scale.rearrange("a b c d (p j) -> p (a b c d j)", p=P))
         load_h(1)
         load_w(0)
@@ -292,15 +288,13 @@ def tile_model_pb_w8_kernel(tc, h_bytes, h_scale, dec_W, dec_b, map_W_words, map
         load_h(3)
         load_w(2)
         load_w(3)
-        nc.sync.dma_start(out=map_rows[0:2, :], in_=map_b[1024:T].rearrange("(q s) -> q s", q=2))
-        load_map_w(0, 0, 4)
+        nc.sync.dma_start(out=map_rows[0:4, :], in_=map_b.rearrange("(q s) -> q s", q=4))
+        load_map_w(0, 0, T)
         load_map_scales(nc.sync, range(4))
-        load_map_w(1, 0, 4)
-        load_map_w(2, 0, 2)
-        load_map_w(3, 0, 2)
-        load_map_w(2, 2, 2)
-        load_map_w(3, 2, 1)
-        load_map_w(3, 3, 1)
+        load_map_w(1, 0, T)
+        load_map_w(2, 0, T)
+        load_map_w(3, 0, 1024)
+        load_map_w(3, 1024, 1024)
 
         batch("wh01", w_keys(0) + h_keys(0) + w_keys(1) + h_keys(1))
         batch("wh23", w_keys(2) + h_keys(2) + w_keys(3) + h_keys(3))
@@ -309,18 +303,17 @@ def tile_model_pb_w8_kernel(tc, h_bytes, h_scale, dec_W, dec_b, map_W_words, map
         for g in range(GROUPS):
             batch("x%d" % g, [("x", g)])
 
-        turn_map_bias(7)
         turn_dec_rows(2)
         widen(nc.vector.tensor_copy, 0, [0])
         widen(nc.vector.tensor_copy, 4, [0])
         widen(nc.scalar.copy, 0, [1])
         widen(nc.vector.tensor_copy, 4, [1])
         dec_cols_out()
-        turn(0, 0, 0, 1)
-        turn(0, 1, 1, 1)
+        turn(0, 0, [0])
+        h_out_scaled_half(0, 0)
+        turn(0, 1, [1])
         turn(4, 4)
-        h_out_scaled(0, 0, 1)
-        h_out_scaled(0, 1, 1)
+        h_out_scaled_half(0, 1)
         widen(nc.scalar.copy, 1)
         turn(1, 5)
         spread_dec_bias(3)
@@ -329,7 +322,6 @@ def tile_model_pb_w8_kernel(tc, h_bytes, h_scale, dec_W, dec_b, map_W_words, map
         h_out_scaled(4)
         widen(nc.scalar.copy, 2)
         turn(2, 6)
-        turn(5, 0)
         widen(nc.scalar.copy, 6)
         turn(6, 4)
         w_group_pool(1)
@@ -342,27 +334,31 @@ def tile_model_pb_w8_kernel(tc, h_bytes, h_scale, dec_W, dec_b, map_W_words, map
         widen(nc.scalar.copy, 7)
         w_group(3, 0, 5)
         w_group(3, 1, 6)
+        turn(5, 0)
         h_out_scaled(3)
         h_out_planes(6)
         turn(7, 4)
         w_out(3, 0)
         w_out(3, 1)
-        h_group(6, 1)
+        h_group(6, 0, 1)
         h_out_planes(5)
         quantise("wh01")
         decode(0)
         decode(1)
+        h_group(6, 1, 1)
+        spread_map_bias(0, 0, 5)
         h_group_out(6)
-        map_turned_out(nc.scalar.copy)
         quantise("wh23")
         batch("h5", h_keys(5), "in_wh23")
         h_group_pool(5)
         decode(2)
         decode(3)
+        spread_map_bias(0, 1, 5)
+        map_bias_out(0)
         x_bias(0, 0, [0, 1])
-        spread_map_bias(1, 0, 7)
         x_turn((0,), 0, 0)
         x_turn((1,), 0, 6)
+        spread_map_bias(1, 0, 7)
         h_out_scaled(7, 0, 1)
         x_bias(0, 1, [0, 1])
         x_turn((0,), 1, 0)
@@ -380,11 +376,11 @@ def tile_model_pb_w8_kernel(tc, h_bytes, h_scale, dec_W, dec_b, map_W_words, map
         decode(4)
         decode(5)
         time_map(0, 0)
-        time_map(0, 1)
+        time_map(0, 512)
         decode(6)
         decode(7)
-        time_map(0, 2)
-        time_map(0, 3)
+        time_map(0, 1024)
+        time_map(1, 0)
         x_bias(1, 0, [0, 1])
         x_bias(1, 1, [0])
         x_bias(1, 1, [1])
@@ -392,16 +388,24 @@ def tile_model_pb_w8_kernel(tc, h_bytes, h_scale, dec_W, dec_b, map_W_words, map
         x_turn((3,), 0, 1)
         x_turn((2,), 1, 0)
         x_turn((3,), 1, 1)
-        time_map(1, 0)
-        time_map(1, 1)
-        time_map(1, 2)
+        time_map(1, 512)
+        time_map(0, 1536)
+        time_map(1, 1024)
         x_out((2,))
         x_out((3,))
         quantise("x2")
         quantise("x3")
-        for s in range(4):
-            if s == 3:
-                time_map(1, s)
-            time_map(2, s)
-            time_map(3, s)
-            finish(s, 2 if s in (0, 3) else 1)
+        time_map(2, 0)
+        time_map(3, 0)
+        finish(0, 256)
+        finish(0, 256, 256)
+        time_map(2, 512)
+        time_map(3, 512)
+        finish(512, 512)
+        time_map(2, 1024)
+        time_map(3, 1024)
+        finish(1024, 512)
+        time_map(1, 1536)
+        time_map(2, 1536)
+        time_map(3, 1536)
+        finish(1536, 512)

from contextlib import ExitStack

import concourse.mybir as mybir
from concourse.masks import make_identity

F32 = mybir.dt.float32
BF16 = mybir.dt.bfloat16
I32 = mybir.dt.int32
U32 = mybir.dt.uint32
U8 = mybir.dt.uint8
FP8 = mybir.dt.float8_e4m3fn
FP8X4 = mybir.dt.float8_e4m3fn_x4
MULT = mybir.AluOpType.mult
ADD = mybir.AluOpType.add
COPY = mybir.ActivationFunctionType.Copy

P = 128
MODELS = 8
D = 512
T = 2048
BC = 128
PATCHES = 2
GROUPS = T // 512
HALF = 64
FIRST_MODEL = (0, 4, 2, 6)
ACC_BANK = {0: 4, 512: 5, 1024: 6, 1536: 7, 1792: 2}

FLOPS = 2 * MODELS * BC * PATCHES * D * P + 2 * BC * T * T


def tile_model_pb_w8_kernel(tc, h_bytes, h_scale, dec_W, dec_b, map_W_words, map_W_scales, map_b, out):
    nc = tc.nc

    with ExitStack() as ctx:
        keep = ctx.enter_context(tc.tile_pool(name="keep", bufs=1))
        psum = ctx.enter_context(tc.psum_pool(name="psum", bufs=1))
        ctx.enter_context(tc.manual_schedule())

        def sb(shape, dtype, name):
            return keep.tile(shape, dtype, name=name, align_bytes=64)

        def bank(i, shape, name, dtype=F32):
            return psum.tile(shape, dtype, name=name, tag="bank%d" % i)

        hb, w_raw, ww = {}, {}, {}

        def load_h(k, parts=1):
            n0 = FIRST_MODEL[k]
            t = sb([P, 2, PATCHES, D], U8, "hb%d" % k)
            rows = h_bytes[n0 : n0 + 2].rearrange("n b (c r) l d -> (n b c) r l d", r=2)
            for a in range(parts):
                of = slice(a * 2 // parts, (a + 1) * 2 // parts)
                nc.sync.dma_start(out=t[:, of], in_=rows[:, of])
            for r in range(2):
                for l in range(PATCHES):
                    hb[4 * l + k, r] = t[:, r, l].bitcast(FP8)

        def load_w(k):
            n0 = FIRST_MODEL[k]
            w_raw[k] = sb([P, 2, 4, P], BF16, "w_raw%d" % k)
            nc.sync.dma_start(out=w_raw[k][:], in_=dec_W[n0 : n0 + 2].rearrange("n (p j) w -> p n j w", j=4))

        def load_map_w(g, first, width):
            if g not in ww:
                ww[g] = sb([P, T], I32, "ww%d" % g)
            words = map_W_words[g].rearrange("p n t -> p (n t)").bitcast(I32)
            nc.sync.dma_start(out=ww[g][:, first : first + width], in_=words[:, first : first + width])

        def load_map_scales(queue, quadrants):
            for q in quadrants:
                queue.dma_start(
                    out=wsc[32 * q : 32 * q + 16, :].bitcast(I32),
                    in_=map_W_scales[:, 4 * q : 4 * q + 4, :].bitcast(I32),
                )

        scale_col = sb([P, 4], F32, "scale_col")
        ident = sb([P, P], F32, "ident")
        ident_bf = sb([P, P], BF16, "ident_bf")
        dec_rows = sb([P, P], BF16, "dec_rows")
        dec_cols = sb([P, MODELS], BF16, "dec_cols")
        map_rows = sb([P, 512], BF16, "map_rows")
        wsc = sb([P, T], U8, "wsc")
        dec_bias = sb([P, 2, P, 2, 2], BF16, "dec_bias")
        map_bias = sb([P, T], BF16, "map_bias")

        y = sb([P, T], F32, "y")

        hx, ht, hw = {}, {}, {}
        batches, place, codes, scales = {}, {}, {}, {}
        x_ps, xb, xt, acc, side_ps = {}, {}, {}, {}, {}

        def turn_dec_rows(b):
            side_ps["rows"] = bank(b, [P, P], "dec_rows_ps", BF16)
            nc.tensor.transpose(side_ps["rows"][:], dec_rows[:], ident_bf[:])

        def dec_cols_out():
            nc.scalar.copy(out=dec_cols[:], in_=side_ps["rows"][:, 0:MODELS])

        def spread(b, name, words):
            side_ps[name] = bank(b, [P, 4, P], name)
            for m in range(4):
                nc.tensor.transpose(side_ps[name][:, m], words[:, m : m + 1].to_broadcast([P, P]), ident[:])

        def spread_dec_bias(b):
            spread(b, "dec_bias_ps", dec_cols[:].bitcast(F32))

        def dec_bias_out(copy):
            to = dec_bias[:].rearrange("b u p h e -> b (u p h e)").bitcast(F32).rearrange("b (u p h) -> b u p h", u=2, h=2)
            copy(out=to, in_=side_ps["dec_bias_ps"][:].rearrange("b (h u) p -> b u p h", u=2))

        def spread_map_bias(c, a, b):
            if a == 0:
                side_ps["map", c] = bank(b, [P, 1024], "map_bias_ps%d" % c, BF16)
            row = 2 * c + a
            pick = ident_bf[:, row : row + 1].to_broadcast([P, P])
            nc.tensor.matmul(side_ps["map", c][:, 512 * a : 512 * (a + 1)], pick, map_rows[:], start=True, stop=True)

        def map_bias_out(c):
            nc.scalar.copy(out=map_bias[:, 1024 * c : 1024 * (c + 1)], in_=side_ps["map", c][:])

        def widen(engine_copy, unit, models=(0, 1)):
            for e in models:
                t = sb([P, D], BF16, "hx%d_%d" % (unit, e))
                engine_copy(out=t[:], in_=hb[unit, e])
                hx[unit, e] = t[:]

        def turn(unit, b, rows=(0, 1)):
            ht[unit] = bank(b, [P, 2, 2, 2, HALF], "ht%d_%d" % (unit, rows[0]))
            for r in rows:
                words = hx[unit, r].bitcast(F32)
                for v in range(2):
                    nc.tensor.transpose(ht[unit][:, v, :, r], words[:, v::2], ident[:])

        def batch(name, keys, tag=None):
            t = keep.tile([P, len(keys) * D], BF16, name="in_" + name, tag=tag or "in_" + name, align_bytes=64)
            batches[name] = (t, keys)
            for m, key in enumerate(keys):
                place[key] = (t, m)

        def slots(key, count):
            t, m = place[key]
            return t[:, m * D : (m + count) * D]

        def quantise(name):
            t, keys = batches[name]
            words = sb([P, len(keys) * P], U32, "codes_" + name)
            plane = sb([P, len(keys) * P], U8, "scales_" + name)
            nc.vector.quantize_mx(out=words[:].bitcast(FP8X4), scales=plane[:], in_=t[:])
            for m, key in enumerate(keys):
                codes[key] = words[:, m * P : (m + 1) * P].bitcast(FP8X4)
                scales[key] = plane[:, m * P : (m + 1) * P]

        def h_out_scaled(unit, first=0, count=2):
            column = first * P
            to = slots(("h", unit, first), count).rearrange("p (r v z) -> p r v z", v=2, z=2)
            of = ht[unit][:].rearrange("p v e r c -> p (v e r c)").bitcast(BF16).rearrange("p (v r z) -> p r v z", v=2, z=2)
            by = scale_col[:].rearrange("p (o v z) -> p o v z", o=1, v=2).to_broadcast([P, count * P, 2, 2])
            nc.vector.tensor_tensor(out=to, in0=of[:, column : column + count * P], in1=by, op=MULT)

        def h_out_scaled_half(unit, r):
            for e in range(2):
                of = ht[unit][:, :, e, r].bitcast(BF16).rearrange("p v (c z) -> p c v z", z=2)
                to = slots(("h", unit, e), 1)[:, 256 * r : 256 * (r + 1)].rearrange("p (c v z) -> p c v z", v=2, z=2)
                by = scale_col[:].rearrange("p (o v z) -> p o v z", o=1, v=2).to_broadcast([P, HALF, 2, 2])
                nc.vector.tensor_tensor(out=to, in0=of, in1=by, op=MULT)

        def h_out_planes(unit, planes=range(4), first=0):
            if unit not in hw:
                hw[unit] = sb([P, 4, (2 - first) * P], BF16, "hw%d" % unit)
            of = ht[unit][:].rearrange("p v e r c -> p (v e r c)").bitcast(BF16).rearrange("p (v r z) -> p v z r", v=2, z=2)
            for t in planes:
                nc.scalar.activation(out=hw[unit][:, t], in_=of[:, t // 2, t % 2, first * P :], func=COPY, scale=scale_col[:, t : t + 1])

        def h_group_pool(unit, first=0):
            to = slots(("h", unit, first), 2 - first).rearrange("p (r t) -> p r t", t=4)
            nc.gpsimd.tensor_scalar(out=to, in0=hw[unit][:].rearrange("p t r -> p r t"), scalar1=1.0, scalar2=0.0, op0=MULT, op1=ADD)

        def h_group_scalar(unit):
            to = slots(("h", unit, 0), 2).rearrange("p (r t) -> p r t", t=4)
            nc.scalar.copy(out=to, in_=hw[unit][:].rearrange("p t r -> p r t"))

        def h_group(unit, e, b):
            if e == 0:
                side_ps["h", unit] = bank(b, [P, 2, 512], "h_ps%d" % unit, BF16)
            planes = hw[unit][:, :, e * P : (e + 1) * P].rearrange("p t r -> p r t")
            nc.tensor.matmul(side_ps["h", unit][:, e], ident_bf[:], planes, start=True, stop=True)

        def h_group_out(unit, first=0):
            nc.scalar.copy(out=slots(("h", unit, first), 2 - first), in_=side_ps["h", unit][:].rearrange("p e x -> p (e x)"))

        def w_group(k, e, b):
            side_ps["w", k, e] = bank(b, [P, 512], "w_ps%d_%d" % (k, e), BF16)
            nc.tensor.matmul(side_ps["w", k, e][:], ident_bf[:], w_raw[k][:, e].rearrange("p t c -> p c t"), start=True, stop=True)

        def w_out(k, e):
            nc.scalar.copy(out=slots(("w", k, e), 1), in_=side_ps["w", k, e][:])

        def w_group_pool(k, count=2):
            to = slots(("w", k, 0), count).rearrange("p (e c t) -> p e c t", e=count, t=4)
            nc.gpsimd.tensor_scalar(out=to, in0=w_raw[k][:, 0:count].rearrange("p e t c -> p e c t"), scalar1=1.0, scalar2=0.0, op0=MULT, op1=ADD)


        def w_group_scalar(k, e):
            to = slots(("w", k, e), 1).rearrange("p (c t) -> p c t", t=4)
            nc.scalar.copy(out=to, in_=w_raw[k][:, e].rearrange("p t c -> p c t"))

        def warm_up(b, count):
            zeros = sb([P, P], F32, "zeros")
            nc.vector.memset(zeros[:], 0.0)
            spare = bank(b, [P, P], "spare")
            for a in range(count):
                nc.tensor.matmul(spare[:], zeros[:], zeros[:], start=True, stop=True)

        def decode(unit):
            l, k = divmod(unit, 4)
            u, h = divmod(k, 2)
            if (l, u) not in x_ps:
                x_ps[l, u] = bank(2 + u, [P, 2, 2, P], "x_ps%d_%d" % (l, u))
            for e in range(2):
                nc.tensor.matmul_mx(
                    out=x_ps[l, u][:, h, e],
                    lhsT=codes["h", unit, e],
                    lhsT_scale=scales["h", unit, e],
                    rhs=codes["w", k, e],
                    rhs_scale=scales["w", k, e],
                    start=True,
                    stop=True,
                )

        def x_bias(l, u, halves):
            t = sb([P, len(halves) * HALF, 2, 2], BF16, "xb%d_%d_%d" % (l, u, halves[0]))
            samples = slice(halves[0] * HALF, (halves[-1] + 1) * HALF)
            nc.vector.tensor_tensor(
                out=t[:], in0=x_ps[l, u][:, :, :, samples].rearrange("b h e p -> b p h e"), in1=dec_bias[:, u, samples], op=ADD
            )
            for a, half in enumerate(halves):
                xb[2 * l + half, u] = t[:, a * HALF : (a + 1) * HALF].rearrange("b p h e -> b (p h e)").bitcast(F32)

        def x_turn(groups, u, b):
            if groups not in xt:
                xt[groups] = bank(b, [P, len(groups), 2, P], "xt%d" % groups[0])
            for a, g in enumerate(groups):
                nc.tensor.transpose(xt[groups][:, a, u], xb[g, u], ident[:])

        def x_out(groups):
            to = slots(("x", groups[0]), 1).bitcast(F32).rearrange("p (c r u) -> p c r u", r=2, u=2)
            nc.scalar.copy(out=to, in_=xt[groups][:, 0].rearrange("p u (r c) -> p c r u", r=2))

        def time_map(g, first, width=512):
            if g == 0:
                acc[first] = bank(ACC_BANK[first], [P, width], "acc%d" % first)
            cols = slice(first, first + width)
            nc.tensor.matmul_mx(
                out=acc[first][:],
                lhsT=codes["x", g],
                lhsT_scale=scales["x", g],
                rhs=ww[g][:, cols].bitcast(FP8X4),
                rhs_scale=wsc[4 * g : P, cols],
                start=(g == 0),
                stop=(g == GROUPS - 1),
            )

        def finish(first, width, start=0):
            cols = slice(first + start, first + start + width)
            nc.vector.tensor_tensor(out=y[:, cols], in0=acc[first][:, start : start + width], in1=map_bias[:, cols], op=ADD)
            nc.sync.dma_start(out=out.rearrange("b c s -> (b c) s")[:, cols], in_=y[:, cols])

        def h_keys(*units):
            return [("h", unit, e) for unit in units for e in range(2)]

        def w_keys(k):
            return [("w", k, e) for e in range(2)]

        nc.vector.memset(ident[:], 0.0)
        make_identity(nc, ident[:], nomemset=True)
        nc.vector.memset(dec_rows[:].bitcast(I32), 0)
        nc.vector.memset(map_rows[:].bitcast(I32), 0)
        nc.vector.tensor_copy(out=ident_bf[:], in_=ident[:])
        nc.vector.memset(wsc[:].bitcast(I32), 0)

        load_h(0, 2)
        nc.sync.dma_start(out=dec_rows[0:MODELS, :], in_=dec_b)
        nc.sync.dma_start(out=scale_col[:], in_=h_scale.rearrange("a b c d (p j) -> p (a b c d j)", p=P))
        load_h(1)
        load_w(0)
        load_h(2)
        load_w(1)
        load_h(3)
        load_w(2)
        load_w(3)
        nc.sync.dma_start(out=map_rows[0:4, :], in_=map_b.rearrange("(q s) -> q s", q=4))
        load_map_w(0, 0, T)
        load_map_scales(nc.sync, range(4))
        load_map_w(1, 0, T)
        load_map_w(2, 0, T)
        load_map_w(3, 0, 1024)
        load_map_w(3, 1024, 1024)

        batch("wh01", w_keys(0) + h_keys(0) + w_keys(1) + h_keys(1))
        batch("wh23", w_keys(2) + h_keys(2) + w_keys(3) + h_keys(3))
        batch("h4", h_keys(4))
        batch("h67", h_keys(6, 7))
        for g in range(GROUPS):
            batch("x%d" % g, [("x", g)])

        turn_dec_rows(2)
        widen(nc.vector.tensor_copy, 0, [0])
        widen(nc.vector.tensor_copy, 4, [0])
        widen(nc.scalar.copy, 0, [1])
        widen(nc.vector.tensor_copy, 4, [1])
        dec_cols_out()
        turn(0, 0, [0])
        h_out_scaled_half(0, 0)
        turn(0, 1, [1])
        turn(4, 4)
        h_out_scaled_half(0, 1)
        widen(nc.scalar.copy, 1)
        turn(1, 5)
        spread_dec_bias(3)
        widen(nc.scalar.copy, 5)
        w_group_pool(0)
        h_out_scaled(4)
        widen(nc.scalar.copy, 2)
        turn(2, 6)
        widen(nc.scalar.copy, 6)
        turn(6, 4)
        w_group_pool(1)
        h_out_scaled(1)
        widen(nc.scalar.copy, 3)
        turn(3, 1)
        h_out_scaled(2)
        dec_bias_out(nc.vector.tensor_copy)
        w_group_pool(2)
        widen(nc.scalar.copy, 7)
        w_group(3, 0, 5)
        w_group(3, 1, 6)
        turn(5, 0)
        h_out_scaled(3)
        h_out_planes(6)
        turn(7, 4)
        w_out(3, 0)
        w_out(3, 1)
        h_group(6, 0, 1)
        h_out_planes(5)
        quantise("wh01")
        decode(0)
        decode(1)
        h_group(6, 1, 1)
        spread_map_bias(0, 0, 5)
        h_group_out(6)
        quantise("wh23")
        batch("h5", h_keys(5), "in_wh23")
        h_group_pool(5)
        decode(2)
        decode(3)
        spread_map_bias(0, 1, 5)
        map_bias_out(0)
        x_bias(0, 0, [0, 1])
        x_turn((0,), 0, 0)
        x_turn((1,), 0, 6)
        spread_map_bias(1, 0, 7)
        h_out_scaled(7, 0, 1)
        x_bias(0, 1, [0, 1])
        x_turn((0,), 1, 0)
        x_turn((1,), 1, 6)
        spread_map_bias(1, 1, 7)
        h_out_scaled(7, 1, 1)
        x_out((0,))
        x_out((1,))
        map_bias_out(1)
        quantise("h4")
        quantise("h5")
        quantise("x0")
        quantise("h67")
        quantise("x1")
        decode(4)
        decode(5)
        time_map(0, 0)
        time_map(0, 512)
        decode(6)
        decode(7)
        time_map(0, 1024)
        time_map(1, 0)
        x_bias(1, 0, [0, 1])
        x_bias(1, 1, [0])
        x_bias(1, 1, [1])
        x_turn((2,), 0, 0)
        x_turn((3,), 0, 1)
        x_turn((2,), 1, 0)
        x_turn((3,), 1, 1)
        time_map(1, 512)
        time_map(0, 1536)
        time_map(1, 1024)
        x_out((2,))
        x_out((3,))
        quantise("x2")
        quantise("x3")
        time_map(2, 0)
        time_map(3, 0)
        finish(0, 256)
        finish(0, 256, 256)
        time_map(2, 512)
        time_map(3, 512)
        finish(512, 512)
        time_map(2, 1024)
        time_map(3, 1024)
        finish(1024, 512)
        time_map(1, 1536)
        time_map(2, 1536)
        time_map(3, 1536)
        finish(1536, 512)
